import numpy as np
import ml_dtypes


def mxq(x, axis, fmt="e4m3"):
    dtype, down = {"e4m3": (ml_dtypes.float8_e4m3fn, 7), "e5m2": (ml_dtypes.float8_e5m2, 14)}[fmt]
    v = np.moveaxis(np.asarray(x, np.float32).astype(ml_dtypes.bfloat16).astype(np.float64), axis, -1)
    blocks = v.reshape(v.shape[:-1] + (-1, 32))
    amax = np.abs(blocks).max(-1, keepdims=True)
    byte = np.maximum(np.where(amax > 0, np.frexp(amax)[1] - 1 + 127, 0) - down, 1)
    scale = np.exp2(byte - 127.0)
    codes = (blocks / scale).astype(np.float32).astype(dtype).astype(np.float64)
    return np.moveaxis((codes * scale).reshape(v.shape), -1, axis)


WIDE = False


def mx_kscale(k):
    if not WIDE:
        return np.ones(k)
    levels = np.array([10, -10, 5, -5, 0])
    a = np.random.permutation(np.resize(levels, k // 512 * 4)).reshape(k // 512, 4)
    idx = np.arange(k)
    return np.exp2(a[idx // 512, idx % 128 // 32])


BF16 = ml_dtypes.bfloat16


def bf(x):
    return np.asarray(x, np.float32).astype(BF16)


def f64(x):
    return np.asarray(x).astype(np.float64)


B, S, HD, H, G, QB = 1, 1024, 2048, 16, 4, 512
D = HD // H
REP = H // G
A = 1.4


def alibi_slopes():
    m0 = 2.0 ** (-8.0 / H)
    return m0 ** np.arange(1, H + 1)


def setup_inputs():
    s = mx_kscale(HD)
    return {"q": bf(np.random.standard_normal((B, S, HD)) * A),
            "k": bf(np.random.standard_normal((B, S, G * D)) * A),
            "x": bf(np.random.standard_normal((B, S, HD)) * s),
            "Wv": bf(np.random.standard_normal((G * D, HD)) * A / np.sqrt(HD) / s)}


def reference(q, k, x, Wv):
    qh = f64(q).reshape(B, S, H, D).transpose(0, 2, 1, 3).reshape(B * G, REP, S, D)
    kt = f64(k).reshape(B, S, G, D).transpose(0, 2, 3, 1).reshape(B * G, 1, D, S)
    v = mxq(f64(x), 2, "e4m3") @ mxq(f64(Wv).T, 0, "e4m3")
    vq = mxq(v.reshape(B, S, G, D).transpose(0, 2, 1, 3).reshape(B * G, 1, S, D), 2, "e4m3")
    scale = 1.0 / np.sqrt(D)
    slopes = np.tile(alibi_slopes().reshape(G, REP), (B, 1))[:, :, None, None]
    blocks = []
    for q0 in range(0, S, QB):
        q1 = q0 + QB
        i = np.arange(q0, q1)[:, None]
        j = np.arange(q1)[None, :]
        bias = np.where(j <= i, -slopes * np.sqrt(np.maximum(i - j, 0)), -np.inf)
        sc = qh[:, :, q0:q1] @ kt[:, :, :, :q1] * scale + bias
        e = np.exp(sc - sc.max(-1, keepdims=True))
        o = (mxq(e, 3, "e4m3") @ vq[:, :, :q1]) / e.sum(-1, keepdims=True)
        blocks.append(o.reshape(B, H, QB, D).transpose(0, 2, 1, 3).reshape(B, QB, HD))
    return np.concatenate(blocks, axis=1)

@@ -1,0 +1,316 @@
+import math
+from contextlib import ExitStack
+
+import concourse.mybir as mybir
+from concourse.masks import make_identity
+
+F32 = mybir.dt.float32
+BF16 = mybir.dt.bfloat16
+I32 = mybir.dt.int32
+U32 = mybir.dt.uint32
+U8 = mybir.dt.uint8
+FP8X4 = mybir.dt.float8_e4m3fn_x4
+ALU = mybir.AluOpType
+ACT = mybir.ActivationFunctionType
+AXIS = mybir.AxisListType
+
+P = 128
+S = 1024
+HD = 2048
+HEADS = 16
+GROUPS = 4
+REP = HEADS // GROUPS
+GD = GROUPS * P
+Q_TILES = S // P
+K_PASS = 512
+PLANE = 256
+BANK = 512
+SCALE = 1.0 / math.sqrt(P)
+MASKED = 1.0e30
+E_RING = 2 * REP
+
+FLOPS = 2 * S * HD * GD + 2 * 2 * HEADS * P * (K_PASS * K_PASS + K_PASS * S)
+
+
+def tile_step1attention_pa_kernel(tc, q, k, x, Wv, out):
+    nc = tc.nc
+    q_rows = q.flatten_outer_dims()
+    k_rows = k.flatten_outer_dims()
+    x_rows = x.flatten_outer_dims()
+    out_rows = out.flatten_outer_dims()
+
+    with ExitStack() as ctx:
+        keep = ctx.enter_context(tc.tile_pool(name="keep", bufs=1))
+        loads = ctx.enter_context(tc.tile_pool(name="loads", bufs=4))
+        q_pool = ctx.enter_context(tc.tile_pool(name="q_pool", bufs=3))
+        grouped_pool = ctx.enter_context(tc.tile_pool(name="grouped_pool", bufs=8))
+        ps_scores = ctx.enter_context(tc.psum_pool(name="ps_scores", bufs=3))
+        ps_planes = ctx.enter_context(tc.psum_pool(name="ps_planes", bufs=3))
+        ps_sums = ctx.enter_context(tc.psum_pool(name="ps_sums", bufs=2))
+
+        ident_bf = keep.tile([P, P], BF16, name="ident_bf")
+        make_identity(nc, ident_bf[:])
+        ident_f32 = keep.tile([P, P], F32, name="ident_f32")
+        make_identity(nc, ident_f32[:])
+
+        neg_root = keep.tile([P, S], F32, name="neg_root")
+        with tc.tile_pool(name="setup", bufs=1) as setup:
+            dist_int = setup.tile([P, S], I32, name="dist_int")
+            nc.gpsimd.iota(dist_int[:], pattern=[[1, S]], base=0, channel_multiplier=-1)
+            dist = setup.tile([P, S], F32, name="dist")
+            nc.vector.tensor_copy(out=dist[:], in_=dist_int[:])
+            root = setup.tile([P, S], F32, name="root")
+            nc.vector.tensor_scalar_max(out=root[:], in0=dist[:], scalar1=1.0)
+            nc.scalar.activation(out=root[:], in_=root[:], func=ACT.Sqrt)
+            is_past = setup.tile([P, S], F32, name="is_past")
+            nc.vector.tensor_scalar(
+                out=is_past[:], in0=dist[:], scalar1=0.0, scalar2=1.0, op0=ALU.max, op1=ALU.min
+            )
+            nc.vector.scalar_tensor_tensor(
+                out=neg_root[:], in0=root[:], scalar=-1.0, in1=is_past[:], op0=ALU.mult, op1=ALU.mult
+            )
+            future = setup.tile([P, S], F32, name="future")
+            nc.vector.tensor_scalar(
+                out=future[:], in0=dist[:], scalar1=0.0, scalar2=MASKED, op0=ALU.min, op1=ALU.mult
+            )
+            nc.vector.tensor_add(out=neg_root[:], in0=neg_root[:], in1=future[:])
+
+        def planes_to_grouped(planes, copy):
+            bank = ps_planes.tile([P, 4, P], F32, name="bank", tag="planes")
+            for j in range(4):
+                nc.tensor.transpose(out=bank[:, j, :], in_=planes[j], identity=ident_f32[:])
+            grouped = grouped_pool.tile([P, 2 * K_PASS], BF16, name="grouped", align_bytes=64)
+            copy(
+                out=grouped[:].bitcast(F32).rearrange("p (c w u) -> p c w u", c=2, u=2),
+                in_=bank[:].rearrange("p (c u) w -> p c w u", u=2),
+            )
+            return grouped
+
+        def quantise(grouped, codes, scales):
+            nc.vector.quantize_mx(out=codes.bitcast(FP8X4), scales=scales, in_=grouped[:])
+
+        w_codes = keep.tile([P, GROUPS, 4 * P], U32, name="w_codes", align_bytes=64)
+        w_scales = keep.tile([P, GROUPS, 4 * P], U8, name="w_scales", align_bytes=64)
+        x_codes = keep.tile([P, Q_TILES, 4 * P], U32, name="x_codes", align_bytes=64)
+        x_scales = keep.tile([P, Q_TILES, 4 * P], U8, name="x_scales", align_bytes=64)
+        v_codes = keep.tile([P, S // K_PASS, GD], U32, name="v_codes", align_bytes=64)
+        v_scales = keep.tile([P, S // K_PASS, GD], U8, name="v_scales", align_bytes=64)
+
+        def quantise_rows(rows, codes, scales):
+            raw = loads.tile([P, HD], BF16, name="raw")
+            nc.sync.dma_start(out=raw[:], in_=rows)
+            words = raw[:].bitcast(F32)
+            for half in range(2):
+                planes = [words[:, (4 * half + j) * P : (4 * half + j + 1) * P] for j in range(4)]
+                copy = nc.vector.tensor_copy if half == 0 else nc.scalar.copy
+                grouped = planes_to_grouped(planes, copy)
+                cols = slice(2 * half * P, 2 * (half + 1) * P)
+                quantise(grouped, codes[:, cols], scales[:, cols])
+
+        x_tiles = x_rows.rearrange("(a p e) c -> a e p c", p=P, e=2)
+
+        def project_values(key_pass):
+            for g in range(GROUPS):
+                sums = ps_sums.tile([P, 4, P], F32, name="sums", tag="sums")
+                for t in range(4):
+                    for c in range(HD // K_PASS):
+                        cols = slice(c * P, (c + 1) * P)
+                        nc.tensor.matmul_mx(
+                            out=sums[:, t, :],
+                            lhsT=x_codes[:, 4 * key_pass + t, cols].bitcast(FP8X4),
+                            lhsT_scale=x_scales[:, 4 * key_pass + t, cols],
+                            rhs=w_codes[:, g, cols].bitcast(FP8X4),
+                            rhs_scale=w_scales[:, g, cols],
+                            start=(c == 0),
+                            stop=(c == HD // K_PASS - 1),
+                        )
+                grouped = grouped_pool.tile([P, P, 4], BF16, name="grouped_v", tag="grouped", align_bytes=64)
+                nc.scalar.copy(out=grouped[:], in_=sums[:].rearrange("p t n -> p n t"))
+                cols = slice(g * P, (g + 1) * P)
+                nc.vector.quantize_mx(
+                    out=v_codes[:, key_pass, cols].bitcast(FP8X4),
+                    scales=v_scales[:, key_pass, cols],
+                    in_=grouped[:].rearrange("p n t -> p (n t)"),
+                )
+
+        for g in range(GROUPS):
+            quantise_rows(Wv[g * P : (g + 1) * P, :], w_codes[:, g, :], w_scales[:, g, :])
+
+        k_raw = keep.tile([P, Q_TILES, GD], BF16, name="k_raw")
+        q_raw = {}
+
+        def load_queries(it):
+            q_raw[it] = q_pool.tile([P, HD], BF16, name="q_raw")
+            nc.sync.dma_start(out=q_raw[it][:], in_=q_rows[it * P : (it + 1) * P, :])
+
+        for key_pass in range(S // K_PASS):
+            for t in range(4):
+                tile_no = 4 * key_pass + t
+                quantise_rows(x_tiles[tile_no // 2, tile_no % 2], x_codes[:, tile_no, :], x_scales[:, tile_no, :])
+            if key_pass == 0:
+                nc.sync.dma_start(out=k_raw[:], in_=k_rows.rearrange("(t p) c -> p t c", p=P))
+                for it in range(3):
+                    load_queries(it)
+            project_values(key_pass)
+
+        kT = keep.tile([P, GROUPS, S], BF16, name="kT")
+        qT_pool = ctx.enter_context(tc.tile_pool(name="qT_pool", bufs=2))
+        qT = {}
+
+        def transpose_queries_and_keys(it):
+            qT[it] = qT_pool.tile([P, HEADS, P], BF16, name="qT")
+            for half in range(2):
+                bank = ps_planes.tile([P, 8, P], BF16, name="bank_q", tag="planes")
+                for j in range(8):
+                    h = 8 * half + j
+                    nc.tensor.transpose(out=bank[:, j, :], in_=q_raw[it][:, h * P : (h + 1) * P], identity=ident_bf[:])
+                nc.scalar.copy(out=qT[it][:, 8 * half : 8 * (half + 1), :], in_=bank[:])
+            bank = ps_planes.tile([P, GROUPS, P], BF16, name="bank_k", tag="planes")
+            for g in range(GROUPS):
+                nc.tensor.transpose(out=bank[:, g, :], in_=k_raw[:, it, g * P : (g + 1) * P], identity=ident_bf[:])
+            nc.scalar.copy(out=kT[:, :, it * P : (it + 1) * P], in_=bank[:])
+            if it + 3 < Q_TILES:
+                load_queries(it + 3)
+
+        s_pool = ctx.enter_context(tc.tile_pool(name="s_pool", bufs=2))
+        bias_pool = ctx.enter_context(tc.tile_pool(name="bias_pool", bufs=2))
+        stats = ctx.enter_context(tc.tile_pool(name="stats", bufs=4))
+        e_codes_pool = ctx.enter_context(tc.tile_pool(name="e_codes_pool", bufs=3))
+        o_pool = ctx.enter_context(tc.tile_pool(name="o_pool", bufs=3))
+        e_ring = [keep.tile([P, S], BF16, name="e_ring%d" % n) for n in range(E_RING)]
+
+        units = [(it, g) for it in range(Q_TILES) for g in range(GROUPS)]
+        live = {}
+
+        def scores(n):
+            it, g = units[n]
+            keys = P * (it + 1)
+            z = s_pool.tile([P, REP, S], F32, name="z")
+            bias = bias_pool.tile([P, REP, S], F32, name="bias")
+            for r in range(REP):
+                h = REP * g + r
+                slope = 2.0 ** (-(h + 1) / 2.0)
+                nc.gpsimd.tensor_scalar(
+                    out=bias[:, r, :keys], in0=neg_root[:, :keys], scalar1=slope / SCALE, scalar2=0.0,
+                    op0=ALU.mult, op1=ALU.add,
+                )
+                for k0 in range(0, keys, BANK):
+                    width = min(BANK, keys - k0)
+                    qk = ps_scores.tile([P, BANK], F32, name="qk")
+                    nc.tensor.matmul(
+                        out=qk[:, :width], lhsT=qT[it][:, h, :], rhs=kT[:, g, k0 : k0 + width], start=True, stop=False
+                    )
+                    for j in range(width // P):
+                        delta = it - (k0 // P + j)
+                        nc.tensor.matmul(
+                            out=qk[:, j * P : (j + 1) * P],
+                            lhsT=bias[:, r, delta * P : (delta + 1) * P],
+                            rhs=ident_f32[:],
+                            is_transpose=True,
+                            start=False,
+                            stop=(j == width // P - 1),
+                        )
+                    nc.vector.tensor_copy(out=z[:, r, k0 : k0 + width], in_=qk[:, :width])
+            live[n] = {"z": z}
+
+        def row_maxima(n):
+            it, g = units[n]
+            neg_max = stats.tile([P, REP], F32, name="neg_max")
+            nc.vector.tensor_reduce(
+                out=neg_max[:], in_=live[n]["z"][:, :, : P * (it + 1)], axis=AXIS.X, op=ALU.max, negate=True
+            )
+            live[n]["neg_max"] = neg_max
+
+        def exp_biases(n):
+            exp_bias = stats.tile([P, REP], F32, name="exp_bias")
+            nc.scalar.mul(out=exp_bias[:], in_=live[n]["neg_max"][:], mul=SCALE)
+            live[n]["exp_bias"] = exp_bias
+
+        def exponentials(n):
+            it, g = units[n]
+            keys = P * (it + 1)
+            first = 0 if keys > K_PASS else K_PASS
+            if it % 4 == 0 and g == 0:
+                for e_tile in e_ring:
+                    nc.gpsimd.memset(e_tile[:, K_PASS + P :], 0.0)
+            row_sum = stats.tile([P, REP], F32, name="row_sum")
+            for r in range(REP):
+                nc.scalar.activation(
+                    out=e_ring[(REP * n + r) % E_RING][:, first : first + keys],
+                    in_=live[n]["z"][:, r, :keys],
+                    func=ACT.Exp,
+                    bias=live[n]["exp_bias"][:, r : r + 1],
+                    scale=SCALE,
+                    accum_out=row_sum[:, r : r + 1],
+                )
+            live[n]["row_sum"] = row_sum
+
+        def transpose_e(n):
+            it, g = units[n]
+            first_plane = 0 if P * (it + 1) > K_PASS else K_PASS // PLANE
+            planes = []
+            for r in range(REP):
+                words = e_ring[(REP * n + r) % E_RING][:].bitcast(F32)
+                planes.extend(words[:, a * P : (a + 1) * P] for a in range(first_plane, S // PLANE))
+            live[n]["grouped"] = [
+                planes_to_grouped(planes[b : b + 4], nc.scalar.copy) for b in range(0, len(planes), 4)
+            ]
+
+        def quantise_e(n):
+            e_codes = e_codes_pool.tile([P, 2 * REP * P], U32, name="e_codes", align_bytes=64)
+            e_scales = e_codes_pool.tile([P, 2 * REP * P], U8, name="e_scales", align_bytes=64)
+            for b, grouped in enumerate(live[n]["grouped"]):
+                cols = slice(2 * b * P, 2 * (b + 1) * P)
+                quantise(grouped, e_codes[:, cols], e_scales[:, cols])
+            live[n]["e_codes"] = e_codes
+            live[n]["e_scales"] = e_scales
+
+        def reciprocals(n):
+            inv_sum = stats.tile([P, REP], F32, name="inv_sum")
+            nc.vector.reciprocal(out=inv_sum[:], in_=live[n]["row_sum"][:])
+            live[n]["inv_sum"] = inv_sum
+
+        def weighted_values(n):
+            it, g = units[n]
+            passes = (P * (it + 1) + K_PASS - 1) // K_PASS
+            sums = ps_sums.tile([P, REP, P], F32, name="o_sums", tag="sums")
+            for r in range(REP):
+                for c in range(passes):
+                    cols = slice((r * passes + c) * P, (r * passes + c + 1) * P)
+                    nc.tensor.matmul_mx(
+                        out=sums[:, r, :],
+                        lhsT=live[n]["e_codes"][:, cols].bitcast(FP8X4),
+                        lhsT_scale=live[n]["e_scales"][:, cols],
+                        rhs=v_codes[:, c, g * P : (g + 1) * P].bitcast(FP8X4),
+                        rhs_scale=v_scales[:, c, g * P : (g + 1) * P],
+                        start=(c == 0),
+                        stop=(c == passes - 1),
+                    )
+            o = o_pool.tile([P, REP * P], F32, name="o")
+            for r in range(REP):
+                nc.scalar.activation(
+                    out=o[:, r * P : (r + 1) * P],
+                    in_=sums[:, r, :],
+                    func=ACT.Copy,
+                    scale=live[n]["inv_sum"][:, r : r + 1],
+                )
+            nc.gpsimd.dma_start(out=out_rows[it * P : (it + 1) * P, g * REP * P : (g + 1) * REP * P], in_=o[:])
+
+        transpose_queries_and_keys(0)
+        for n in range(len(units) + 2):
+            if n < len(units):
+                scores(n)
+            if 0 <= n - 2:
+                quantise_e(n - 2)
+            if n < len(units):
+                row_maxima(n)
+            if 0 <= n - 1 < len(units):
+                exponentials(n - 1)
+                transpose_e(n - 1)
+                reciprocals(n - 1)
+            if n < len(units) and units[n][1] == 1 and units[n][0] + 1 < Q_TILES:
+                transpose_queries_and_keys(units[n][0] + 1)
+            if 0 <= n - 2:
+                weighted_values(n - 2)
+            if n < len(units):
+                exp_biases(n)

@@ -6,7 +6,6 @@ from concourse.masks import make_identity
 
 F32 = mybir.dt.float32
 BF16 = mybir.dt.bfloat16
-I32 = mybir.dt.int32
 U32 = mybir.dt.uint32
 U8 = mybir.dt.uint8
 FP8X4 = mybir.dt.float8_e4m3fn_x4
@@ -23,11 +22,10 @@ REP = HEADS // GROUPS
 GD = GROUPS * P
 Q_TILES = S // P
 K_PASS = 512
-PLANE = 256
-BANK = 512
 SCALE = 1.0 / math.sqrt(P)
 MASKED = 1.0e30
-E_RING = 2 * REP
+TINY = 1.0e-30
+E_RING = 4
 
 FLOPS = 2 * S * HD * GD + 2 * 2 * HEADS * P * (K_PASS * K_PASS + K_PASS * S)
 
@@ -40,45 +38,53 @@ def tile_step1attention_pa_kernel(tc, q, k, x, Wv, out):
     out_rows = out.flatten_outer_dims()
 
     with ExitStack() as ctx:
+        ctx.enter_context(tc.manual_schedule())
         keep = ctx.enter_context(tc.tile_pool(name="keep", bufs=1))
         loads = ctx.enter_context(tc.tile_pool(name="loads", bufs=4))
         q_pool = ctx.enter_context(tc.tile_pool(name="q_pool", bufs=3))
-        grouped_pool = ctx.enter_context(tc.tile_pool(name="grouped_pool", bufs=8))
-        ps_scores = ctx.enter_context(tc.psum_pool(name="ps_scores", bufs=3))
-        ps_planes = ctx.enter_context(tc.psum_pool(name="ps_planes", bufs=3))
-        ps_sums = ctx.enter_context(tc.psum_pool(name="ps_sums", bufs=2))
+        grouped_pool = ctx.enter_context(tc.tile_pool(name="grouped_pool", bufs=6))
+        ps_scores = ctx.enter_context(tc.psum_pool(name="ps_scores", bufs=5))
+        ps_planes = ctx.enter_context(tc.psum_pool(name="ps_planes", bufs=2))
+        ps_sums = ctx.enter_context(tc.psum_pool(name="ps_sums", bufs=1))
 
         ident_bf = keep.tile([P, P], BF16, name="ident_bf")
         make_identity(nc, ident_bf[:])
         ident_f32 = keep.tile([P, P], F32, name="ident_f32")
         make_identity(nc, ident_f32[:])
 
+        dist = keep.tile([P, S], F32, name="dist")
+        nc.gpsimd.iota(
+            dist[:], pattern=[[1, S]], base=0, channel_multiplier=-1, allow_small_or_imprecise_dtypes=True
+        )
+        future = keep.tile([P, S], F32, name="future")
+        root = keep.tile([P, S], F32, name="root")
         neg_root = keep.tile([P, S], F32, name="neg_root")
-        with tc.tile_pool(name="setup", bufs=1) as setup:
-            dist_int = setup.tile([P, S], I32, name="dist_int")
-            nc.gpsimd.iota(dist_int[:], pattern=[[1, S]], base=0, channel_multiplier=-1)
-            dist = setup.tile([P, S], F32, name="dist")
-            nc.vector.tensor_copy(out=dist[:], in_=dist_int[:])
-            root = setup.tile([P, S], F32, name="root")
-            nc.vector.tensor_scalar_max(out=root[:], in0=dist[:], scalar1=1.0)
-            nc.scalar.activation(out=root[:], in_=root[:], func=ACT.Sqrt)
-            is_past = setup.tile([P, S], F32, name="is_past")
-            nc.vector.tensor_scalar(
-                out=is_past[:], in0=dist[:], scalar1=0.0, scalar2=1.0, op0=ALU.max, op1=ALU.min
-            )
-            nc.vector.scalar_tensor_tensor(
-                out=neg_root[:], in0=root[:], scalar=-1.0, in1=is_past[:], op0=ALU.mult, op1=ALU.mult
-            )
-            future = setup.tile([P, S], F32, name="future")
-            nc.vector.tensor_scalar(
-                out=future[:], in0=dist[:], scalar1=0.0, scalar2=MASKED, op0=ALU.min, op1=ALU.mult
-            )
-            nc.vector.tensor_add(out=neg_root[:], in0=neg_root[:], in1=future[:])
 
-        def planes_to_grouped(planes, copy):
+        def build_neg_root():
+            nc.vector.tensor_scalar(out=root[:], in0=dist[:], scalar1=0.0, scalar2=TINY, op0=ALU.max, op1=ALU.add)
+            nc.scalar.activation(out=root[:], in_=root[:], func=ACT.Sqrt)
+            nc.vector.tensor_scalar(out=future[:], in0=dist[:], scalar1=0.0, scalar2=MASKED, op0=ALU.min, op1=ALU.mult)
+            nc.vector.scalar_tensor_tensor(
+                out=neg_root[:], in0=root[:], scalar=-1.0, in1=future[:], op0=ALU.mult, op1=ALU.add
+            )
+
+        bias = keep.tile([P, HEADS, S], F32, name="bias")
+
+        def scale_bias(h, it):
+            cols = slice(it * P, (it + 1) * P)
+            slope = 2.0 ** (-(h + 1) / 2.0)
+            nc.gpsimd.tensor_scalar(
+                out=bias[:, h, cols], in0=neg_root[:, cols], scalar1=slope / SCALE, scalar2=0.0,
+                op0=ALU.mult, op1=ALU.add,
+            )
+
+        def transpose_planes(words):
             bank = ps_planes.tile([P, 4, P], F32, name="bank", tag="planes")
-            for j in range(4):
-                nc.tensor.transpose(out=bank[:, j, :], in_=planes[j], identity=ident_f32[:])
+            for a in range(4):
+                nc.tensor.transpose(out=bank[:, a, :], in_=words[:, a * P : (a + 1) * P], identity=ident_f32[:])
+            return bank
+
+        def regroup(bank, copy):
             grouped = grouped_pool.tile([P, 2 * K_PASS], BF16, name="grouped", align_bytes=64)
             copy(
                 out=grouped[:].bitcast(F32).rearrange("p (c w u) -> p c w u", c=2, u=2),
@@ -96,14 +102,15 @@ def tile_step1attention_pa_kernel(tc, q, k, x, Wv, out):
         v_codes = keep.tile([P, S // K_PASS, GD], U32, name="v_codes", align_bytes=64)
         v_scales = keep.tile([P, S // K_PASS, GD], U8, name="v_scales", align_bytes=64)
 
-        def quantise_rows(rows, codes, scales):
+        def spread_rows(rows):
             raw = loads.tile([P, HD], BF16, name="raw")
             nc.sync.dma_start(out=raw[:], in_=rows)
             words = raw[:].bitcast(F32)
-            for half in range(2):
-                planes = [words[:, (4 * half + j) * P : (4 * half + j + 1) * P] for j in range(4)]
-                copy = nc.vector.tensor_copy if half == 0 else nc.scalar.copy
-                grouped = planes_to_grouped(planes, copy)
+            banks = [transpose_planes(words[:, 4 * half * P : 4 * (half + 1) * P]) for half in range(2)]
+            return [regroup(banks[0], nc.vector.tensor_copy), regroup(banks[1], nc.scalar.copy)]
+
+        def quantise_rows(halves, codes, scales):
+            for half, grouped in enumerate(halves):
                 cols = slice(2 * half * P, 2 * (half + 1) * P)
                 quantise(grouped, codes[:, cols], scales[:, cols])
 
@@ -111,7 +118,7 @@ def tile_step1attention_pa_kernel(tc, q, k, x, Wv, out):
 
         def project_values(key_pass):
             for g in range(GROUPS):
-                sums = ps_sums.tile([P, 4, P], F32, name="sums", tag="sums")
+                sums = ps_scores.tile([P, 4, P], F32, name="v_sums", tag="z")
                 for t in range(4):
                     for c in range(HD // K_PASS):
                         cols = slice(c * P, (c + 1) * P)
@@ -133,9 +140,6 @@ def tile_step1attention_pa_kernel(tc, q, k, x, Wv, out):
                     in_=grouped[:].rearrange("p n t -> p (n t)"),
                 )
 
-        for g in range(GROUPS):
-            quantise_rows(Wv[g * P : (g + 1) * P, :], w_codes[:, g, :], w_scales[:, g, :])
-
         k_raw = keep.tile([P, Q_TILES, GD], BF16, name="k_raw")
         q_raw = {}
 
@@ -143,174 +147,208 @@ def tile_step1attention_pa_kernel(tc, q, k, x, Wv, out):
             q_raw[it] = q_pool.tile([P, HD], BF16, name="q_raw")
             nc.sync.dma_start(out=q_raw[it][:], in_=q_rows[it * P : (it + 1) * P, :])
 
-        for key_pass in range(S // K_PASS):
-            for t in range(4):
-                tile_no = 4 * key_pass + t
-                quantise_rows(x_tiles[tile_no // 2, tile_no % 2], x_codes[:, tile_no, :], x_scales[:, tile_no, :])
-            if key_pass == 0:
+        row_tiles = [(Wv[g * P : (g + 1) * P, :], w_codes[:, g, :], w_scales[:, g, :]) for g in range(GROUPS)]
+        row_tiles.extend(
+            (x_tiles[n // 2, n % 2], x_codes[:, n, :], x_scales[:, n, :]) for n in range(Q_TILES)
+        )
+        spread = []
+        for n in range(len(row_tiles) + 1):
+            if n < len(row_tiles):
+                spread.append(spread_rows(row_tiles[n][0]))
+            if n >= 1:
+                quantise_rows(spread[n - 1], row_tiles[n - 1][1], row_tiles[n - 1][2])
+            if n == GROUPS:
+                build_neg_root()
+                for h in range(HEADS):
+                    scale_bias(h, 0)
+            if n == GROUPS + 4:
                 nc.sync.dma_start(out=k_raw[:], in_=k_rows.rearrange("(t p) c -> p t c", p=P))
                 for it in range(3):
                     load_queries(it)
-            project_values(key_pass)
+                project_values(0)
+        project_values(1)
 
         kT = keep.tile([P, GROUPS, S], BF16, name="kT")
         qT_pool = ctx.enter_context(tc.tile_pool(name="qT_pool", bufs=2))
         qT = {}
 
-        def transpose_queries_and_keys(it):
-            qT[it] = qT_pool.tile([P, HEADS, P], BF16, name="qT")
-            for half in range(2):
+        def transpose_part(it, part):
+            if part == 0:
+                qT[it] = qT_pool.tile([P, HEADS, P], BF16, name="qT")
+            if part < 2:
                 bank = ps_planes.tile([P, 8, P], BF16, name="bank_q", tag="planes")
                 for j in range(8):
-                    h = 8 * half + j
+                    h = 8 * part + j
                     nc.tensor.transpose(out=bank[:, j, :], in_=q_raw[it][:, h * P : (h + 1) * P], identity=ident_bf[:])
-                nc.scalar.copy(out=qT[it][:, 8 * half : 8 * (half + 1), :], in_=bank[:])
-            bank = ps_planes.tile([P, GROUPS, P], BF16, name="bank_k", tag="planes")
-            for g in range(GROUPS):
-                nc.tensor.transpose(out=bank[:, g, :], in_=k_raw[:, it, g * P : (g + 1) * P], identity=ident_bf[:])
-            nc.scalar.copy(out=kT[:, :, it * P : (it + 1) * P], in_=bank[:])
-            if it + 3 < Q_TILES:
-                load_queries(it + 3)
+            else:
+                bank = ps_planes.tile([P, GROUPS, P], BF16, name="bank_k", tag="planes")
+                for g in range(GROUPS):
+                    nc.tensor.transpose(out=bank[:, g, :], in_=k_raw[:, it, g * P : (g + 1) * P], identity=ident_bf[:])
+            return bank
 
-        s_pool = ctx.enter_context(tc.tile_pool(name="s_pool", bufs=2))
-        bias_pool = ctx.enter_context(tc.tile_pool(name="bias_pool", bufs=2))
+        def keep_part(it, part, bank):
+            if part < 2:
+                nc.scalar.copy(out=qT[it][:, 8 * part : 8 * (part + 1), :], in_=bank[:])
+            else:
+                nc.scalar.copy(out=kT[:, :, it * P : (it + 1) * P], in_=bank[:])
+                if it + 3 < Q_TILES:
+                    load_queries(it + 3)
+
+        packs = []
+        for it in range(Q_TILES):
+            keys = P * (it + 1)
+            for g in range(GROUPS):
+                if keys <= K_PASS:
+                    pairs = [[(r, 0, keys), (r + 1, 0, keys)] for r in range(0, REP, 2)]
+                else:
+                    pairs = [[(r, 0, K_PASS), (r, K_PASS, keys - K_PASS)] for r in range(REP)]
+                for slot, banks in enumerate(pairs):
+                    packs.append(
+                        {"it": it, "g": g, "banks": banks, "slot": slot, "last": slot == len(pairs) - 1,
+                         "turn": g * len(pairs) + slot}
+                    )
+
         stats = ctx.enter_context(tc.tile_pool(name="stats", bufs=4))
         e_codes_pool = ctx.enter_context(tc.tile_pool(name="e_codes_pool", bufs=3))
         o_pool = ctx.enter_context(tc.tile_pool(name="o_pool", bufs=3))
-        e_ring = [keep.tile([P, S], BF16, name="e_ring%d" % n) for n in range(E_RING)]
+        e_ring = [keep.tile([P, 2, K_PASS], BF16, name="e_ring%d" % n) for n in range(E_RING)]
+        unit = {}
 
-        units = [(it, g) for it in range(Q_TILES) for g in range(GROUPS)]
-        live = {}
-
-        def scores(n):
-            it, g = units[n]
-            keys = P * (it + 1)
-            z = s_pool.tile([P, REP, S], F32, name="z")
-            bias = bias_pool.tile([P, REP, S], F32, name="bias")
-            for r in range(REP):
+        def fill(m):
+            pack = packs[m]
+            it, g = pack["it"], pack["g"]
+            pack["z"] = []
+            for r, k0, width in pack["banks"]:
                 h = REP * g + r
-                slope = 2.0 ** (-(h + 1) / 2.0)
-                nc.gpsimd.tensor_scalar(
-                    out=bias[:, r, :keys], in0=neg_root[:, :keys], scalar1=slope / SCALE, scalar2=0.0,
-                    op0=ALU.mult, op1=ALU.add,
+                z = ps_scores.tile([P, K_PASS], F32, name="z")
+                nc.tensor.matmul(
+                    out=z[:, :width], lhsT=qT[it][:, h, :], rhs=kT[:, g, k0 : k0 + width], start=True, stop=False
                 )
-                for k0 in range(0, keys, BANK):
-                    width = min(BANK, keys - k0)
-                    qk = ps_scores.tile([P, BANK], F32, name="qk")
+                for j in range(width // P):
+                    delta = it - (k0 // P + j)
                     nc.tensor.matmul(
-                        out=qk[:, :width], lhsT=qT[it][:, h, :], rhs=kT[:, g, k0 : k0 + width], start=True, stop=False
+                        out=z[:, j * P : (j + 1) * P],
+                        lhsT=bias[:, h, delta * P : (delta + 1) * P],
+                        rhs=ident_f32[:],
+                        is_transpose=True,
+                        start=False,
+                        stop=(j == width // P - 1),
                     )
-                    for j in range(width // P):
-                        delta = it - (k0 // P + j)
-                        nc.tensor.matmul(
-                            out=qk[:, j * P : (j + 1) * P],
-                            lhsT=bias[:, r, delta * P : (delta + 1) * P],
-                            rhs=ident_f32[:],
-                            is_transpose=True,
-                            start=False,
-                            stop=(j == width // P - 1),
-                        )
-                    nc.vector.tensor_copy(out=z[:, r, k0 : k0 + width], in_=qk[:, :width])
-            live[n] = {"z": z}
+                pack["z"].append(z)
+                if k0 == 0 and it + 1 < Q_TILES:
+                    scale_bias(h, it + 1)
 
-        def row_maxima(n):
-            it, g = units[n]
-            neg_max = stats.tile([P, REP], F32, name="neg_max")
-            nc.vector.tensor_reduce(
-                out=neg_max[:], in_=live[n]["z"][:, :, : P * (it + 1)], axis=AXIS.X, op=ALU.max, negate=True
-            )
-            live[n]["neg_max"] = neg_max
-
-        def exp_biases(n):
-            exp_bias = stats.tile([P, REP], F32, name="exp_bias")
-            nc.scalar.mul(out=exp_bias[:], in_=live[n]["neg_max"][:], mul=SCALE)
-            live[n]["exp_bias"] = exp_bias
-
-        def exponentials(n):
-            it, g = units[n]
-            keys = P * (it + 1)
-            first = 0 if keys > K_PASS else K_PASS
-            if it % 4 == 0 and g == 0:
-                for e_tile in e_ring:
-                    nc.gpsimd.memset(e_tile[:, K_PASS + P :], 0.0)
-            row_sum = stats.tile([P, REP], F32, name="row_sum")
-            for r in range(REP):
-                nc.scalar.activation(
-                    out=e_ring[(REP * n + r) % E_RING][:, first : first + keys],
-                    in_=live[n]["z"][:, r, :keys],
-                    func=ACT.Exp,
-                    bias=live[n]["exp_bias"][:, r : r + 1],
-                    scale=SCALE,
-                    accum_out=row_sum[:, r : r + 1],
+        def maxima(m):
+            pack = packs[m]
+            neg_max = stats.tile([P, 2], F32, name="neg_max")
+            for c, (r, k0, width) in enumerate(pack["banks"]):
+                nc.vector.tensor_reduce(
+                    out=neg_max[:, c : c + 1], in_=pack["z"][c][:, :width], axis=AXIS.X, op=ALU.max, negate=True
                 )
-            live[n]["row_sum"] = row_sum
+            exp_bias = stats.tile([P, 2], F32, name="exp_bias")
+            if pack["banks"][0][0] != pack["banks"][1][0]:
+                nc.gpsimd.tensor_scalar(
+                    out=exp_bias[:], in0=neg_max[:], scalar1=SCALE, scalar2=0.0, op0=ALU.mult, op1=ALU.add
+                )
+                pack["exp_bias"] = [exp_bias[:, 0:1], exp_bias[:, 1:2]]
+            else:
+                nc.gpsimd.tensor_scalar(
+                    out=exp_bias[:, 0:1], in0=neg_max[:, 0:1], scalar1=neg_max[:, 1:2], scalar2=SCALE,
+                    op0=ALU.min, op1=ALU.mult,
+                )
+                pack["exp_bias"] = [exp_bias[:, 0:1], exp_bias[:, 0:1]]
 
-        def transpose_e(n):
-            it, g = units[n]
-            first_plane = 0 if P * (it + 1) > K_PASS else K_PASS // PLANE
-            planes = []
-            for r in range(REP):
-                words = e_ring[(REP * n + r) % E_RING][:].bitcast(F32)
-                planes.extend(words[:, a * P : (a + 1) * P] for a in range(first_plane, S // PLANE))
-            live[n]["grouped"] = [
-                planes_to_grouped(planes[b : b + 4], nc.scalar.copy) for b in range(0, len(planes), 4)
-            ]
+        def exponentials(m):
+            pack = packs[m]
+            it, g = pack["it"], pack["g"]
+            if it % 4 == 0 and g == 0 and pack["slot"] == 0:
+                for e_tile in e_ring:
+                    nc.vector.memset(e_tile[:, :, P:], 0.0)
+            if pack["slot"] == 0:
+                unit[(it, g)] = {"row_sums": stats.tile([P, 2 * REP], F32, name="row_sums")}
+            for c, (r, k0, width) in enumerate(pack["banks"]):
+                col = 2 * pack["slot"] + c
+                nc.scalar.activation(
+                    out=e_ring[m % E_RING][:, c, :width],
+                    in_=pack["z"][c][:, :width],
+                    func=ACT.Exp,
+                    bias=pack["exp_bias"][c],
+                    scale=SCALE,
+                    accum_out=unit[(it, g)]["row_sums"][:, col : col + 1],
+                )
 
-        def quantise_e(n):
-            e_codes = e_codes_pool.tile([P, 2 * REP * P], U32, name="e_codes", align_bytes=64)
-            e_scales = e_codes_pool.tile([P, 2 * REP * P], U8, name="e_scales", align_bytes=64)
-            for b, grouped in enumerate(live[n]["grouped"]):
-                cols = slice(2 * b * P, 2 * (b + 1) * P)
-                quantise(grouped, e_codes[:, cols], e_scales[:, cols])
-            live[n]["e_codes"] = e_codes
-            live[n]["e_scales"] = e_scales
+        def quantise_e(m):
+            pack = packs[m]
+            tiles = unit[(pack["it"], pack["g"])]
+            if pack["slot"] == 0:
+                tiles["e_codes"] = e_codes_pool.tile([P, 2 * REP * P], U32, name="e_codes", align_bytes=64)
+                tiles["e_scales"] = e_codes_pool.tile([P, 2 * REP * P], U8, name="e_scales", align_bytes=64)
+            cols = slice(2 * pack["slot"] * P, 2 * (pack["slot"] + 1) * P)
+            quantise(pack["grouped"], tiles["e_codes"][:, cols], tiles["e_scales"][:, cols])
 
-        def reciprocals(n):
-            inv_sum = stats.tile([P, REP], F32, name="inv_sum")
-            nc.vector.reciprocal(out=inv_sum[:], in_=live[n]["row_sum"][:])
-            live[n]["inv_sum"] = inv_sum
-
-        def weighted_values(n):
-            it, g = units[n]
+        def weighted_values(it, g):
+            tiles = unit[(it, g)]
             passes = (P * (it + 1) + K_PASS - 1) // K_PASS
+            inv_sum = stats.tile([P, REP], F32, name="inv_sum")
+            if passes == 1:
+                nc.vector.reciprocal(out=inv_sum[:], in_=tiles["row_sums"][:, :REP])
+            else:
+                halves = tiles["row_sums"][:].rearrange("p (r c) -> p r c", c=2)
+                row_sum = stats.tile([P, REP], F32, name="row_sum")
+                nc.gpsimd.tensor_tensor(out=row_sum[:], in0=halves[:, :, 0], in1=halves[:, :, 1], op=ALU.add)
+                nc.vector.reciprocal(out=inv_sum[:], in_=row_sum[:])
             sums = ps_sums.tile([P, REP, P], F32, name="o_sums", tag="sums")
             for r in range(REP):
                 for c in range(passes):
                     cols = slice((r * passes + c) * P, (r * passes + c + 1) * P)
                     nc.tensor.matmul_mx(
                         out=sums[:, r, :],
-                        lhsT=live[n]["e_codes"][:, cols].bitcast(FP8X4),
-                        lhsT_scale=live[n]["e_scales"][:, cols],
+                        lhsT=tiles["e_codes"][:, cols].bitcast(FP8X4),
+                        lhsT_scale=tiles["e_scales"][:, cols],
                         rhs=v_codes[:, c, g * P : (g + 1) * P].bitcast(FP8X4),
                         rhs_scale=v_scales[:, c, g * P : (g + 1) * P],
                         start=(c == 0),
                         stop=(c == passes - 1),
                     )
+            tiles["sums"] = sums
+            tiles["inv_sum"] = inv_sum
+
+        def divide_and_store(it, g):
+            tiles = unit[(it, g)]
             o = o_pool.tile([P, REP * P], F32, name="o")
             for r in range(REP):
                 nc.scalar.activation(
                     out=o[:, r * P : (r + 1) * P],
-                    in_=sums[:, r, :],
+                    in_=tiles["sums"][:, r, :],
                     func=ACT.Copy,
-                    scale=live[n]["inv_sum"][:, r : r + 1],
+                    scale=tiles["inv_sum"][:, r : r + 1],
                 )
-            nc.gpsimd.dma_start(out=out_rows[it * P : (it + 1) * P, g * REP * P : (g + 1) * REP * P], in_=o[:])
+            nc.sync.dma_start(out=out_rows[it * P : (it + 1) * P, g * REP * P : (g + 1) * REP * P], in_=o[:])
 
-        transpose_queries_and_keys(0)
-        for n in range(len(units) + 2):
-            if n < len(units):
-                scores(n)
-            if 0 <= n - 2:
-                quantise_e(n - 2)
-            if n < len(units):
-                row_maxima(n)
-            if 0 <= n - 1 < len(units):
-                exponentials(n - 1)
-                transpose_e(n - 1)
-                reciprocals(n - 1)
-            if n < len(units) and units[n][1] == 1 and units[n][0] + 1 < Q_TILES:
-                transpose_queries_and_keys(units[n][0] + 1)
-            if 0 <= n - 2:
-                weighted_values(n - 2)
-            if n < len(units):
-                exp_biases(n)
+        for part in range(3):
+            keep_part(0, part, transpose_part(0, part))
+        count = len(packs)
+        for m in range(-1, count + 5):
+            if 0 <= m - 2 < count:
+                words = e_ring[(m - 2) % E_RING][:].rearrange("p c k -> p (c k)").bitcast(F32)
+                packs[m - 2]["bank"] = transpose_planes(words)
+            part = packs[m]["turn"] - 1 if 0 <= m < count and packs[m]["it"] + 1 < Q_TILES else -1
+            if 0 <= part < 3:
+                part_bank = transpose_part(packs[m]["it"] + 1, part)
+            if m + 1 < count:
+                fill(m + 1)
+            if 0 <= m < count:
+                maxima(m)
+            if 0 <= m - 1 < count:
+                exponentials(m - 1)
+            if 0 <= m - 2 < count:
+                copy = nc.scalar.copy if (m - 2) % 2 == 0 else nc.vector.tensor_copy
+                packs[m - 2]["grouped"] = regroup(packs[m - 2]["bank"], copy)
+            if 0 <= part < 3:
+                keep_part(packs[m]["it"] + 1, part, part_bank)
+            if 0 <= m - 4 < count and packs[m - 4]["last"]:
+                divide_and_store(packs[m - 4]["it"], packs[m - 4]["g"])
+            if 0 <= m - 3 < count:
+                quantise_e(m - 3)
+                if packs[m - 3]["last"]:
+                    weighted_values(packs[m - 3]["it"], packs[m - 3]["g"])

@@ -315,20 +315,19 @@ def tile_step1attention_pa_kernel(tc, q, k, x, Wv, out):
 
         def divide_and_store(it, g):
             tiles = unit[(it, g)]
-            o = o_pool.tile([P, REP * P], F32, name="o")
-            for r in range(REP):
-                nc.scalar.activation(
-                    out=o[:, r * P : (r + 1) * P],
-                    in_=tiles["sums"][:, r, :],
-                    func=ACT.Copy,
-                    scale=tiles["inv_sum"][:, r : r + 1],
-                )
-            nc.sync.dma_start(out=out_rows[it * P : (it + 1) * P, g * REP * P : (g + 1) * REP * P], in_=o[:])
+            o = o_pool.tile([P, REP, P], F32, name="o")
+            nc.vector.tensor_tensor(
+                out=o[:],
+                in0=tiles["sums"][:],
+                in1=tiles["inv_sum"][:].unsqueeze(2).to_broadcast([P, REP, P]),
+                op=ALU.mult,
+            )
+            nc.sync.dma_start(out=out_rows[it * P : (it + 1) * P, g * REP * P : (g + 1) * REP * P], in_=o[:].rearrange("p r d -> p (r d)"))
 
         for part in range(3):
             keep_part(0, part, transpose_part(0, part))
         count = len(packs)
-        for m in range(-1, count + 5):
+        for m in range(-1, count + 6):
             if 0 <= m - 2 < count:
                 words = e_ring[(m - 2) % E_RING][:].rearrange("p c k -> p (c k)").bitcast(F32)
                 packs[m - 2]["bank"] = transpose_planes(words)
@@ -337,18 +336,17 @@ def tile_step1attention_pa_kernel(tc, q, k, x, Wv, out):
                 part_bank = transpose_part(packs[m]["it"] + 1, part)
             if m + 1 < count:
                 fill(m + 1)
+            if 0 <= m - 4 < count and packs[m - 4]["last"]:
+                weighted_values(packs[m - 4]["it"], packs[m - 4]["g"])
             if 0 <= m < count:
                 maxima(m)
             if 0 <= m - 1 < count:
                 exponentials(m - 1)
             if 0 <= m - 2 < count:
-                copy = nc.scalar.copy if (m - 2) % 2 == 0 else nc.vector.tensor_copy
-                packs[m - 2]["grouped"] = regroup(packs[m - 2]["bank"], copy)
+                packs[m - 2]["grouped"] = regroup(packs[m - 2]["bank"], nc.scalar.copy)
             if 0 <= part < 3:
                 keep_part(packs[m]["it"] + 1, part, part_bank)
-            if 0 <= m - 4 < count and packs[m - 4]["last"]:
-                divide_and_store(packs[m - 4]["it"], packs[m - 4]["g"])
+            if 0 <= m - 5 < count and packs[m - 5]["last"]:
+                divide_and_store(packs[m - 5]["it"], packs[m - 5]["g"])
             if 0 <= m - 3 < count:
                 quantise_e(m - 3)
-                if packs[m - 3]["last"]:
-                    weighted_values(packs[m - 3]["it"], packs[m - 3]["g"])

@@ -224,6 +224,13 @@ def tile_step1attention_pa_kernel(tc, q, k, x, Wv, out):
                 nc.tensor.matmul(
                     out=z[:, :width], lhsT=qT[it][:, h, :], rhs=kT[:, g, k0 : k0 + width], start=True, stop=False
                 )
+                pack["z"].append(z)
+
+        def add_bias(m):
+            pack = packs[m]
+            it, g = pack["it"], pack["g"]
+            for z, (r, k0, width) in zip(pack["z"], pack["banks"]):
+                h = REP * g + r
                 for j in range(width // P):
                     delta = it - (k0 // P + j)
                     nc.tensor.matmul(
@@ -234,7 +241,6 @@ def tile_step1attention_pa_kernel(tc, q, k, x, Wv, out):
                         start=False,
                         stop=(j == width // P - 1),
                     )
-                pack["z"].append(z)
                 if k0 == 0 and it + 1 < Q_TILES:
                     scale_bias(h, it + 1)
 
@@ -328,16 +334,18 @@ def tile_step1attention_pa_kernel(tc, q, k, x, Wv, out):
             keep_part(0, part, transpose_part(0, part))
         count = len(packs)
         for m in range(-1, count + 6):
+            if m + 1 < count:
+                fill(m + 1)
+            if 0 <= m - 4 < count and packs[m - 4]["last"]:
+                weighted_values(packs[m - 4]["it"], packs[m - 4]["g"])
+            if m + 1 < count:
+                add_bias(m + 1)
             if 0 <= m - 2 < count:
                 words = e_ring[(m - 2) % E_RING][:].rearrange("p c k -> p (c k)").bitcast(F32)
                 packs[m - 2]["bank"] = transpose_planes(words)
             part = packs[m]["turn"] - 1 if 0 <= m < count and packs[m]["it"] + 1 < Q_TILES else -1
             if 0 <= part < 3:
                 part_bank = transpose_part(packs[m]["it"] + 1, part)
-            if m + 1 < count:
-                fill(m + 1)
-            if 0 <= m - 4 < count and packs[m - 4]["last"]:
-                weighted_values(packs[m - 4]["it"], packs[m - 4]["g"])
             if 0 <= m < count:
                 maxima(m)
             if 0 <= m - 1 < count:

@@ -334,18 +334,18 @@ def tile_step1attention_pa_kernel(tc, q, k, x, Wv, out):
             keep_part(0, part, transpose_part(0, part))
         count = len(packs)
         for m in range(-1, count + 6):
-            if m + 1 < count:
-                fill(m + 1)
-            if 0 <= m - 4 < count and packs[m - 4]["last"]:
-                weighted_values(packs[m - 4]["it"], packs[m - 4]["g"])
-            if m + 1 < count:
-                add_bias(m + 1)
             if 0 <= m - 2 < count:
                 words = e_ring[(m - 2) % E_RING][:].rearrange("p c k -> p (c k)").bitcast(F32)
                 packs[m - 2]["bank"] = transpose_planes(words)
             part = packs[m]["turn"] - 1 if 0 <= m < count and packs[m]["it"] + 1 < Q_TILES else -1
             if 0 <= part < 3:
                 part_bank = transpose_part(packs[m]["it"] + 1, part)
+            if m + 1 < count:
+                fill(m + 1)
+            if 0 <= m - 4 < count and packs[m - 4]["last"]:
+                weighted_values(packs[m - 4]["it"], packs[m - 4]["g"])
+            if m + 1 < count:
+                add_bias(m + 1)
             if 0 <= m < count:
                 maxima(m)
             if 0 <= m - 1 < count:

@@ -26,6 +26,7 @@ SCALE = 1.0 / math.sqrt(P)
 MASKED = 1.0e30
 TINY = 1.0e-30
 E_RING = 4
+E_LATER = 4
 
 FLOPS = 2 * S * HD * GD + 2 * 2 * HEADS * P * (K_PASS * K_PASS + K_PASS * S)
 
@@ -42,30 +43,69 @@ def tile_step1attention_pa_kernel(tc, q, k, x, Wv, out):
         keep = ctx.enter_context(tc.tile_pool(name="keep", bufs=1))
         loads = ctx.enter_context(tc.tile_pool(name="loads", bufs=4))
         q_pool = ctx.enter_context(tc.tile_pool(name="q_pool", bufs=3))
+        qT_pool = ctx.enter_context(tc.tile_pool(name="qT_pool", bufs=2))
         grouped_pool = ctx.enter_context(tc.tile_pool(name="grouped_pool", bufs=6))
-        ps_scores = ctx.enter_context(tc.psum_pool(name="ps_scores", bufs=5))
-        ps_planes = ctx.enter_context(tc.psum_pool(name="ps_planes", bufs=2))
-        ps_sums = ctx.enter_context(tc.psum_pool(name="ps_sums", bufs=1))
+        stats = ctx.enter_context(tc.tile_pool(name="stats", bufs=6))
+        e_codes_pool = ctx.enter_context(tc.tile_pool(name="e_codes_pool", bufs=6))
+        o_pool = ctx.enter_context(tc.tile_pool(name="o_pool", bufs=3))
+        ps_scores = ctx.enter_context(tc.psum_pool(name="ps_scores", bufs=6))
+        ps_other = ctx.enter_context(tc.psum_pool(name="ps_other", bufs=2))
 
-        ident_bf = keep.tile([P, P], BF16, name="ident_bf")
-        make_identity(nc, ident_bf[:])
-        ident_f32 = keep.tile([P, P], F32, name="ident_f32")
-        make_identity(nc, ident_f32[:])
+        k_raw = [keep.tile([P, GD], BF16, name="k_raw%d" % t) for t in range(Q_TILES)]
+        q_raw = {}
+        raw = {}
+
+        def load_keys(t):
+            nc.sync.dma_start(out=k_raw[t][:], in_=k_rows[t * P : (t + 1) * P, :])
+
+        def load_queries(it):
+            q_raw[it] = q_pool.tile([P, HD], BF16, name="q_raw")
+            nc.sync.dma_start(out=q_raw[it][:], in_=q_rows[it * P : (it + 1) * P, :])
+
+        w_codes = keep.tile([P, GROUPS, 4 * P], U32, name="w_codes", align_bytes=64)
+        w_scales = keep.tile([P, GROUPS, 4 * P], U8, name="w_scales", align_bytes=64)
+        x_codes = keep.tile([P, Q_TILES, 4 * P], U32, name="x_codes", align_bytes=64)
+        x_scales = keep.tile([P, Q_TILES, 4 * P], U8, name="x_scales", align_bytes=64)
+        v_codes = keep.tile([P, S // K_PASS, GD], U32, name="v_codes", align_bytes=64)
+        v_scales = keep.tile([P, S // K_PASS, GD], U8, name="v_scales", align_bytes=64)
+
+        x_tiles = x_rows.rearrange("(a p e) c -> a e p c", p=P, e=2)
+        w_tile = [(Wv[g * P : (g + 1) * P, :], w_codes[:, g, :], w_scales[:, g, :]) for g in range(GROUPS)]
+        x_tile = [(x_tiles[n // 2, n % 2], x_codes[:, n, :], x_scales[:, n, :]) for n in range(Q_TILES)]
+        row_tiles = [w_tile[0]] + x_tile[:4] + w_tile[1:] + x_tile[4:]
+
+        def load_rows(n):
+            raw[n] = loads.tile([P, HD], BF16, name="raw")
+            nc.sync.dma_start(out=raw[n][:], in_=row_tiles[n][0])
+
+        load_keys(0)
+        load_queries(0)
+        for n in range(4):
+            load_rows(n)
+        load_keys(1)
+        load_queries(1)
 
         dist = keep.tile([P, S], F32, name="dist")
         nc.gpsimd.iota(
             dist[:], pattern=[[1, S]], base=0, channel_multiplier=-1, allow_small_or_imprecise_dtypes=True
         )
+        ident_bf = keep.tile([P, P], BF16, name="ident_bf")
+        make_identity(nc, ident_bf[:])
+        ident_f32 = keep.tile([P, P], F32, name="ident_f32")
+        make_identity(nc, ident_f32[:])
         future = keep.tile([P, S], F32, name="future")
         root = keep.tile([P, S], F32, name="root")
         neg_root = keep.tile([P, S], F32, name="neg_root")
-
-        def build_neg_root():
-            nc.vector.tensor_scalar(out=root[:], in0=dist[:], scalar1=0.0, scalar2=TINY, op0=ALU.max, op1=ALU.add)
-            nc.scalar.activation(out=root[:], in_=root[:], func=ACT.Sqrt)
-            nc.vector.tensor_scalar(out=future[:], in0=dist[:], scalar1=0.0, scalar2=MASKED, op0=ALU.min, op1=ALU.mult)
+        for cols in (slice(0, P), slice(P, S)):
+            nc.vector.tensor_scalar(
+                out=root[:, cols], in0=dist[:, cols], scalar1=0.0, scalar2=TINY, op0=ALU.max, op1=ALU.add
+            )
+            nc.scalar.activation(out=root[:, cols], in_=root[:, cols], func=ACT.Sqrt)
+            nc.vector.tensor_scalar(
+                out=future[:, cols], in0=dist[:, cols], scalar1=0.0, scalar2=MASKED, op0=ALU.min, op1=ALU.mult
+            )
             nc.vector.scalar_tensor_tensor(
-                out=neg_root[:], in0=root[:], scalar=-1.0, in1=future[:], op0=ALU.mult, op1=ALU.add
+                out=neg_root[:, cols], in0=root[:, cols], scalar=-1.0, in1=future[:, cols], op0=ALU.mult, op1=ALU.add
             )
 
         bias = keep.tile([P, HEADS, S], F32, name="bias")
@@ -78,8 +118,18 @@ def tile_step1attention_pa_kernel(tc, q, k, x, Wv, out):
                 op0=ALU.mult, op1=ALU.add,
             )
 
-        def transpose_planes(words):
-            bank = ps_planes.tile([P, 4, P], F32, name="bank", tag="planes")
+        for h in range(HEADS):
+            scale_bias(h, 0)
+
+        e_early = [keep.tile([P, 2, K_PASS], BF16, name="e_early%d" % n) for n in range(E_RING)]
+        e_late = [keep.tile([P, 2, K_PASS], BF16, name="e_late%d" % n) for n in range(E_RING)]
+        for e_tile in e_early:
+            nc.vector.memset(e_tile[:].bitcast(F32)[:, :, P // 2 :], 0.0)
+        for e_tile in e_late:
+            nc.vector.memset(e_tile[:].bitcast(F32)[:, 1, P // 2 :], 0.0)
+
+        def transpose_planes(words, pool, tag):
+            bank = pool.tile([P, 4, P], F32, name="bank", tag=tag)
             for a in range(4):
                 nc.tensor.transpose(out=bank[:, a, :], in_=words[:, a * P : (a + 1) * P], identity=ident_f32[:])
             return bank
@@ -95,104 +145,81 @@ def tile_step1attention_pa_kernel(tc, q, k, x, Wv, out):
         def quantise(grouped, codes, scales):
             nc.vector.quantize_mx(out=codes.bitcast(FP8X4), scales=scales, in_=grouped[:])
 
-        w_codes = keep.tile([P, GROUPS, 4 * P], U32, name="w_codes", align_bytes=64)
-        w_scales = keep.tile([P, GROUPS, 4 * P], U8, name="w_scales", align_bytes=64)
-        x_codes = keep.tile([P, Q_TILES, 4 * P], U32, name="x_codes", align_bytes=64)
-        x_scales = keep.tile([P, Q_TILES, 4 * P], U8, name="x_scales", align_bytes=64)
-        v_codes = keep.tile([P, S // K_PASS, GD], U32, name="v_codes", align_bytes=64)
-        v_scales = keep.tile([P, S // K_PASS, GD], U8, name="v_scales", align_bytes=64)
+        banks = {}
+        halves = {}
 
-        def spread_rows(rows):
-            raw = loads.tile([P, HD], BF16, name="raw")
-            nc.sync.dma_start(out=raw[:], in_=rows)
-            words = raw[:].bitcast(F32)
-            banks = [transpose_planes(words[:, 4 * half * P : 4 * (half + 1) * P]) for half in range(2)]
-            return [regroup(banks[0], nc.vector.tensor_copy), regroup(banks[1], nc.scalar.copy)]
+        def spread_transposes(n):
+            words = raw[n][:].bitcast(F32)
+            banks[n] = [
+                transpose_planes(words[:, 4 * half * P : 4 * (half + 1) * P], ps_scores, "z") for half in range(2)
+            ]
 
-        def quantise_rows(halves, codes, scales):
-            for half, grouped in enumerate(halves):
+        def spread_copies(n):
+            halves[n] = [regroup(banks[n][0], nc.vector.tensor_copy), regroup(banks[n][1], nc.scalar.copy)]
+
+        def quantise_rows(n):
+            for half, grouped in enumerate(halves[n]):
                 cols = slice(2 * half * P, 2 * (half + 1) * P)
-                quantise(grouped, codes[:, cols], scales[:, cols])
+                quantise(grouped, row_tiles[n][1][:, cols], row_tiles[n][2][:, cols])
 
-        x_tiles = x_rows.rearrange("(a p e) c -> a e p c", p=P, e=2)
+        v_sums = {}
+        v_grouped = {}
 
-        def project_values(key_pass):
-            for g in range(GROUPS):
-                sums = ps_scores.tile([P, 4, P], F32, name="v_sums", tag="z")
-                for t in range(4):
-                    for c in range(HD // K_PASS):
-                        cols = slice(c * P, (c + 1) * P)
-                        nc.tensor.matmul_mx(
-                            out=sums[:, t, :],
-                            lhsT=x_codes[:, 4 * key_pass + t, cols].bitcast(FP8X4),
-                            lhsT_scale=x_scales[:, 4 * key_pass + t, cols],
-                            rhs=w_codes[:, g, cols].bitcast(FP8X4),
-                            rhs_scale=w_scales[:, g, cols],
-                            start=(c == 0),
-                            stop=(c == HD // K_PASS - 1),
-                        )
-                grouped = grouped_pool.tile([P, P, 4], BF16, name="grouped_v", tag="grouped", align_bytes=64)
-                nc.scalar.copy(out=grouped[:], in_=sums[:].rearrange("p t n -> p n t"))
-                cols = slice(g * P, (g + 1) * P)
-                nc.vector.quantize_mx(
-                    out=v_codes[:, key_pass, cols].bitcast(FP8X4),
-                    scales=v_scales[:, key_pass, cols],
-                    in_=grouped[:].rearrange("p n t -> p (n t)"),
-                )
+        def project_values(key_pass, g):
+            sums = ps_scores.tile([P, 4, P], F32, name="v_sums", tag="z")
+            for t in range(4):
+                for c in range(HD // K_PASS):
+                    cols = slice(c * P, (c + 1) * P)
+                    nc.tensor.matmul_mx(
+                        out=sums[:, t, :],
+                        lhsT=x_codes[:, 4 * key_pass + t, cols].bitcast(FP8X4),
+                        lhsT_scale=x_scales[:, 4 * key_pass + t, cols],
+                        rhs=w_codes[:, g, cols].bitcast(FP8X4),
+                        rhs_scale=w_scales[:, g, cols],
+                        start=(c == 0),
+                        stop=(c == HD // K_PASS - 1),
+                    )
+            v_sums[(key_pass, g)] = sums
 
-        k_raw = keep.tile([P, Q_TILES, GD], BF16, name="k_raw")
-        q_raw = {}
+        def group_values(key_pass, g):
+            grouped = grouped_pool.tile([P, P, 4], BF16, name="grouped_v", tag="grouped", align_bytes=64)
+            nc.scalar.copy(out=grouped[:], in_=v_sums[(key_pass, g)][:].rearrange("p t n -> p n t"))
+            v_grouped[(key_pass, g)] = grouped
 
-        def load_queries(it):
-            q_raw[it] = q_pool.tile([P, HD], BF16, name="q_raw")
-            nc.sync.dma_start(out=q_raw[it][:], in_=q_rows[it * P : (it + 1) * P, :])
+        def quantise_values(key_pass, g):
+            cols = slice(g * P, (g + 1) * P)
+            nc.vector.quantize_mx(
+                out=v_codes[:, key_pass, cols].bitcast(FP8X4),
+                scales=v_scales[:, key_pass, cols],
+                in_=v_grouped[(key_pass, g)][:].rearrange("p n t -> p (n t)"),
+            )
 
-        row_tiles = [(Wv[g * P : (g + 1) * P, :], w_codes[:, g, :], w_scales[:, g, :]) for g in range(GROUPS)]
-        row_tiles.extend(
-            (x_tiles[n // 2, n % 2], x_codes[:, n, :], x_scales[:, n, :]) for n in range(Q_TILES)
-        )
-        spread = []
-        for n in range(len(row_tiles) + 1):
-            if n < len(row_tiles):
-                spread.append(spread_rows(row_tiles[n][0]))
-            if n >= 1:
-                quantise_rows(spread[n - 1], row_tiles[n - 1][1], row_tiles[n - 1][2])
-            if n == GROUPS:
-                build_neg_root()
-                for h in range(HEADS):
-                    scale_bias(h, 0)
-            if n == GROUPS + 4:
-                nc.sync.dma_start(out=k_raw[:], in_=k_rows.rearrange("(t p) c -> p t c", p=P))
-                for it in range(3):
-                    load_queries(it)
-                project_values(0)
-        project_values(1)
-
-        kT = keep.tile([P, GROUPS, S], BF16, name="kT")
-        qT_pool = ctx.enter_context(tc.tile_pool(name="qT_pool", bufs=2))
+        kT = [keep.tile([P, GROUPS, K_PASS], BF16, name="kT%d" % c) for c in range(S // K_PASS)]
         qT = {}
 
         def transpose_part(it, part):
             if part == 0:
                 qT[it] = qT_pool.tile([P, HEADS, P], BF16, name="qT")
             if part < 2:
-                bank = ps_planes.tile([P, 8, P], BF16, name="bank_q", tag="planes")
+                bank = ps_other.tile([P, 8, P], BF16, name="bank_q", tag="other")
                 for j in range(8):
                     h = 8 * part + j
                     nc.tensor.transpose(out=bank[:, j, :], in_=q_raw[it][:, h * P : (h + 1) * P], identity=ident_bf[:])
             else:
-                bank = ps_planes.tile([P, GROUPS, P], BF16, name="bank_k", tag="planes")
+                bank = ps_other.tile([P, GROUPS, P], BF16, name="bank_k", tag="other")
                 for g in range(GROUPS):
-                    nc.tensor.transpose(out=bank[:, g, :], in_=k_raw[:, it, g * P : (g + 1) * P], identity=ident_bf[:])
+                    nc.tensor.transpose(out=bank[:, g, :], in_=k_raw[it][:, g * P : (g + 1) * P], identity=ident_bf[:])
             return bank
 
         def keep_part(it, part, bank):
             if part < 2:
-                nc.scalar.copy(out=qT[it][:, 8 * part : 8 * (part + 1), :], in_=bank[:])
+                nc.vector.tensor_copy(out=qT[it][:, 8 * part : 8 * (part + 1), :], in_=bank[:])
             else:
-                nc.scalar.copy(out=kT[:, :, it * P : (it + 1) * P], in_=bank[:])
-                if it + 3 < Q_TILES:
-                    load_queries(it + 3)
+                cols = slice((it % 4) * P, (it % 4 + 1) * P)
+                nc.scalar.copy(out=kT[it // 4][:, :, cols], in_=bank[:])
+                if it + 2 < Q_TILES:
+                    load_keys(it + 2)
+                    load_queries(it + 2)
 
         packs = []
         for it in range(Q_TILES):
@@ -202,47 +229,43 @@ def tile_step1attention_pa_kernel(tc, q, k, x, Wv, out):
                     pairs = [[(r, 0, keys), (r + 1, 0, keys)] for r in range(0, REP, 2)]
                 else:
                     pairs = [[(r, 0, K_PASS), (r, K_PASS, keys - K_PASS)] for r in range(REP)]
-                for slot, banks in enumerate(pairs):
+                for slot, bank_list in enumerate(pairs):
                     packs.append(
-                        {"it": it, "g": g, "banks": banks, "slot": slot, "last": slot == len(pairs) - 1,
-                         "turn": g * len(pairs) + slot}
+                        {"it": it, "g": g, "banks": bank_list, "slot": slot, "last": slot == len(pairs) - 1,
+                         "turn": g * len(pairs) + slot, "e": (e_early if keys <= K_PASS else e_late)[len(packs) % E_RING]}
                     )
-
-        stats = ctx.enter_context(tc.tile_pool(name="stats", bufs=4))
-        e_codes_pool = ctx.enter_context(tc.tile_pool(name="e_codes_pool", bufs=3))
-        o_pool = ctx.enter_context(tc.tile_pool(name="o_pool", bufs=3))
-        e_ring = [keep.tile([P, 2, K_PASS], BF16, name="e_ring%d" % n) for n in range(E_RING)]
         unit = {}
 
-        def fill(m):
+        def scores(m):
             pack = packs[m]
             it, g = pack["it"], pack["g"]
             pack["z"] = []
             for r, k0, width in pack["banks"]:
-                h = REP * g + r
                 z = ps_scores.tile([P, K_PASS], F32, name="z")
                 nc.tensor.matmul(
-                    out=z[:, :width], lhsT=qT[it][:, h, :], rhs=kT[:, g, k0 : k0 + width], start=True, stop=False
+                    out=z[:, :width], lhsT=qT[it][:, REP * g + r, :], rhs=kT[k0 // K_PASS][:, g, :width],
+                    start=True, stop=False,
                 )
                 pack["z"].append(z)
 
-        def add_bias(m):
+        def add_bias_bank(m, b):
             pack = packs[m]
             it, g = pack["it"], pack["g"]
-            for z, (r, k0, width) in zip(pack["z"], pack["banks"]):
-                h = REP * g + r
-                for j in range(width // P):
-                    delta = it - (k0 // P + j)
-                    nc.tensor.matmul(
-                        out=z[:, j * P : (j + 1) * P],
-                        lhsT=bias[:, h, delta * P : (delta + 1) * P],
-                        rhs=ident_f32[:],
-                        is_transpose=True,
-                        start=False,
-                        stop=(j == width // P - 1),
-                    )
-                if k0 == 0 and it + 1 < Q_TILES:
-                    scale_bias(h, it + 1)
+            r, k0, width = pack["banks"][b]
+            h = REP * g + r
+            z = pack["z"][b]
+            for j in range(width // P):
+                delta = it - (k0 // P + j)
+                nc.tensor.matmul(
+                    out=z[:, j * P : (j + 1) * P],
+                    lhsT=bias[:, h, delta * P : (delta + 1) * P],
+                    rhs=ident_f32[:],
+                    is_transpose=True,
+                    start=False,
+                    stop=(j == width // P - 1),
+                )
+            if k0 == 0 and it + 1 < Q_TILES:
+                scale_bias(h, it + 1)
 
         def maxima(m):
             pack = packs[m]
@@ -267,15 +290,12 @@ def tile_step1attention_pa_kernel(tc, q, k, x, Wv, out):
         def exponentials(m):
             pack = packs[m]
             it, g = pack["it"], pack["g"]
-            if it % 4 == 0 and g == 0 and pack["slot"] == 0:
-                for e_tile in e_ring:
-                    nc.vector.memset(e_tile[:, :, P:], 0.0)
             if pack["slot"] == 0:
                 unit[(it, g)] = {"row_sums": stats.tile([P, 2 * REP], F32, name="row_sums")}
             for c, (r, k0, width) in enumerate(pack["banks"]):
                 col = 2 * pack["slot"] + c
                 nc.scalar.activation(
-                    out=e_ring[m % E_RING][:, c, :width],
+                    out=pack["e"][:, c, :width],
                     in_=pack["z"][c][:, :width],
                     func=ACT.Exp,
                     bias=pack["exp_bias"][c],
@@ -292,18 +312,22 @@ def tile_step1attention_pa_kernel(tc, q, k, x, Wv, out):
             cols = slice(2 * pack["slot"] * P, 2 * (pack["slot"] + 1) * P)
             quantise(pack["grouped"], tiles["e_codes"][:, cols], tiles["e_scales"][:, cols])
 
+        def invert_sums(it, g):
+            tiles = unit[(it, g)]
+            inv_sum = stats.tile([P, REP], F32, name="inv_sum")
+            if it < 4:
+                nc.vector.reciprocal(out=inv_sum[:], in_=tiles["row_sums"][:, :REP])
+            else:
+                sums_of_banks = tiles["row_sums"][:].rearrange("p (r c) -> p r c", c=2)
+                row_sum = stats.tile([P, REP], F32, name="row_sum")
+                nc.gpsimd.tensor_tensor(out=row_sum[:], in0=sums_of_banks[:, :, 0], in1=sums_of_banks[:, :, 1], op=ALU.add)
+                nc.vector.reciprocal(out=inv_sum[:], in_=row_sum[:])
+            tiles["inv_sum"] = inv_sum
+
         def weighted_values(it, g):
             tiles = unit[(it, g)]
             passes = (P * (it + 1) + K_PASS - 1) // K_PASS
-            inv_sum = stats.tile([P, REP], F32, name="inv_sum")
-            if passes == 1:
-                nc.vector.reciprocal(out=inv_sum[:], in_=tiles["row_sums"][:, :REP])
-            else:
-                halves = tiles["row_sums"][:].rearrange("p (r c) -> p r c", c=2)
-                row_sum = stats.tile([P, REP], F32, name="row_sum")
-                nc.gpsimd.tensor_tensor(out=row_sum[:], in0=halves[:, :, 0], in1=halves[:, :, 1], op=ALU.add)
-                nc.vector.reciprocal(out=inv_sum[:], in_=row_sum[:])
-            sums = ps_sums.tile([P, REP, P], F32, name="o_sums", tag="sums")
+            sums = ps_other.tile([P, REP, P], F32, name="o_sums", tag="other")
             for r in range(REP):
                 for c in range(passes):
                     cols = slice((r * passes + c) * P, (r * passes + c + 1) * P)
@@ -317,7 +341,6 @@ def tile_step1attention_pa_kernel(tc, q, k, x, Wv, out):
                         stop=(c == passes - 1),
                     )
             tiles["sums"] = sums
-            tiles["inv_sum"] = inv_sum
 
         def divide_and_store(it, g):
             tiles = unit[(it, g)]
@@ -330,31 +353,64 @@ def tile_step1attention_pa_kernel(tc, q, k, x, Wv, out):
             )
             nc.sync.dma_start(out=out_rows[it * P : (it + 1) * P, g * REP * P : (g + 1) * REP * P], in_=o[:].rearrange("p r d -> p (r d)"))
 
-        for part in range(3):
+        for part in (0, 2, 1):
             keep_part(0, part, transpose_part(0, part))
         count = len(packs)
-        for m in range(-1, count + 6):
-            if 0 <= m - 2 < count:
-                words = e_ring[(m - 2) % E_RING][:].rearrange("p c k -> p (c k)").bitcast(F32)
-                packs[m - 2]["bank"] = transpose_planes(words)
+        row_step = list(range(0, 8)) + list(range(9, 17, 2))
+        project_step = [6, 7, 8, 9] + [17, 19, 21, 23]
+        last_project = [max(project_step[4 * key_pass : 4 * key_pass + 4]) for key_pass in range(2)]
+        waiting = []
+        dividing = []
+        m = -1
+        while m < count + 4 or waiting or dividing:
+            e_pack = m - 2
+            if 0 <= e_pack < count:
+                words = packs[e_pack]["e"][:].rearrange("p c k -> p (c k)").bitcast(F32)
+                packs[e_pack]["bank"] = transpose_planes(words, ps_other, "other")
             part = packs[m]["turn"] - 1 if 0 <= m < count and packs[m]["it"] + 1 < Q_TILES else -1
             if 0 <= part < 3:
                 part_bank = transpose_part(packs[m]["it"] + 1, part)
+            new_rows = row_step.index(m) if m in row_step else -1
+            if new_rows >= 0:
+                spread_transposes(new_rows)
             if m + 1 < count:
-                fill(m + 1)
-            if 0 <= m - 4 < count and packs[m - 4]["last"]:
-                weighted_values(packs[m - 4]["it"], packs[m - 4]["g"])
+                scores(m + 1)
+            new_values = project_step.index(m) if m in project_step else -1
+            if new_values >= 0:
+                project_values(new_values // 4, new_values % 4)
+            finished = dividing
+            dividing = []
+            if waiting and waiting[0][0] <= m and m > last_project[0 if waiting[0][1][0] < 4 else 1] + 1:
+                dividing.append(waiting[0][1])
+                waiting = waiting[1:]
+                weighted_values(*dividing[0])
             if m + 1 < count:
-                add_bias(m + 1)
+                for b in range(2):
+                    add_bias_bank(m + 1, b)
             if 0 <= m < count:
                 maxima(m)
             if 0 <= m - 1 < count:
                 exponentials(m - 1)
-            if 0 <= m - 2 < count:
-                packs[m - 2]["grouped"] = regroup(packs[m - 2]["bank"], nc.scalar.copy)
+            if 0 <= e_pack < count:
+                packs[e_pack]["grouped"] = regroup(packs[e_pack]["bank"], nc.scalar.copy)
             if 0 <= part < 3:
                 keep_part(packs[m]["it"] + 1, part, part_bank)
-            if 0 <= m - 5 < count and packs[m - 5]["last"]:
-                divide_and_store(packs[m - 5]["it"], packs[m - 5]["g"])
-            if 0 <= m - 3 < count:
-                quantise_e(m - 3)
+            if new_rows >= 0:
+                spread_copies(new_rows)
+                if new_rows + 4 < len(row_tiles):
+                    load_rows(new_rows + 4)
+            if m - 1 in row_step:
+                quantise_rows(row_step.index(m - 1))
+            if new_values >= 0:
+                group_values(new_values // 4, new_values % 4)
+            if m - 1 in project_step:
+                quantise_values(project_step.index(m - 1) // 4, project_step.index(m - 1) % 4)
+            for it, g in finished:
+                divide_and_store(it, g)
+            for it, g in dividing:
+                invert_sums(it, g)
+            if 0 <= e_pack - 1 < count:
+                quantise_e(e_pack - 1)
+                if packs[e_pack - 1]["last"]:
+                    waiting.append((m + 1, (packs[e_pack - 1]["it"], packs[e_pack - 1]["g"])))
+            m += 1

@@ -26,7 +26,6 @@ SCALE = 1.0 / math.sqrt(P)
 MASKED = 1.0e30
 TINY = 1.0e-30
 E_RING = 4
-E_LATER = 4
 
 FLOPS = 2 * S * HD * GD + 2 * 2 * HEADS * P * (K_PASS * K_PASS + K_PASS * S)
 
@@ -234,6 +233,7 @@ def tile_step1attention_pa_kernel(tc, q, k, x, Wv, out):
                         {"it": it, "g": g, "banks": bank_list, "slot": slot, "last": slot == len(pairs) - 1,
                          "turn": g * len(pairs) + slot, "e": (e_early if keys <= K_PASS else e_late)[len(packs) % E_RING]}
                     )
+        unread = keep.tile([P, K_PASS], BF16, name="unread")
         unit = {}
 
         def scores(m):
@@ -267,25 +267,16 @@ def tile_step1attention_pa_kernel(tc, q, k, x, Wv, out):
             if k0 == 0 and it + 1 < Q_TILES:
                 scale_bias(h, it + 1)
 
-        def maxima(m):
+        def maximum(m, b):
             pack = packs[m]
-            neg_max = stats.tile([P, 2], F32, name="neg_max")
-            for c, (r, k0, width) in enumerate(pack["banks"]):
-                nc.vector.tensor_reduce(
-                    out=neg_max[:, c : c + 1], in_=pack["z"][c][:, :width], axis=AXIS.X, op=ALU.max, negate=True
-                )
-            exp_bias = stats.tile([P, 2], F32, name="exp_bias")
-            if pack["banks"][0][0] != pack["banks"][1][0]:
-                nc.gpsimd.tensor_scalar(
-                    out=exp_bias[:], in0=neg_max[:], scalar1=SCALE, scalar2=0.0, op0=ALU.mult, op1=ALU.add
-                )
-                pack["exp_bias"] = [exp_bias[:, 0:1], exp_bias[:, 1:2]]
-            else:
-                nc.gpsimd.tensor_scalar(
-                    out=exp_bias[:, 0:1], in0=neg_max[:, 0:1], scalar1=neg_max[:, 1:2], scalar2=SCALE,
-                    op0=ALU.min, op1=ALU.mult,
-                )
-                pack["exp_bias"] = [exp_bias[:, 0:1], exp_bias[:, 0:1]]
+            r, k0, width = pack["banks"][b]
+            if b == 0:
+                pack["exp_bias"] = [stats.tile([P, 1], F32, name="exp_bias%d" % c, tag="exp_bias%d" % c) for c in range(2)]
+            nc.vector.tensor_scalar(
+                out=unread[:, :width], in0=pack["z"][b][:, :width], scalar1=-SCALE,
+                scalar2=pack["exp_bias"][0][:] if k0 > 0 else None,
+                op0=ALU.mult, op1=ALU.min, accum_out=pack["exp_bias"][b][:],
+            )
 
         def exponentials(m):
             pack = packs[m]
@@ -298,7 +289,7 @@ def tile_step1attention_pa_kernel(tc, q, k, x, Wv, out):
                     out=pack["e"][:, c, :width],
                     in_=pack["z"][c][:, :width],
                     func=ACT.Exp,
-                    bias=pack["exp_bias"][c],
+                    bias=pack["exp_bias"][c if pack["it"] < 4 else 1][:],
                     scale=SCALE,
                     accum_out=unit[(it, g)]["row_sums"][:, col : col + 1],
                 )
@@ -362,7 +353,7 @@ def tile_step1attention_pa_kernel(tc, q, k, x, Wv, out):
         waiting = []
         dividing = []
         m = -1
-        while m < count + 4 or waiting or dividing:
+        while m < count + 5 or waiting or dividing:
             e_pack = m - 2
             if 0 <= e_pack < count:
                 words = packs[e_pack]["e"][:].rearrange("p c k -> p (c k)").bitcast(F32)
@@ -388,7 +379,14 @@ def tile_step1attention_pa_kernel(tc, q, k, x, Wv, out):
                 for b in range(2):
                     add_bias_bank(m + 1, b)
             if 0 <= m < count:
-                maxima(m)
+                maximum(m, 0)
+            q_pack = e_pack - 1
+            if 0 <= q_pack < count:
+                quantise_e(q_pack)
+                if packs[q_pack]["last"]:
+                    waiting.append((m + 1, (packs[q_pack]["it"], packs[q_pack]["g"])))
+            if 0 <= m < count:
+                maximum(m, 1)
             if 0 <= m - 1 < count:
                 exponentials(m - 1)
             if 0 <= e_pack < count:
@@ -409,8 +407,4 @@ def tile_step1attention_pa_kernel(tc, q, k, x, Wv, out):
                 divide_and_store(it, g)
             for it, g in dividing:
                 invert_sums(it, g)
-            if 0 <= e_pack - 1 < count:
-                quantise_e(e_pack - 1)
-                if packs[e_pack - 1]["last"]:
-                    waiting.append((m + 1, (packs[e_pack - 1]["it"], packs[e_pack - 1]["g"])))
             m += 1

@@ -40,15 +40,15 @@ def tile_step1attention_pa_kernel(tc, q, k, x, Wv, out):
     with ExitStack() as ctx:
         ctx.enter_context(tc.manual_schedule())
         keep = ctx.enter_context(tc.tile_pool(name="keep", bufs=1))
-        loads = ctx.enter_context(tc.tile_pool(name="loads", bufs=4))
+        loads = ctx.enter_context(tc.tile_pool(name="loads", bufs=6))
         q_pool = ctx.enter_context(tc.tile_pool(name="q_pool", bufs=3))
         qT_pool = ctx.enter_context(tc.tile_pool(name="qT_pool", bufs=2))
         grouped_pool = ctx.enter_context(tc.tile_pool(name="grouped_pool", bufs=6))
         stats = ctx.enter_context(tc.tile_pool(name="stats", bufs=6))
         e_codes_pool = ctx.enter_context(tc.tile_pool(name="e_codes_pool", bufs=6))
         o_pool = ctx.enter_context(tc.tile_pool(name="o_pool", bufs=3))
-        ps_scores = ctx.enter_context(tc.psum_pool(name="ps_scores", bufs=6))
-        ps_other = ctx.enter_context(tc.psum_pool(name="ps_other", bufs=2))
+        ps_scores = ctx.enter_context(tc.psum_pool(name="ps_scores", bufs=4))
+        ps_other = ctx.enter_context(tc.psum_pool(name="ps_other", bufs=4))
 
         k_raw = [keep.tile([P, GD], BF16, name="k_raw%d" % t) for t in range(Q_TILES)]
         q_raw = {}
@@ -74,7 +74,7 @@ def tile_step1attention_pa_kernel(tc, q, k, x, Wv, out):
         row_tiles = [w_tile[0]] + x_tile[:4] + w_tile[1:] + x_tile[4:]
 
         def load_rows(n):
-            raw[n] = loads.tile([P, HD], BF16, name="raw")
+            raw[n] = loads.tile([P, HD], BF16, name="raw", tag="raw")
             nc.sync.dma_start(out=raw[n][:], in_=row_tiles[n][0])
 
         load_keys(0)
@@ -92,19 +92,17 @@ def tile_step1attention_pa_kernel(tc, q, k, x, Wv, out):
         make_identity(nc, ident_bf[:])
         ident_f32 = keep.tile([P, P], F32, name="ident_f32")
         make_identity(nc, ident_f32[:])
-        future = keep.tile([P, S], F32, name="future")
-        root = keep.tile([P, S], F32, name="root")
         neg_root = keep.tile([P, S], F32, name="neg_root")
         for cols in (slice(0, P), slice(P, S)):
             nc.vector.tensor_scalar(
-                out=root[:, cols], in0=dist[:, cols], scalar1=0.0, scalar2=TINY, op0=ALU.max, op1=ALU.add
+                out=neg_root[:, cols], in0=dist[:, cols], scalar1=0.0, scalar2=TINY, op0=ALU.max, op1=ALU.add
             )
-            nc.scalar.activation(out=root[:, cols], in_=root[:, cols], func=ACT.Sqrt)
+            nc.scalar.activation(out=neg_root[:, cols], in_=neg_root[:, cols], func=ACT.Sqrt)
             nc.vector.tensor_scalar(
-                out=future[:, cols], in0=dist[:, cols], scalar1=0.0, scalar2=MASKED, op0=ALU.min, op1=ALU.mult
+                out=dist[:, cols], in0=dist[:, cols], scalar1=0.0, scalar2=MASKED, op0=ALU.min, op1=ALU.mult
             )
             nc.vector.scalar_tensor_tensor(
-                out=neg_root[:, cols], in0=root[:, cols], scalar=-1.0, in1=future[:, cols], op0=ALU.mult, op1=ALU.add
+                out=neg_root[:, cols], in0=neg_root[:, cols], scalar=-1.0, in1=dist[:, cols], op0=ALU.mult, op1=ALU.add
             )
 
         bias = keep.tile([P, HEADS, S], F32, name="bias")
@@ -150,7 +148,7 @@ def tile_step1attention_pa_kernel(tc, q, k, x, Wv, out):
         def spread_transposes(n):
             words = raw[n][:].bitcast(F32)
             banks[n] = [
-                transpose_planes(words[:, 4 * half * P : 4 * (half + 1) * P], ps_scores, "z") for half in range(2)
+                transpose_planes(words[:, 4 * half * P : 4 * (half + 1) * P], ps_other, "other") for half in range(2)
             ]
 
         def spread_copies(n):
@@ -165,7 +163,7 @@ def tile_step1attention_pa_kernel(tc, q, k, x, Wv, out):
         v_grouped = {}
 
         def project_values(key_pass, g):
-            sums = ps_scores.tile([P, 4, P], F32, name="v_sums", tag="z")
+            sums = ps_other.tile([P, 4, P], F32, name="v_sums", tag="other")
             for t in range(4):
                 for c in range(HD // K_PASS):
                     cols = slice(c * P, (c + 1) * P)
@@ -212,7 +210,7 @@ def tile_step1attention_pa_kernel(tc, q, k, x, Wv, out):
 
         def keep_part(it, part, bank):
             if part < 2:
-                nc.vector.tensor_copy(out=qT[it][:, 8 * part : 8 * (part + 1), :], in_=bank[:])
+                nc.scalar.copy(out=qT[it][:, 8 * part : 8 * (part + 1), :], in_=bank[:])
             else:
                 cols = slice((it % 4) * P, (it % 4 + 1) * P)
                 nc.scalar.copy(out=kT[it // 4][:, :, cols], in_=bank[:])
@@ -233,7 +231,6 @@ def tile_step1attention_pa_kernel(tc, q, k, x, Wv, out):
                         {"it": it, "g": g, "banks": bank_list, "slot": slot, "last": slot == len(pairs) - 1,
                          "turn": g * len(pairs) + slot, "e": (e_early if keys <= K_PASS else e_late)[len(packs) % E_RING]}
                     )
-        unread = keep.tile([P, K_PASS], BF16, name="unread")
         unit = {}
 
         def scores(m):
@@ -271,9 +268,10 @@ def tile_step1attention_pa_kernel(tc, q, k, x, Wv, out):
             pack = packs[m]
             r, k0, width = pack["banks"][b]
             if b == 0:
+                pack["scaled"] = loads.tile([P, 2, K_PASS], F32, name="scaled", tag="raw")
                 pack["exp_bias"] = [stats.tile([P, 1], F32, name="exp_bias%d" % c, tag="exp_bias%d" % c) for c in range(2)]
             nc.vector.tensor_scalar(
-                out=unread[:, :width], in0=pack["z"][b][:, :width], scalar1=-SCALE,
+                out=pack["scaled"][:, b, :width], in0=pack["z"][b][:, :width], scalar1=-SCALE,
                 scalar2=pack["exp_bias"][0][:] if k0 > 0 else None,
                 op0=ALU.mult, op1=ALU.min, accum_out=pack["exp_bias"][b][:],
             )
@@ -287,10 +285,10 @@ def tile_step1attention_pa_kernel(tc, q, k, x, Wv, out):
                 col = 2 * pack["slot"] + c
                 nc.scalar.activation(
                     out=pack["e"][:, c, :width],
-                    in_=pack["z"][c][:, :width],
+                    in_=pack["scaled"][:, c, :width],
                     func=ACT.Exp,
                     bias=pack["exp_bias"][c if pack["it"] < 4 else 1][:],
-                    scale=SCALE,
+                    scale=-1.0,
                     accum_out=unit[(it, g)]["row_sums"][:, col : col + 1],
                 )
 
@@ -353,8 +351,8 @@ def tile_step1attention_pa_kernel(tc, q, k, x, Wv, out):
         waiting = []
         dividing = []
         m = -1
-        while m < count + 5 or waiting or dividing:
-            e_pack = m - 2
+        while m < count + 6 or waiting or dividing:
+            e_pack = m - 3
             if 0 <= e_pack < count:
                 words = packs[e_pack]["e"][:].rearrange("p c k -> p (c k)").bitcast(F32)
                 packs[e_pack]["bank"] = transpose_planes(words, ps_other, "other")

@@ -40,7 +40,7 @@ def tile_step1attention_pa_kernel(tc, q, k, x, Wv, out):
     with ExitStack() as ctx:
         ctx.enter_context(tc.manual_schedule())
         keep = ctx.enter_context(tc.tile_pool(name="keep", bufs=1))
-        loads = ctx.enter_context(tc.tile_pool(name="loads", bufs=6))
+        wide_pool = ctx.enter_context(tc.tile_pool(name="wide_pool", bufs=6))
         q_pool = ctx.enter_context(tc.tile_pool(name="q_pool", bufs=3))
         qT_pool = ctx.enter_context(tc.tile_pool(name="qT_pool", bufs=2))
         grouped_pool = ctx.enter_context(tc.tile_pool(name="grouped_pool", bufs=6))
@@ -50,6 +50,8 @@ def tile_step1attention_pa_kernel(tc, q, k, x, Wv, out):
         ps_scores = ctx.enter_context(tc.psum_pool(name="ps_scores", bufs=4))
         ps_other = ctx.enter_context(tc.psum_pool(name="ps_other", bufs=4))
 
+        order = list(range(Q_TILES))
+
         k_raw = [keep.tile([P, GD], BF16, name="k_raw%d" % t) for t in range(Q_TILES)]
         q_raw = {}
         raw = {}
@@ -57,9 +59,11 @@ def tile_step1attention_pa_kernel(tc, q, k, x, Wv, out):
         def load_keys(t):
             nc.sync.dma_start(out=k_raw[t][:], in_=k_rows[t * P : (t + 1) * P, :])
 
-        def load_queries(it):
+        def load_queries(it, pieces=1):
             q_raw[it] = q_pool.tile([P, HD], BF16, name="q_raw")
-            nc.sync.dma_start(out=q_raw[it][:], in_=q_rows[it * P : (it + 1) * P, :])
+            for n in range(pieces):
+                cols = slice(n * HD // pieces, (n + 1) * HD // pieces)
+                nc.sync.dma_start(out=q_raw[it][:, cols], in_=q_rows[it * P : (it + 1) * P, cols])
 
         w_codes = keep.tile([P, GROUPS, 4 * P], U32, name="w_codes", align_bytes=64)
         w_scales = keep.tile([P, GROUPS, 4 * P], U8, name="w_scales", align_bytes=64)
@@ -74,17 +78,18 @@ def tile_step1attention_pa_kernel(tc, q, k, x, Wv, out):
         row_tiles = [w_tile[0]] + x_tile[:4] + w_tile[1:] + x_tile[4:]
 
         def load_rows(n):
-            raw[n] = loads.tile([P, HD], BF16, name="raw", tag="raw")
+            raw[n] = wide_pool.tile([P, HD], BF16, name="raw", tag="wide")
             nc.sync.dma_start(out=raw[n][:], in_=row_tiles[n][0])
 
-        load_keys(0)
-        load_queries(0)
+        for t in range(order[0] + 1):
+            load_keys(t)
+        load_queries(order[0], pieces=2)
         for n in range(4):
             load_rows(n)
-        load_keys(1)
-        load_queries(1)
+        load_keys(order[1])
+        load_queries(order[1])
 
-        dist = keep.tile([P, S], F32, name="dist")
+        dist = wide_pool.tile([P, S], F32, name="dist", tag="wide")
         nc.gpsimd.iota(
             dist[:], pattern=[[1, S]], base=0, channel_multiplier=-1, allow_small_or_imprecise_dtypes=True
         )
@@ -93,11 +98,10 @@ def tile_step1attention_pa_kernel(tc, q, k, x, Wv, out):
         ident_f32 = keep.tile([P, P], F32, name="ident_f32")
         make_identity(nc, ident_f32[:])
         neg_root = keep.tile([P, S], F32, name="neg_root")
-        for cols in (slice(0, P), slice(P, S)):
-            nc.vector.tensor_scalar(
-                out=neg_root[:, cols], in0=dist[:, cols], scalar1=0.0, scalar2=TINY, op0=ALU.max, op1=ALU.add
-            )
-            nc.scalar.activation(out=neg_root[:, cols], in_=neg_root[:, cols], func=ACT.Sqrt)
+        nc.vector.tensor_scalar(out=neg_root[:], in0=dist[:], scalar1=0.0, scalar2=TINY, op0=ALU.max, op1=ALU.add)
+        nc.scalar.activation(out=neg_root[:], in_=neg_root[:], func=ACT.Sqrt)
+
+        def mask_root(cols):
             nc.vector.tensor_scalar(
                 out=dist[:, cols], in0=dist[:, cols], scalar1=0.0, scalar2=MASKED, op0=ALU.min, op1=ALU.mult
             )
@@ -105,10 +109,16 @@ def tile_step1attention_pa_kernel(tc, q, k, x, Wv, out):
                 out=neg_root[:, cols], in0=neg_root[:, cols], scalar=-1.0, in1=dist[:, cols], op0=ALU.mult, op1=ALU.add
             )
 
+        first = P * (order[0] + 1)
+        mask_root(slice(0, first))
+
+        e_ring = [keep.tile([P, 2, K_PASS], BF16, name="e_ring%d" % n) for n in range(E_RING)]
+        for e_tile in e_ring:
+            nc.gpsimd.memset(e_tile[:].bitcast(F32)[:, :, P // 2 :], 0.0)
+
         bias = keep.tile([P, HEADS, S], F32, name="bias")
 
-        def scale_bias(h, it):
-            cols = slice(it * P, (it + 1) * P)
+        def scale_bias(h, cols):
             slope = 2.0 ** (-(h + 1) / 2.0)
             nc.gpsimd.tensor_scalar(
                 out=bias[:, h, cols], in0=neg_root[:, cols], scalar1=slope / SCALE, scalar2=0.0,
@@ -116,17 +126,10 @@ def tile_step1attention_pa_kernel(tc, q, k, x, Wv, out):
             )
 
         for h in range(HEADS):
-            scale_bias(h, 0)
+            scale_bias(h, slice(0, first))
 
-        e_early = [keep.tile([P, 2, K_PASS], BF16, name="e_early%d" % n) for n in range(E_RING)]
-        e_late = [keep.tile([P, 2, K_PASS], BF16, name="e_late%d" % n) for n in range(E_RING)]
-        for e_tile in e_early:
-            nc.vector.memset(e_tile[:].bitcast(F32)[:, :, P // 2 :], 0.0)
-        for e_tile in e_late:
-            nc.vector.memset(e_tile[:].bitcast(F32)[:, 1, P // 2 :], 0.0)
-
-        def transpose_planes(words, pool, tag):
-            bank = pool.tile([P, 4, P], F32, name="bank", tag=tag)
+        def transpose_planes(words):
+            bank = ps_other.tile([P, 4, P], F32, name="bank", tag="other")
             for a in range(4):
                 nc.tensor.transpose(out=bank[:, a, :], in_=words[:, a * P : (a + 1) * P], identity=ident_f32[:])
             return bank
@@ -142,20 +145,18 @@ def tile_step1attention_pa_kernel(tc, q, k, x, Wv, out):
         def quantise(grouped, codes, scales):
             nc.vector.quantize_mx(out=codes.bitcast(FP8X4), scales=scales, in_=grouped[:])
 
-        banks = {}
-        halves = {}
+        row_banks = {}
+        row_grouped = {}
 
         def spread_transposes(n):
             words = raw[n][:].bitcast(F32)
-            banks[n] = [
-                transpose_planes(words[:, 4 * half * P : 4 * (half + 1) * P], ps_other, "other") for half in range(2)
-            ]
+            row_banks[n] = [transpose_planes(words[:, 4 * half * P : 4 * (half + 1) * P]) for half in range(2)]
 
         def spread_copies(n):
-            halves[n] = [regroup(banks[n][0], nc.vector.tensor_copy), regroup(banks[n][1], nc.scalar.copy)]
+            row_grouped[n] = [regroup(row_banks[n][0], nc.vector.tensor_copy if n % 2 == 0 else nc.scalar.copy), regroup(row_banks[n][1], nc.scalar.copy)]
 
         def quantise_rows(n):
-            for half, grouped in enumerate(halves[n]):
+            for half, grouped in enumerate(row_grouped[n]):
                 cols = slice(2 * half * P, 2 * (half + 1) * P)
                 quantise(grouped, row_tiles[n][1][:, cols], row_tiles[n][2][:, cols])
 
@@ -194,32 +195,30 @@ def tile_step1attention_pa_kernel(tc, q, k, x, Wv, out):
         kT = [keep.tile([P, GROUPS, K_PASS], BF16, name="kT%d" % c) for c in range(S // K_PASS)]
         qT = {}
 
-        def transpose_part(it, part):
+        def transpose_queries(it, part):
             if part == 0:
                 qT[it] = qT_pool.tile([P, HEADS, P], BF16, name="qT")
-            if part < 2:
-                bank = ps_other.tile([P, 8, P], BF16, name="bank_q", tag="other")
-                for j in range(8):
-                    h = 8 * part + j
-                    nc.tensor.transpose(out=bank[:, j, :], in_=q_raw[it][:, h * P : (h + 1) * P], identity=ident_bf[:])
-            else:
-                bank = ps_other.tile([P, GROUPS, P], BF16, name="bank_k", tag="other")
-                for g in range(GROUPS):
-                    nc.tensor.transpose(out=bank[:, g, :], in_=k_raw[it][:, g * P : (g + 1) * P], identity=ident_bf[:])
+            bank = ps_other.tile([P, 8, P], BF16, name="bank_q", tag="other")
+            for j in range(8):
+                h = 8 * part + j
+                nc.tensor.transpose(out=bank[:, j, :], in_=q_raw[it][:, h * P : (h + 1) * P], identity=ident_bf[:])
             return bank
 
-        def keep_part(it, part, bank):
-            if part < 2:
-                nc.scalar.copy(out=qT[it][:, 8 * part : 8 * (part + 1), :], in_=bank[:])
-            else:
-                cols = slice((it % 4) * P, (it % 4 + 1) * P)
-                nc.scalar.copy(out=kT[it // 4][:, :, cols], in_=bank[:])
-                if it + 2 < Q_TILES:
-                    load_keys(it + 2)
-                    load_queries(it + 2)
+        def transpose_keys(t):
+            bank = ps_other.tile([P, GROUPS, P], BF16, name="bank_k", tag="other")
+            for g in range(GROUPS):
+                nc.tensor.transpose(out=bank[:, g, :], in_=k_raw[t][:, g * P : (g + 1) * P], identity=ident_bf[:])
+            return bank
+
+        def keep_queries(it, part, bank, copy):
+            copy(out=qT[it][:, 8 * part : 8 * (part + 1), :], in_=bank[:])
+
+        def keep_keys(t, bank, copy):
+            cols = slice((t % 4) * P, (t % 4 + 1) * P)
+            copy(out=kT[t // 4][:, :, cols], in_=bank[:])
 
         packs = []
-        for it in range(Q_TILES):
+        for place, it in enumerate(order):
             keys = P * (it + 1)
             for g in range(GROUPS):
                 if keys <= K_PASS:
@@ -229,8 +228,10 @@ def tile_step1attention_pa_kernel(tc, q, k, x, Wv, out):
                 for slot, bank_list in enumerate(pairs):
                     packs.append(
                         {"it": it, "g": g, "banks": bank_list, "slot": slot, "last": slot == len(pairs) - 1,
-                         "turn": g * len(pairs) + slot, "e": (e_early if keys <= K_PASS else e_late)[len(packs) % E_RING]}
+                         "place": place, "turn": g * len(pairs) + slot, "e": e_ring[len(packs) % E_RING]}
                     )
+        first_late = [pack["it"] >= 4 for pack in packs].index(True)
+
         unit = {}
 
         def scores(m):
@@ -245,30 +246,29 @@ def tile_step1attention_pa_kernel(tc, q, k, x, Wv, out):
                 )
                 pack["z"].append(z)
 
-        def add_bias_bank(m, b):
+        def add_bias(m):
             pack = packs[m]
             it, g = pack["it"], pack["g"]
-            r, k0, width = pack["banks"][b]
-            h = REP * g + r
-            z = pack["z"][b]
-            for j in range(width // P):
-                delta = it - (k0 // P + j)
-                nc.tensor.matmul(
-                    out=z[:, j * P : (j + 1) * P],
-                    lhsT=bias[:, h, delta * P : (delta + 1) * P],
-                    rhs=ident_f32[:],
-                    is_transpose=True,
-                    start=False,
-                    stop=(j == width // P - 1),
-                )
-            if k0 == 0 and it + 1 < Q_TILES:
-                scale_bias(h, it + 1)
+            for z, (r, k0, width) in zip(pack["z"], pack["banks"]):
+                h = REP * g + r
+                for j in range(width // P):
+                    delta = it - (k0 // P + j)
+                    nc.tensor.matmul(
+                        out=z[:, j * P : (j + 1) * P],
+                        lhsT=bias[:, h, delta * P : (delta + 1) * P],
+                        rhs=ident_f32[:],
+                        is_transpose=True,
+                        start=False,
+                        stop=(j == width // P - 1),
+                    )
+                if k0 == 0 and it % 2 == 0 and it + 1 < Q_TILES:
+                    scale_bias(h, slice(P * (it + 1), min(P * (it + 3), S)))
 
         def maximum(m, b):
             pack = packs[m]
             r, k0, width = pack["banks"][b]
             if b == 0:
-                pack["scaled"] = loads.tile([P, 2, K_PASS], F32, name="scaled", tag="raw")
+                pack["scaled"] = wide_pool.tile([P, 2, K_PASS], F32, name="scaled", tag="wide")
                 pack["exp_bias"] = [stats.tile([P, 1], F32, name="exp_bias%d" % c, tag="exp_bias%d" % c) for c in range(2)]
             nc.vector.tensor_scalar(
                 out=pack["scaled"][:, b, :width], in0=pack["z"][b][:, :width], scalar1=-SCALE,
@@ -279,6 +279,8 @@ def tile_step1attention_pa_kernel(tc, q, k, x, Wv, out):
         def exponentials(m):
             pack = packs[m]
             it, g = pack["it"], pack["g"]
+            if first_late <= m < first_late + E_RING:
+                nc.gpsimd.memset(pack["e"][:].bitcast(F32)[:, 1, P // 2 :], 0.0)
             if pack["slot"] == 0:
                 unit[(it, g)] = {"row_sums": stats.tile([P, 2 * REP], F32, name="row_sums")}
             for c, (r, k0, width) in enumerate(pack["banks"]):
@@ -287,7 +289,7 @@ def tile_step1attention_pa_kernel(tc, q, k, x, Wv, out):
                     out=pack["e"][:, c, :width],
                     in_=pack["scaled"][:, c, :width],
                     func=ACT.Exp,
-                    bias=pack["exp_bias"][c if pack["it"] < 4 else 1][:],
+                    bias=pack["exp_bias"][c if it < 4 else 1][:],
                     scale=-1.0,
                     accum_out=unit[(it, g)]["row_sums"][:, col : col + 1],
                 )
@@ -342,43 +344,46 @@ def tile_step1attention_pa_kernel(tc, q, k, x, Wv, out):
             )
             nc.sync.dma_start(out=out_rows[it * P : (it + 1) * P, g * REP * P : (g + 1) * REP * P], in_=o[:].rearrange("p r d -> p (r d)"))
 
-        for part in (0, 2, 1):
-            keep_part(0, part, transpose_part(0, part))
+        for t in range(order[0] + 1):
+            keep_keys(t, transpose_keys(t), nc.vector.tensor_copy)
+        for part in range(2):
+            keep_queries(order[0], part, transpose_queries(order[0], part), nc.vector.tensor_copy)
         count = len(packs)
-        row_step = list(range(0, 8)) + list(range(9, 17, 2))
-        project_step = [6, 7, 8, 9] + [17, 19, 21, 23]
-        last_project = [max(project_step[4 * key_pass : 4 * key_pass + 4]) for key_pass in range(2)]
+        rows_of_step = {n: [n] for n in range(12)}
+        values_of_step = {6: [(0, 0)], 7: [(0, 1)], 8: [(0, 2)], 9: [(0, 3)], 17: [(1, 0)], 19: [(1, 1)], 21: [(1, 2)], 23: [(1, 3)]}
+        last_values = [max(step for step in values_of_step if any(kp == key_pass for kp, g in values_of_step[step])) for key_pass in range(2)]
         waiting = []
         dividing = []
+        mask_root(slice(first, S))
         m = -1
-        while m < count + 6 or waiting or dividing:
+        while m < count + 5 or waiting or dividing:
             e_pack = m - 3
+            q_pack = m - 4
             if 0 <= e_pack < count:
-                words = packs[e_pack]["e"][:].rearrange("p c k -> p (c k)").bitcast(F32)
-                packs[e_pack]["bank"] = transpose_planes(words, ps_other, "other")
-            part = packs[m]["turn"] - 1 if 0 <= m < count and packs[m]["it"] + 1 < Q_TILES else -1
+                packs[e_pack]["bank"] = transpose_planes(packs[e_pack]["e"][:].rearrange("p c k -> p (c k)").bitcast(F32))
+            part = packs[m]["turn"] - 3 if 0 <= m < count and packs[m]["place"] + 1 < len(order) else -1
             if 0 <= part < 3:
-                part_bank = transpose_part(packs[m]["it"] + 1, part)
-            new_rows = row_step.index(m) if m in row_step else -1
-            if new_rows >= 0:
-                spread_transposes(new_rows)
+                after = order[packs[m]["place"] + 1]
+                if part < 2:
+                    part_bank = transpose_queries(after, part)
+                elif after > 0:
+                    part_bank = transpose_keys(after)
+            for n in rows_of_step.get(m, []):
+                spread_transposes(n)
             if m + 1 < count:
                 scores(m + 1)
-            new_values = project_step.index(m) if m in project_step else -1
-            if new_values >= 0:
-                project_values(new_values // 4, new_values % 4)
+            for key_pass, g in values_of_step.get(m, []):
+                project_values(key_pass, g)
             finished = dividing
             dividing = []
-            if waiting and waiting[0][0] <= m and m > last_project[0 if waiting[0][1][0] < 4 else 1] + 1:
+            if waiting and waiting[0][0] <= m and m > last_values[0 if waiting[0][1][0] < 4 else 1] + 1:
                 dividing.append(waiting[0][1])
                 waiting = waiting[1:]
                 weighted_values(*dividing[0])
             if m + 1 < count:
-                for b in range(2):
-                    add_bias_bank(m + 1, b)
+                add_bias(m + 1)
             if 0 <= m < count:
                 maximum(m, 0)
-            q_pack = e_pack - 1
             if 0 <= q_pack < count:
                 quantise_e(q_pack)
                 if packs[q_pack]["last"]:
@@ -389,18 +394,25 @@ def tile_step1attention_pa_kernel(tc, q, k, x, Wv, out):
                 exponentials(m - 1)
             if 0 <= e_pack < count:
                 packs[e_pack]["grouped"] = regroup(packs[e_pack]["bank"], nc.scalar.copy)
-            if 0 <= part < 3:
-                keep_part(packs[m]["it"] + 1, part, part_bank)
-            if new_rows >= 0:
-                spread_copies(new_rows)
-                if new_rows + 4 < len(row_tiles):
-                    load_rows(new_rows + 4)
-            if m - 1 in row_step:
-                quantise_rows(row_step.index(m - 1))
-            if new_values >= 0:
-                group_values(new_values // 4, new_values % 4)
-            if m - 1 in project_step:
-                quantise_values(project_step.index(m - 1) // 4, project_step.index(m - 1) % 4)
+            if 0 <= part < 2:
+                keep_queries(after, part, part_bank, nc.scalar.copy)
+            if part == 2:
+                if after > 0:
+                    keep_keys(after, part_bank, nc.scalar.copy)
+                if packs[m]["place"] + 2 < len(order):
+                    if order[packs[m]["place"] + 2] > 0:
+                        load_keys(order[packs[m]["place"] + 2])
+                    load_queries(order[packs[m]["place"] + 2])
+            for n in rows_of_step.get(m - 1, []):
+                quantise_rows(n)
+            for n in rows_of_step.get(m, []):
+                spread_copies(n)
+                if n + 4 < len(row_tiles):
+                    load_rows(n + 4)
+            for key_pass, g in values_of_step.get(m - 1, []):
+                quantise_values(key_pass, g)
+            for key_pass, g in values_of_step.get(m, []):
+                group_values(key_pass, g)
             for it, g in finished:
                 divide_and_store(it, g)
             for it, g in dividing:

@@ -41,9 +41,9 @@ def tile_step1attention_pa_kernel(tc, q, k, x, Wv, out):
         ctx.enter_context(tc.manual_schedule())
         keep = ctx.enter_context(tc.tile_pool(name="keep", bufs=1))
         wide_pool = ctx.enter_context(tc.tile_pool(name="wide_pool", bufs=6))
-        q_pool = ctx.enter_context(tc.tile_pool(name="q_pool", bufs=3))
+        q_pool = ctx.enter_context(tc.tile_pool(name="q_pool", bufs=2))
         qT_pool = ctx.enter_context(tc.tile_pool(name="qT_pool", bufs=2))
-        grouped_pool = ctx.enter_context(tc.tile_pool(name="grouped_pool", bufs=6))
+        grouped_pool = ctx.enter_context(tc.tile_pool(name="grouped_pool", bufs=4))
         stats = ctx.enter_context(tc.tile_pool(name="stats", bufs=6))
         e_codes_pool = ctx.enter_context(tc.tile_pool(name="e_codes_pool", bufs=6))
         o_pool = ctx.enter_context(tc.tile_pool(name="o_pool", bufs=3))
@@ -134,16 +134,23 @@ def tile_step1attention_pa_kernel(tc, q, k, x, Wv, out):
                 nc.tensor.transpose(out=bank[:, a, :], in_=words[:, a * P : (a + 1) * P], identity=ident_f32[:])
             return bank
 
-        def regroup(bank, copy):
-            grouped = grouped_pool.tile([P, 2 * K_PASS], BF16, name="grouped", align_bytes=64)
+        def regroup(bank, grouped, copy):
             copy(
-                out=grouped[:].bitcast(F32).rearrange("p (c w u) -> p c w u", c=2, u=2),
+                out=grouped.bitcast(F32).rearrange("p (c w u) -> p c w u", c=2, u=2),
                 in_=bank[:].rearrange("p (c u) w -> p c w u", u=2),
             )
-            return grouped
 
         def quantise(grouped, codes, scales):
-            nc.vector.quantize_mx(out=codes.bitcast(FP8X4), scales=scales, in_=grouped[:])
+            nc.vector.quantize_mx(
+                out=codes.bitcast(FP8X4), scales=scales, in_=grouped[:].rearrange("p n k -> p (n k)")
+            )
+
+        def grouped_tile(banks):
+            if banks == 1:
+                return grouped_pool.tile(
+                    [P, 1, 2 * K_PASS], BF16, name="grouped1", tag="grouped1", align_bytes=64, bufs=5
+                )
+            return grouped_pool.tile([P, 2, 2 * K_PASS], BF16, name="grouped", tag="grouped", align_bytes=64)
 
         row_banks = {}
         row_grouped = {}
@@ -153,12 +160,12 @@ def tile_step1attention_pa_kernel(tc, q, k, x, Wv, out):
             row_banks[n] = [transpose_planes(words[:, 4 * half * P : 4 * (half + 1) * P]) for half in range(2)]
 
         def spread_copies(n):
-            row_grouped[n] = [regroup(row_banks[n][0], nc.vector.tensor_copy if n % 2 == 0 else nc.scalar.copy), regroup(row_banks[n][1], nc.scalar.copy)]
+            row_grouped[n] = grouped_tile(2)
+            regroup(row_banks[n][0], row_grouped[n][:, 0, :], nc.vector.tensor_copy if n % 2 == 0 else nc.scalar.copy)
+            regroup(row_banks[n][1], row_grouped[n][:, 1, :], nc.scalar.copy)
 
         def quantise_rows(n):
-            for half, grouped in enumerate(row_grouped[n]):
-                cols = slice(2 * half * P, 2 * (half + 1) * P)
-                quantise(grouped, row_tiles[n][1][:, cols], row_tiles[n][2][:, cols])
+            quantise(row_grouped[n], row_tiles[n][1], row_tiles[n][2])
 
         v_sums = {}
         v_grouped = {}
@@ -228,7 +235,7 @@ def tile_step1attention_pa_kernel(tc, q, k, x, Wv, out):
                 for slot, bank_list in enumerate(pairs):
                     packs.append(
                         {"it": it, "g": g, "banks": bank_list, "slot": slot, "last": slot == len(pairs) - 1,
-                         "place": place, "turn": g * len(pairs) + slot, "e": e_ring[len(packs) % E_RING]}
+                         "joined": 2 if keys <= K_PASS else 1, "place": place, "turn": g * len(pairs) + slot, "e": e_ring[len(packs) % E_RING]}
                     )
         first_late = [pack["it"] >= 4 for pack in packs].index(True)
 
@@ -261,6 +268,11 @@ def tile_step1attention_pa_kernel(tc, q, k, x, Wv, out):
                         start=False,
                         stop=(j == width // P - 1),
                     )
+
+        def scale_next(m):
+            it = packs[m]["it"]
+            for r, k0, width in packs[m]["banks"]:
+                h = REP * packs[m]["g"] + r
                 if k0 == 0 and it % 2 == 0 and it + 1 < Q_TILES:
                     scale_bias(h, slice(P * (it + 1), min(P * (it + 3), S)))
 
@@ -282,44 +294,49 @@ def tile_step1attention_pa_kernel(tc, q, k, x, Wv, out):
             if first_late <= m < first_late + E_RING:
                 nc.gpsimd.memset(pack["e"][:].bitcast(F32)[:, 1, P // 2 :], 0.0)
             if pack["slot"] == 0:
-                unit[(it, g)] = {"row_sums": stats.tile([P, 2 * REP], F32, name="row_sums")}
-            for c, (r, k0, width) in enumerate(pack["banks"]):
-                col = 2 * pack["slot"] + c
+                unit[(it, g)] = {"row_sums": stats.tile([P, REP], F32, name="row_sums")}
+            e = pack["e"][:].rearrange("p c k -> p (c k)")
+            scaled = pack["scaled"][:].rearrange("p c k -> p (c k)")
+            if it < 4:
+                pieces = [(r, slice(c * K_PASS, c * K_PASS + width)) for c, (r, k0, width) in enumerate(pack["banks"])]
+            else:
+                pieces = [(pack["slot"], slice(0, P * (it + 1)))]
+            for r, cols in pieces:
                 nc.scalar.activation(
-                    out=pack["e"][:, c, :width],
-                    in_=pack["scaled"][:, c, :width],
+                    out=e[:, cols],
+                    in_=scaled[:, cols],
                     func=ACT.Exp,
-                    bias=pack["exp_bias"][c if it < 4 else 1][:],
+                    bias=pack["exp_bias"][r % 2 if it < 4 else 1][:],
                     scale=-1.0,
-                    accum_out=unit[(it, g)]["row_sums"][:, col : col + 1],
+                    accum_out=unit[(it, g)]["row_sums"][:, r : r + 1],
                 )
+
+        def regroup_e(m):
+            pack = packs[m]
+            n = pack["slot"] % pack["joined"]
+            pack["grouped"] = grouped_tile(pack["joined"]) if n == 0 else packs[m - 1]["grouped"]
+            regroup(pack["bank"], pack["grouped"][:, n, :], nc.vector.tensor_copy if m in (count - 3, count - 2) else nc.scalar.copy)
 
         def quantise_e(m):
             pack = packs[m]
             tiles = unit[(pack["it"], pack["g"])]
-            if pack["slot"] == 0:
+            if "e_codes" not in tiles:
                 tiles["e_codes"] = e_codes_pool.tile([P, 2 * REP * P], U32, name="e_codes", align_bytes=64)
                 tiles["e_scales"] = e_codes_pool.tile([P, 2 * REP * P], U8, name="e_scales", align_bytes=64)
-            cols = slice(2 * pack["slot"] * P, 2 * (pack["slot"] + 1) * P)
+            cols = slice(2 * (pack["slot"] + 1 - pack["joined"]) * P, 2 * (pack["slot"] + 1) * P)
             quantise(pack["grouped"], tiles["e_codes"][:, cols], tiles["e_scales"][:, cols])
 
-        def invert_sums(it, g):
+        def invert_sums(it, g, r0, r1):
             tiles = unit[(it, g)]
             inv_sum = stats.tile([P, REP], F32, name="inv_sum")
-            if it < 4:
-                nc.vector.reciprocal(out=inv_sum[:], in_=tiles["row_sums"][:, :REP])
-            else:
-                sums_of_banks = tiles["row_sums"][:].rearrange("p (r c) -> p r c", c=2)
-                row_sum = stats.tile([P, REP], F32, name="row_sum")
-                nc.gpsimd.tensor_tensor(out=row_sum[:], in0=sums_of_banks[:, :, 0], in1=sums_of_banks[:, :, 1], op=ALU.add)
-                nc.vector.reciprocal(out=inv_sum[:], in_=row_sum[:])
-            tiles["inv_sum"] = inv_sum
+            nc.vector.reciprocal(out=inv_sum[:, r0:r1], in_=tiles["row_sums"][:, r0:r1])
+            tiles["inv_sum", r0] = inv_sum
 
-        def weighted_values(it, g):
+        def weighted_values(it, g, r0, r1):
             tiles = unit[(it, g)]
             passes = (P * (it + 1) + K_PASS - 1) // K_PASS
             sums = ps_other.tile([P, REP, P], F32, name="o_sums", tag="other")
-            for r in range(REP):
+            for r in range(r0, r1):
                 for c in range(passes):
                     cols = slice((r * passes + c) * P, (r * passes + c + 1) * P)
                     nc.tensor.matmul_mx(
@@ -331,34 +348,52 @@ def tile_step1attention_pa_kernel(tc, q, k, x, Wv, out):
                         start=(c == 0),
                         stop=(c == passes - 1),
                     )
-            tiles["sums"] = sums
+            tiles["sums", r0] = sums
 
-        def divide_and_store(it, g):
+        def divide_and_store(it, g, r0, r1):
             tiles = unit[(it, g)]
             o = o_pool.tile([P, REP, P], F32, name="o")
-            nc.vector.tensor_tensor(
-                out=o[:],
-                in0=tiles["sums"][:],
-                in1=tiles["inv_sum"][:].unsqueeze(2).to_broadcast([P, REP, P]),
-                op=ALU.mult,
+            if g % 2 == 1:
+                for r in range(r0, r1):
+                    nc.scalar.activation(
+                        out=o[:, r, :], in_=tiles["sums", r0][:, r, :], func=ACT.Copy, scale=tiles["inv_sum", r0][:, r : r + 1]
+                    )
+            else:
+                nc.vector.tensor_tensor(
+                    out=o[:, r0:r1, :],
+                    in0=tiles["sums", r0][:, r0:r1, :],
+                    in1=tiles["inv_sum", r0][:, r0:r1].unsqueeze(2).to_broadcast([P, r1 - r0, P]),
+                    op=ALU.mult,
+                )
+            cols = slice((REP * g + r0) * P, (REP * g + r1) * P)
+            nc.sync.dma_start(
+                out=out_rows[it * P : (it + 1) * P, cols], in_=o[:, r0:r1, :].rearrange("p r d -> p (r d)")
             )
-            nc.sync.dma_start(out=out_rows[it * P : (it + 1) * P, g * REP * P : (g + 1) * REP * P], in_=o[:].rearrange("p r d -> p (r d)"))
 
         for t in range(order[0] + 1):
             keep_keys(t, transpose_keys(t), nc.vector.tensor_copy)
         for part in range(2):
-            keep_queries(order[0], part, transpose_queries(order[0], part), nc.vector.tensor_copy)
+            keep_queries(order[0], part, transpose_queries(order[0], part), nc.scalar.copy if part == 0 else nc.vector.tensor_copy)
         count = len(packs)
         rows_of_step = {n: [n] for n in range(12)}
         values_of_step = {6: [(0, 0)], 7: [(0, 1)], 8: [(0, 2)], 9: [(0, 3)], 17: [(1, 0)], 19: [(1, 1)], 21: [(1, 2)], 23: [(1, 3)]}
         last_values = [max(step for step in values_of_step if any(kp == key_pass for kp, g in values_of_step[step])) for key_pass in range(2)]
         waiting = []
         dividing = []
-        mask_root(slice(first, S))
+        quantised = 0
+
+        def finish_pack(m, step):
+            pack = packs[m]
+            if pack["slot"] % pack["joined"] == pack["joined"] - 1:
+                quantise_e(m)
+            if pack["last"] and m < count - 1:
+                waiting.append((step + 1, pack["it"], pack["g"], 0, REP))
+            if m >= count - REP and m % 2 == 1:
+                waiting.append((step + 1, pack["it"], pack["g"], pack["slot"] - 1, pack["slot"] + 1))
+
         m = -1
-        while m < count + 5 or waiting or dividing:
+        while m < count + 6 or waiting or dividing:
             e_pack = m - 3
-            q_pack = m - 4
             if 0 <= e_pack < count:
                 packs[e_pack]["bank"] = transpose_planes(packs[e_pack]["e"][:].rearrange("p c k -> p (c k)").bitcast(F32))
             part = packs[m]["turn"] - 3 if 0 <= m < count and packs[m]["place"] + 1 < len(order) else -1
@@ -376,24 +411,30 @@ def tile_step1attention_pa_kernel(tc, q, k, x, Wv, out):
                 project_values(key_pass, g)
             finished = dividing
             dividing = []
-            if waiting and waiting[0][0] <= m and m > last_values[0 if waiting[0][1][0] < 4 else 1] + 1:
-                dividing.append(waiting[0][1])
-                waiting = waiting[1:]
+            if waiting and waiting[0][0] <= m and m > last_values[0 if waiting[0][1] < 4 else 1] + 1:
+                dividing.append(waiting[0][1:])
+                waiting.remove(waiting[0])
                 weighted_values(*dividing[0])
             if m + 1 < count:
                 add_bias(m + 1)
             if 0 <= m < count:
                 maximum(m, 0)
-            if 0 <= q_pack < count:
-                quantise_e(q_pack)
-                if packs[q_pack]["last"]:
-                    waiting.append((m + 1, (packs[q_pack]["it"], packs[q_pack]["g"])))
+            while quantised < count and quantised <= m - 5:
+                finish_pack(quantised, m)
+                quantised += 1
             if 0 <= m < count:
                 maximum(m, 1)
+            if m == 0:
+                mask_root(slice(first, S))
+            if 0 <= m < count:
+                scale_next(m)
             if 0 <= m - 1 < count:
                 exponentials(m - 1)
             if 0 <= e_pack < count:
-                packs[e_pack]["grouped"] = regroup(packs[e_pack]["bank"], nc.scalar.copy)
+                regroup_e(e_pack)
+            while m >= count and quantised <= min(e_pack, count - 1):
+                finish_pack(quantised, m)
+                quantised += 1
             if 0 <= part < 2:
                 keep_queries(after, part, part_bank, nc.scalar.copy)
             if part == 2:
@@ -413,8 +454,8 @@ def tile_step1attention_pa_kernel(tc, q, k, x, Wv, out):
                 quantise_values(key_pass, g)
             for key_pass, g in values_of_step.get(m, []):
                 group_values(key_pass, g)
-            for it, g in finished:
-                divide_and_store(it, g)
-            for it, g in dividing:
-                invert_sums(it, g)
+            for part_of_unit in finished:
+                divide_and_store(*part_of_unit)
+            for part_of_unit in dividing:
+                invert_sums(*part_of_unit)
             m += 1

@@ -26,6 +26,7 @@ SCALE = 1.0 / math.sqrt(P)
 MASKED = 1.0e30
 TINY = 1.0e-30
 E_RING = 4
+SUB = P // REP
 
 FLOPS = 2 * S * HD * GD + 2 * 2 * HEADS * P * (K_PASS * K_PASS + K_PASS * S)
 
@@ -89,6 +90,11 @@ def tile_step1attention_pa_kernel(tc, q, k, x, Wv, out):
         load_keys(order[1])
         load_queries(order[1])
 
+        e_early = [keep.tile([P, 2, K_PASS], BF16, name="e_early%d" % n) for n in range(E_RING)]
+        e_late = [keep.tile([P, 2, K_PASS], BF16, name="e_late%d" % n) for n in range(E_RING)]
+        for e_tile in e_early:
+            nc.vector.memset(e_tile[:].bitcast(F32), 0.0)
+
         dist = wide_pool.tile([P, S], F32, name="dist", tag="wide")
         nc.gpsimd.iota(
             dist[:], pattern=[[1, S]], base=0, channel_multiplier=-1, allow_small_or_imprecise_dtypes=True
@@ -112,21 +118,21 @@ def tile_step1attention_pa_kernel(tc, q, k, x, Wv, out):
         first = P * (order[0] + 1)
         mask_root(slice(0, first))
 
-        e_ring = [keep.tile([P, 2, K_PASS], BF16, name="e_ring%d" % n) for n in range(E_RING)]
-        for e_tile in e_ring:
-            nc.gpsimd.memset(e_tile[:].bitcast(F32)[:, :, P // 2 :], 0.0)
+        bias = keep.tile([P, GROUPS, S // SUB, REP, SUB], F32, name="bias")
 
-        bias = keep.tile([P, HEADS, S], F32, name="bias")
-
-        def scale_bias(h, cols):
+        def scale_bias(h, cols, engine):
             slope = 2.0 ** (-(h + 1) / 2.0)
-            nc.gpsimd.tensor_scalar(
-                out=bias[:, h, cols], in0=neg_root[:, cols], scalar1=slope / SCALE, scalar2=0.0,
+            engine.tensor_scalar(
+                out=bias[:, h // REP, cols.start // SUB : cols.stop // SUB, h % REP, :],
+                in0=neg_root[:, cols].rearrange("p (n w) -> p n w", w=SUB), scalar1=slope / SCALE, scalar2=0.0,
                 op0=ALU.mult, op1=ALU.add,
             )
 
         for h in range(HEADS):
-            scale_bias(h, slice(0, first))
+            if h >= REP:
+                scale_bias(h, slice(0, first), nc.gpsimd)
+        for e_tile in e_late:
+            nc.gpsimd.memset(e_tile[:, 1, :].bitcast(F32), 0.0)
 
         def transpose_planes(words):
             bank = ps_other.tile([P, 4, P], F32, name="bank", tag="other")
@@ -146,10 +152,6 @@ def tile_step1attention_pa_kernel(tc, q, k, x, Wv, out):
             )
 
         def grouped_tile(banks):
-            if banks == 1:
-                return grouped_pool.tile(
-                    [P, 1, 2 * K_PASS], BF16, name="grouped1", tag="grouped1", align_bytes=64, bufs=5
-                )
             return grouped_pool.tile([P, 2, 2 * K_PASS], BF16, name="grouped", tag="grouped", align_bytes=64)
 
         row_banks = {}
@@ -187,7 +189,7 @@ def tile_step1attention_pa_kernel(tc, q, k, x, Wv, out):
             v_sums[(key_pass, g)] = sums
 
         def group_values(key_pass, g):
-            grouped = grouped_pool.tile([P, P, 4], BF16, name="grouped_v", tag="grouped", align_bytes=64)
+            grouped = grouped_pool.tile([P, P, 4], BF16, name="grouped_v", tag="grouped_v", bufs=3, align_bytes=64)
             nc.scalar.copy(out=grouped[:], in_=v_sums[(key_pass, g)][:].rearrange("p t n -> p n t"))
             v_grouped[(key_pass, g)] = grouped
 
@@ -205,10 +207,12 @@ def tile_step1attention_pa_kernel(tc, q, k, x, Wv, out):
         def transpose_queries(it, part):
             if part == 0:
                 qT[it] = qT_pool.tile([P, HEADS, P], BF16, name="qT")
-            bank = ps_other.tile([P, 8, P], BF16, name="bank_q", tag="other")
+            bank = ps_other.tile([P, 2, REP, REP, SUB], BF16, name="bank_q", tag="other")
             for j in range(8):
                 h = 8 * part + j
-                nc.tensor.transpose(out=bank[:, j, :], in_=q_raw[it][:, h * P : (h + 1) * P], identity=ident_bf[:])
+                nc.tensor.transpose(
+                    out=bank[:, j // REP, :, j % REP, :], in_=q_raw[it][:, h * P : (h + 1) * P], identity=ident_bf[:]
+                )
             return bank
 
         def transpose_keys(t):
@@ -218,7 +222,10 @@ def tile_step1attention_pa_kernel(tc, q, k, x, Wv, out):
             return bank
 
         def keep_queries(it, part, bank, copy):
-            copy(out=qT[it][:, 8 * part : 8 * (part + 1), :], in_=bank[:])
+            copy(
+                out=qT[it][:, 8 * part : 8 * (part + 1), :].rearrange("p t n -> p (t n)"),
+                in_=bank[:].rearrange("p g j r w -> p (g j r w)"),
+            )
 
         def keep_keys(t, bank, copy):
             cols = slice((t % 4) * P, (t % 4 + 1) * P)
@@ -229,78 +236,86 @@ def tile_step1attention_pa_kernel(tc, q, k, x, Wv, out):
             keys = P * (it + 1)
             for g in range(GROUPS):
                 if keys <= K_PASS:
-                    pairs = [[(r, 0, keys), (r + 1, 0, keys)] for r in range(0, REP, 2)]
+                    pairs = [
+                        [(r, 0, keys, keys - P + SUB * (r + 1)) for r in (first_r, first_r + 1)] for first_r in range(0, REP, 2)
+                    ]
                 else:
-                    pairs = [[(r, 0, K_PASS), (r, K_PASS, keys - K_PASS)] for r in range(REP)]
+                    pairs = [
+                        [(r, 0, K_PASS, K_PASS), (r, K_PASS, keys - K_PASS, keys - K_PASS - P + SUB * (r + 1))]
+                        for r in range(REP)
+                    ]
                 for slot, bank_list in enumerate(pairs):
                     packs.append(
                         {"it": it, "g": g, "banks": bank_list, "slot": slot, "last": slot == len(pairs) - 1,
-                         "joined": 2 if keys <= K_PASS else 1, "place": place, "turn": g * len(pairs) + slot, "e": e_ring[len(packs) % E_RING]}
+                         "place": place, "turn": g * len(pairs) + slot, "e": (e_early if keys <= K_PASS else e_late)[len(packs) % E_RING]}
                     )
         first_late = [pack["it"] >= 4 for pack in packs].index(True)
 
         unit = {}
 
-        def scores(m):
-            pack = packs[m]
-            it, g = pack["it"], pack["g"]
-            pack["z"] = []
-            for r, k0, width in pack["banks"]:
-                z = ps_scores.tile([P, K_PASS], F32, name="z")
-                nc.tensor.matmul(
-                    out=z[:, :width], lhsT=qT[it][:, REP * g + r, :], rhs=kT[k0 // K_PASS][:, g, :width],
-                    start=True, stop=False,
-                )
-                pack["z"].append(z)
+        def open_pack(m):
+            packs[m]["z"] = [ps_scores.tile([P, K_PASS], F32, name="z") for b in range(2)]
 
-        def add_bias(m):
+        def add_scores(m, first):
             pack = packs[m]
-            it, g = pack["it"], pack["g"]
-            for z, (r, k0, width) in zip(pack["z"], pack["banks"]):
-                h = REP * g + r
-                for j in range(width // P):
-                    delta = it - (k0 // P + j)
+            for z, (r, k0, width, used) in zip(pack["z"], pack["banks"]):
+                cols = width if first else used
+                nc.tensor.matmul(
+                    out=z[:, :cols], lhsT=qT[pack["it"]][:, REP * pack["g"] + r, :],
+                    rhs=kT[k0 // K_PASS][:, pack["g"], :cols], start=first, stop=not first,
+                )
+
+        def add_bias(m, first):
+            pack = packs[m]
+            for z, (r, k0, width, used) in zip(pack["z"], pack["banks"]):
+                tiles = width // P
+                for j in range(tiles):
+                    delta = pack["it"] - (k0 // P + j)
                     nc.tensor.matmul(
                         out=z[:, j * P : (j + 1) * P],
-                        lhsT=bias[:, h, delta * P : (delta + 1) * P],
+                        lhsT=bias[:, pack["g"], REP * delta + r, :, :].rearrange("p r w -> p (r w)"),
                         rhs=ident_f32[:],
                         is_transpose=True,
-                        start=False,
-                        stop=(j == width // P - 1),
+                        start=first and j == 0,
+                        stop=not first and j == tiles - 1,
                     )
 
         def scale_next(m):
             it = packs[m]["it"]
-            for r, k0, width in packs[m]["banks"]:
+            for r, k0, width, used in packs[m]["banks"]:
                 h = REP * packs[m]["g"] + r
                 if k0 == 0 and it % 2 == 0 and it + 1 < Q_TILES:
-                    scale_bias(h, slice(P * (it + 1), min(P * (it + 3), S)))
+                    scale_bias(h, slice(P * (it + 1), min(P * (it + 3), S)), nc.gpsimd)
 
         def maximum(m, b):
             pack = packs[m]
-            r, k0, width = pack["banks"][b]
+            r, k0, width, used = pack["banks"][b]
             if b == 0:
                 pack["scaled"] = wide_pool.tile([P, 2, K_PASS], F32, name="scaled", tag="wide")
                 pack["exp_bias"] = [stats.tile([P, 1], F32, name="exp_bias%d" % c, tag="exp_bias%d" % c) for c in range(2)]
             nc.vector.tensor_scalar(
-                out=pack["scaled"][:, b, :width], in0=pack["z"][b][:, :width], scalar1=-SCALE,
-                scalar2=pack["exp_bias"][0][:] if k0 > 0 else None,
-                op0=ALU.mult, op1=ALU.min, accum_out=pack["exp_bias"][b][:],
+                out=pack["scaled"][:, b, :used], in0=pack["z"][b][:, :used], scalar1=-SCALE,
+                scalar2=None, op0=ALU.mult, op1=ALU.min, accum_out=pack["exp_bias"][b][:],
             )
+            if k0 > 0:
+                joined = stats.tile([P, 1], F32, name="joined")
+                nc.gpsimd.tensor_scalar(
+                    out=joined[:], in0=pack["exp_bias"][0][:], scalar1=pack["exp_bias"][1][:], scalar2=1.0,
+                    op0=ALU.min, op1=ALU.mult,
+                )
+                pack["exp_bias"][1] = joined
 
         def exponentials(m):
             pack = packs[m]
             it, g = pack["it"], pack["g"]
-            if first_late <= m < first_late + E_RING:
-                nc.gpsimd.memset(pack["e"][:].bitcast(F32)[:, 1, P // 2 :], 0.0)
             if pack["slot"] == 0:
                 unit[(it, g)] = {"row_sums": stats.tile([P, REP], F32, name="row_sums")}
             e = pack["e"][:].rearrange("p c k -> p (c k)")
             scaled = pack["scaled"][:].rearrange("p c k -> p (c k)")
             if it < 4:
-                pieces = [(r, slice(c * K_PASS, c * K_PASS + width)) for c, (r, k0, width) in enumerate(pack["banks"])]
+                pieces = [(r, slice(c * K_PASS, c * K_PASS + used)) for c, (r, k0, width, used) in enumerate(pack["banks"])]
             else:
-                pieces = [(pack["slot"], slice(0, P * (it + 1)))]
+                pieces = [(pack["slot"], slice(0, P * it + SUB * (pack["slot"] + 1)))]
             for r, cols in pieces:
                 nc.scalar.activation(
                     out=e[:, cols],
@@ -313,17 +328,19 @@ def tile_step1attention_pa_kernel(tc, q, k, x, Wv, out):
 
         def regroup_e(m):
             pack = packs[m]
-            n = pack["slot"] % pack["joined"]
-            pack["grouped"] = grouped_tile(pack["joined"]) if n == 0 else packs[m - 1]["grouped"]
+            n = m % 2
+            pack["grouped"] = grouped_tile(2) if n == 0 else packs[m - 1]["grouped"]
             regroup(pack["bank"], pack["grouped"][:, n, :], nc.vector.tensor_copy if m in (count - 3, count - 2) else nc.scalar.copy)
 
         def quantise_e(m):
             pack = packs[m]
             tiles = unit[(pack["it"], pack["g"])]
             if "e_codes" not in tiles:
-                tiles["e_codes"] = e_codes_pool.tile([P, 2 * REP * P], U32, name="e_codes", align_bytes=64)
-                tiles["e_scales"] = e_codes_pool.tile([P, 2 * REP * P], U8, name="e_scales", align_bytes=64)
-            cols = slice(2 * (pack["slot"] + 1 - pack["joined"]) * P, 2 * (pack["slot"] + 1) * P)
+                kind = "early" if pack["it"] < 4 else "late"
+                width, bufs = (REP * P, 7) if pack["it"] < 4 else (2 * REP * P, 3)
+                tiles["e_codes"] = e_codes_pool.tile([P, width], U32, name="e_codes", tag="codes_" + kind, bufs=bufs, align_bytes=64)
+                tiles["e_scales"] = e_codes_pool.tile([P, width], U8, name="e_scales", tag="scales_" + kind, bufs=bufs, align_bytes=64)
+            cols = slice(2 * (pack["slot"] + 1 - 2) * P, 2 * (pack["slot"] + 1) * P)
             quantise(pack["grouped"], tiles["e_codes"][:, cols], tiles["e_scales"][:, cols])
 
         def invert_sums(it, g, r0, r1):
@@ -365,34 +382,45 @@ def tile_step1attention_pa_kernel(tc, q, k, x, Wv, out):
                     in1=tiles["inv_sum", r0][:, r0:r1].unsqueeze(2).to_broadcast([P, r1 - r0, P]),
                     op=ALU.mult,
                 )
-            cols = slice((REP * g + r0) * P, (REP * g + r1) * P)
-            nc.sync.dma_start(
-                out=out_rows[it * P : (it + 1) * P, cols], in_=o[:, r0:r1, :].rearrange("p r d -> p (r d)")
-            )
+            rows = out_rows[it * P + SUB * r0 : it * P + SUB * r1, :]
+            for r in range(REP):
+                cols = slice((REP * g + r) * P, (REP * g + r + 1) * P)
+                nc.sync.dma_start(
+                    out=rows[:, cols].rearrange("(j w) d -> w j d", w=SUB), in_=o[r * SUB : (r + 1) * SUB, r0:r1, :]
+                )
 
         for t in range(order[0] + 1):
             keep_keys(t, transpose_keys(t), nc.vector.tensor_copy)
+        for h in range(REP):
+            scale_bias(h, slice(0, first), nc.vector)
         for part in range(2):
             keep_queries(order[0], part, transpose_queries(order[0], part), nc.scalar.copy if part == 0 else nc.vector.tensor_copy)
         count = len(packs)
+        steps = count // 2
         rows_of_step = {n: [n] for n in range(12)}
         values_of_step = {6: [(0, 0)], 7: [(0, 1)], 8: [(0, 2)], 9: [(0, 3)], 17: [(1, 0)], 19: [(1, 1)], 21: [(1, 2)], 23: [(1, 3)]}
         last_values = [max(step for step in values_of_step if any(kp == key_pass for kp, g in values_of_step[step])) for key_pass in range(2)]
         waiting = []
         dividing = []
-        quantised = 0
+        done = []
 
         def finish_pack(m, step):
+            done.append(m)
+            quantise_e(m)
             pack = packs[m]
-            if pack["slot"] % pack["joined"] == pack["joined"] - 1:
-                quantise_e(m)
-            if pack["last"] and m < count - 1:
-                waiting.append((step + 1, pack["it"], pack["g"], 0, REP))
-            if m >= count - REP and m % 2 == 1:
+            if m >= count - REP:
                 waiting.append((step + 1, pack["it"], pack["g"], pack["slot"] - 1, pack["slot"] + 1))
+            elif pack["last"]:
+                waiting.append((step + 1, pack["it"], pack["g"], 0, REP))
 
-        m = -1
-        while m < count + 6 or waiting or dividing:
+        def exp_and_copy(e_pack, copy_pack):
+            if 0 <= e_pack < count:
+                exponentials(e_pack)
+            if 0 <= copy_pack < count:
+                regroup_e(copy_pack)
+
+        first_pair = 32
+        for m in range(-1, first_pair):
             e_pack = m - 3
             if 0 <= e_pack < count:
                 packs[e_pack]["bank"] = transpose_planes(packs[e_pack]["e"][:].rearrange("p c k -> p (c k)").bitcast(F32))
@@ -405,8 +433,12 @@ def tile_step1attention_pa_kernel(tc, q, k, x, Wv, out):
                     part_bank = transpose_keys(after)
             for n in rows_of_step.get(m, []):
                 spread_transposes(n)
-            if m + 1 < count:
-                scores(m + 1)
+            open_pack(m + 1)
+            if m + 1 < first_pair:
+                add_bias(m + 1, True)
+                add_scores(m + 1, False)
+            else:
+                add_scores(m + 1, True)
             for key_pass, g in values_of_step.get(m, []):
                 project_values(key_pass, g)
             finished = dividing
@@ -415,13 +447,10 @@ def tile_step1attention_pa_kernel(tc, q, k, x, Wv, out):
                 dividing.append(waiting[0][1:])
                 waiting.remove(waiting[0])
                 weighted_values(*dividing[0])
-            if m + 1 < count:
-                add_bias(m + 1)
             if 0 <= m < count:
                 maximum(m, 0)
-            while quantised < count and quantised <= m - 5:
-                finish_pack(quantised, m)
-                quantised += 1
+            if m - 5 >= 0 and (m - 5) % 2 == 1:
+                finish_pack(m - 5, m)
             if 0 <= m < count:
                 maximum(m, 1)
             if m == 0:
@@ -432,9 +461,6 @@ def tile_step1attention_pa_kernel(tc, q, k, x, Wv, out):
                 exponentials(m - 1)
             if 0 <= e_pack < count:
                 regroup_e(e_pack)
-            while m >= count and quantised <= min(e_pack, count - 1):
-                finish_pack(quantised, m)
-                quantised += 1
             if 0 <= part < 2:
                 keep_queries(after, part, part_bank, nc.scalar.copy)
             if part == 2:
@@ -458,4 +484,63 @@ def tile_step1attention_pa_kernel(tc, q, k, x, Wv, out):
                 divide_and_store(*part_of_unit)
             for part_of_unit in dividing:
                 invert_sums(*part_of_unit)
-            m += 1
+
+        waiting = [(0,) + entry[1:] for entry in waiting]
+        s = first_pair // 2
+        while s < steps + 3 or waiting or dividing:
+            a, b = 2 * s, 2 * s + 1
+            turned = [m for m in (a - 3, a - 2) if 0 <= m < count]
+            if 0 <= s < steps:
+                add_bias(a, False)
+                open_pack(b)
+                add_bias(b, True)
+            for m in turned:
+                packs[m]["bank"] = transpose_planes(packs[m]["e"][:].rearrange("p c k -> p (c k)").bitcast(F32))
+            new_parts = []
+            if 0 <= s < steps and packs[a]["place"] + 1 < len(order):
+                after = order[packs[a]["place"] + 1]
+                turn = packs[a]["turn"] // 2 - 0
+                new_parts = [[0], [1], [2], []][turn] if 0 <= turn < 4 else []
+            part_banks = [transpose_queries(after, part) if part < 2 else transpose_keys(after) for part in new_parts if part < 2 or after > 0]
+            if 0 <= s < steps:
+                add_scores(b, False)
+            if s + 1 < steps:
+                open_pack(a + 2)
+                add_scores(a + 2, True)
+            finished = dividing
+            dividing = []
+            while waiting and waiting[0][0] <= s and len(dividing) < 1:
+                dividing.append(waiting[0][1:])
+                waiting.remove(waiting[0])
+                weighted_values(*dividing[-1])
+            if 0 <= s < steps:
+                maximum(a, 0)
+                maximum(a, 1)
+            q_pack = a - 5
+            if 0 <= q_pack < count and s < steps:
+                finish_pack(q_pack, s)
+            if 0 <= s < steps:
+                maximum(b, 0)
+                maximum(b, 1)
+            for part_of_unit in finished:
+                divide_and_store(*part_of_unit)
+            for m in (a, b):
+                if 0 <= m < count:
+                    scale_next(m)
+            exp_and_copy(a - 1, a - 3)
+            exp_and_copy(a - 0, a - 2)
+            if s >= steps:
+                for m in range(max(q_pack, 0), min(a - 2, count)):
+                    if m % 2 == 1 and m not in done:
+                        finish_pack(m, s)
+            for part, part_bank in zip(new_parts, part_banks):
+                if part < 2:
+                    keep_queries(after, part, part_bank, nc.scalar.copy)
+                else:
+                    keep_keys(after, part_bank, nc.scalar.copy)
+            if 2 in new_parts and packs[a]["place"] + 2 < len(order):
+                load_keys(order[packs[a]["place"] + 2])
+                load_queries(order[packs[a]["place"] + 2])
+            for part_of_unit in dividing:
+                invert_sums(*part_of_unit)
+            s += 1

@@ -92,9 +92,6 @@ def tile_step1attention_pa_kernel(tc, q, k, x, Wv, out):
 
         e_early = [keep.tile([P, 2, K_PASS], BF16, name="e_early%d" % n) for n in range(E_RING)]
         e_late = [keep.tile([P, 2, K_PASS], BF16, name="e_late%d" % n) for n in range(E_RING)]
-        for e_tile in e_early:
-            nc.vector.memset(e_tile[:].bitcast(F32), 0.0)
-
         dist = wide_pool.tile([P, S], F32, name="dist", tag="wide")
         nc.gpsimd.iota(
             dist[:], pattern=[[1, S]], base=0, channel_multiplier=-1, allow_small_or_imprecise_dtypes=True
@@ -115,6 +112,8 @@ def tile_step1attention_pa_kernel(tc, q, k, x, Wv, out):
                 out=neg_root[:, cols], in0=neg_root[:, cols], scalar=-1.0, in1=dist[:, cols], op0=ALU.mult, op1=ALU.add
             )
 
+        for e_tile in e_early:
+            nc.vector.memset(e_tile[:].bitcast(F32), 0.0)
         first = P * (order[0] + 1)
         mask_root(slice(0, first))
 
@@ -295,15 +294,9 @@ def tile_step1attention_pa_kernel(tc, q, k, x, Wv, out):
                 pack["exp_bias"] = [stats.tile([P, 1], F32, name="exp_bias%d" % c, tag="exp_bias%d" % c) for c in range(2)]
             nc.vector.tensor_scalar(
                 out=pack["scaled"][:, b, :used], in0=pack["z"][b][:, :used], scalar1=-SCALE,
-                scalar2=None, op0=ALU.mult, op1=ALU.min, accum_out=pack["exp_bias"][b][:],
+                scalar2=pack["exp_bias"][0][:] if k0 > 0 else None,
+                op0=ALU.mult, op1=ALU.min, accum_out=pack["exp_bias"][b][:],
             )
-            if k0 > 0:
-                joined = stats.tile([P, 1], F32, name="joined")
-                nc.gpsimd.tensor_scalar(
-                    out=joined[:], in0=pack["exp_bias"][0][:], scalar1=pack["exp_bias"][1][:], scalar2=1.0,
-                    op0=ALU.min, op1=ALU.mult,
-                )
-                pack["exp_bias"][1] = joined
 
         def exponentials(m):
             pack = packs[m]
@@ -324,6 +317,22 @@ def tile_step1attention_pa_kernel(tc, q, k, x, Wv, out):
                     bias=pack["exp_bias"][r % 2 if it < 4 else 1][:],
                     scale=-1.0,
                     accum_out=unit[(it, g)]["row_sums"][:, r : r + 1],
+                )
+
+        e_banks = []
+
+        def transpose_e(m):
+            pack = packs[m]
+            words = pack["e"][:].rearrange("p c k -> p (c k)").bitcast(F32)
+            if m < first_late:
+                pack["bank"] = transpose_planes(words)
+                return
+            if m < first_late + 2:
+                e_banks.append(ps_other.tile([P, 4, P], F32, name="e_bank", tag="other"))
+            pack["bank"] = e_banks[m % 2]
+            for plane in range(4 if pack["it"] >= 6 or m < first_late + 2 else 3):
+                nc.tensor.transpose(
+                    out=pack["bank"][:, plane, :], in_=words[:, plane * P : (plane + 1) * P], identity=ident_f32[:]
                 )
 
         def regroup_e(m):
@@ -419,11 +428,11 @@ def tile_step1attention_pa_kernel(tc, q, k, x, Wv, out):
             if 0 <= copy_pack < count:
                 regroup_e(copy_pack)
 
-        first_pair = 32
+        first_pair = 96
         for m in range(-1, first_pair):
             e_pack = m - 3
             if 0 <= e_pack < count:
-                packs[e_pack]["bank"] = transpose_planes(packs[e_pack]["e"][:].rearrange("p c k -> p (c k)").bitcast(F32))
+                transpose_e(e_pack)
             part = packs[m]["turn"] - 3 if 0 <= m < count and packs[m]["place"] + 1 < len(order) else -1
             if 0 <= part < 3:
                 after = order[packs[m]["place"] + 1]
@@ -433,11 +442,12 @@ def tile_step1attention_pa_kernel(tc, q, k, x, Wv, out):
                     part_bank = transpose_keys(after)
             for n in rows_of_step.get(m, []):
                 spread_transposes(n)
-            open_pack(m + 1)
+            if m + 1 < count:
+                open_pack(m + 1)
             if m + 1 < first_pair:
                 add_bias(m + 1, True)
                 add_scores(m + 1, False)
-            else:
+            elif m + 1 < count:
                 add_scores(m + 1, True)
             for key_pass, g in values_of_step.get(m, []):
                 project_values(key_pass, g)
@@ -495,7 +505,7 @@ def tile_step1attention_pa_kernel(tc, q, k, x, Wv, out):
                 open_pack(b)
                 add_bias(b, True)
             for m in turned:
-                packs[m]["bank"] = transpose_planes(packs[m]["e"][:].rearrange("p c k -> p (c k)").bitcast(F32))
+                transpose_e(m)
             new_parts = []
             if 0 <= s < steps and packs[a]["place"] + 1 < len(order):
                 after = order[packs[a]["place"] + 1]

@@ -11,7 +11,6 @@ U8 = mybir.dt.uint8
 FP8X4 = mybir.dt.float8_e4m3fn_x4
 ALU = mybir.AluOpType
 ACT = mybir.ActivationFunctionType
-AXIS = mybir.AxisListType
 
 P = 128
 S = 1024
@@ -19,14 +18,17 @@ HD = 2048
 HEADS = 16
 GROUPS = 4
 REP = HEADS // GROUPS
+SUB = P // REP
 GD = GROUPS * P
 Q_TILES = S // P
 K_PASS = 512
+ONE_BANK = K_PASS // P
 SCALE = 1.0 / math.sqrt(P)
 MASKED = 1.0e30
 TINY = 1.0e-30
-E_RING = 4
-SUB = P // REP
+E_RING = REP
+STEEP = 2
+ROWS_AHEAD = 4
 
 FLOPS = 2 * S * HD * GD + 2 * 2 * HEADS * P * (K_PASS * K_PASS + K_PASS * S)
 
@@ -41,26 +43,25 @@ def tile_step1attention_pa_kernel(tc, q, k, x, Wv, out):
     with ExitStack() as ctx:
         ctx.enter_context(tc.manual_schedule())
         keep = ctx.enter_context(tc.tile_pool(name="keep", bufs=1))
-        wide_pool = ctx.enter_context(tc.tile_pool(name="wide_pool", bufs=6))
+        wide_pool = ctx.enter_context(tc.tile_pool(name="wide_pool", bufs=8))
         q_pool = ctx.enter_context(tc.tile_pool(name="q_pool", bufs=2))
         qT_pool = ctx.enter_context(tc.tile_pool(name="qT_pool", bufs=2))
-        grouped_pool = ctx.enter_context(tc.tile_pool(name="grouped_pool", bufs=4))
+        grouped_pool = ctx.enter_context(tc.tile_pool(name="grouped_pool", bufs=5))
         stats = ctx.enter_context(tc.tile_pool(name="stats", bufs=6))
-        e_codes_pool = ctx.enter_context(tc.tile_pool(name="e_codes_pool", bufs=6))
+        early_codes = ctx.enter_context(tc.tile_pool(name="early_codes", bufs=8))
+        late_codes = ctx.enter_context(tc.tile_pool(name="late_codes", bufs=3))
         o_pool = ctx.enter_context(tc.tile_pool(name="o_pool", bufs=3))
         ps_scores = ctx.enter_context(tc.psum_pool(name="ps_scores", bufs=4))
         ps_other = ctx.enter_context(tc.psum_pool(name="ps_other", bufs=4))
 
-        order = list(range(Q_TILES))
-
         k_raw = [keep.tile([P, GD], BF16, name="k_raw%d" % t) for t in range(Q_TILES)]
         q_raw = {}
-        raw = {}
+        row_raw = {}
 
         def load_keys(t):
             nc.sync.dma_start(out=k_raw[t][:], in_=k_rows[t * P : (t + 1) * P, :])
 
-        def load_queries(it, pieces=1):
+        def load_queries(it, pieces):
             q_raw[it] = q_pool.tile([P, HD], BF16, name="q_raw")
             for n in range(pieces):
                 cols = slice(n * HD // pieces, (n + 1) * HD // pieces)
@@ -74,70 +75,119 @@ def tile_step1attention_pa_kernel(tc, q, k, x, Wv, out):
         v_scales = keep.tile([P, S // K_PASS, GD], U8, name="v_scales", align_bytes=64)
 
         x_tiles = x_rows.rearrange("(a p e) c -> a e p c", p=P, e=2)
-        w_tile = [(Wv[g * P : (g + 1) * P, :], w_codes[:, g, :], w_scales[:, g, :]) for g in range(GROUPS)]
-        x_tile = [(x_tiles[n // 2, n % 2], x_codes[:, n, :], x_scales[:, n, :]) for n in range(Q_TILES)]
-        row_tiles = [w_tile[0]] + x_tile[:4] + w_tile[1:] + x_tile[4:]
+        w_rows = [(Wv[g * P : (g + 1) * P, :], w_codes[:, g, :], w_scales[:, g, :]) for g in range(GROUPS)]
+        x_parts = [(x_tiles[n // 2, n % 2], x_codes[:, n, :], x_scales[:, n, :]) for n in range(Q_TILES)]
+        row_tiles = w_rows[:1] + x_parts[:4] + w_rows[1:] + x_parts[4:]
 
         def load_rows(n):
-            raw[n] = wide_pool.tile([P, HD], BF16, name="raw", tag="wide")
-            nc.sync.dma_start(out=raw[n][:], in_=row_tiles[n][0])
+            row_raw[n] = wide_pool.tile([P, HD], BF16, name="row_raw", tag="wide")
+            nc.sync.dma_start(out=row_raw[n][:], in_=row_tiles[n][0])
 
-        for t in range(order[0] + 1):
-            load_keys(t)
-        load_queries(order[0], pieces=2)
-        for n in range(4):
+        load_keys(0)
+        load_queries(0, pieces=2)
+        for n in range(ROWS_AHEAD):
             load_rows(n)
-        load_keys(order[1])
-        load_queries(order[1])
+        load_keys(1)
+        load_queries(1, pieces=1)
 
-        e_early = [keep.tile([P, 2, K_PASS], BF16, name="e_early%d" % n) for n in range(E_RING)]
-        e_late = [keep.tile([P, 2, K_PASS], BF16, name="e_late%d" % n) for n in range(E_RING)]
+        offset = keep.tile([P, 1], F32, name="offset")
+        factor = keep.tile([P, 1], F32, name="factor")
+        power = keep.tile([P, REP], F32, name="power")
+        for n in range(REP):
+            nc.vector.memset(offset[n * SUB : (n + 1) * SUB, :], -float(n * SUB))
+        for c in range(2):
+            nc.vector.memset(factor[c * P // 2 : (c + 1) * P // 2, :], float(c + 1))
+        nc.vector.memset(power[:], 0.0)
+        for r in range(REP):
+            c = r % 2
+            nc.vector.memset(power[c * P // 2 : (c + 1) * P // 2, r : r + 1], -(2.0 ** (3 - (r + c) // 2)))
+
+        ident_bf = keep.tile([P, P], BF16, name="ident_bf")
+        make_identity(nc, ident_bf[:])
         dist = wide_pool.tile([P, S], F32, name="dist", tag="wide")
         nc.gpsimd.iota(
             dist[:], pattern=[[1, S]], base=0, channel_multiplier=-1, allow_small_or_imprecise_dtypes=True
         )
-        ident_bf = keep.tile([P, P], BF16, name="ident_bf")
-        make_identity(nc, ident_bf[:])
+        row_dist = wide_pool.tile([P, S], F32, name="row_dist", tag="wide")
+        nc.gpsimd.iota(
+            row_dist[:], pattern=[[-1, S]], base=S - SUB, channel_multiplier=1, allow_small_or_imprecise_dtypes=True
+        )
         ident_f32 = keep.tile([P, P], F32, name="ident_f32")
         make_identity(nc, ident_f32[:])
-        neg_root = keep.tile([P, S], F32, name="neg_root")
-        nc.vector.tensor_scalar(out=neg_root[:], in0=dist[:], scalar1=0.0, scalar2=TINY, op0=ALU.max, op1=ALU.add)
-        nc.scalar.activation(out=neg_root[:], in_=neg_root[:], func=ACT.Sqrt)
+        root = keep.tile([P, S], F32, name="root")
+        nc.vector.tensor_scalar(out=root[:], in0=dist[:], scalar1=0.0, scalar2=TINY, op0=ALU.add, op1=ALU.max)
+        nc.scalar.activation(out=root[:], in_=root[:], func=ACT.Sqrt)
 
-        def mask_root(cols):
+        e_early = [keep.tile([P, 2, K_PASS], BF16, name="e_early%d" % n) for n in range(E_RING)]
+        e_late = [keep.tile([P, 2, K_PASS], BF16, name="e_late%d" % n) for n in range(E_RING)]
+        row_root = wide_pool.tile([P, S], F32, name="row_root", tag="wide")
+        nc.vector.tensor_scalar(
+            out=row_root[:], in0=row_dist[:], scalar1=offset[:], scalar2=TINY, op0=ALU.add, op1=ALU.max
+        )
+        nc.scalar.activation(out=row_root[:], in_=row_root[:], func=ACT.Sqrt, scale=factor[:])
+        nc.vector.tensor_scalar(
+            out=dist[:, :P], in0=dist[:, :P], scalar1=0.0, scalar2=-MASKED, op0=ALU.min, op1=ALU.mult
+        )
+        nc.vector.tensor_tensor(out=root[:, :P], in0=root[:, :P], in1=dist[:, :P], op=ALU.add)
+
+        bias = keep.tile([P, STEEP, S // SUB, REP, SUB], F32, name="bias")
+
+        def scale_bias(engine, g, r, cols):
+            slope = 2.0 ** (-(REP * g + r + 1) / 2.0)
+            engine.tensor_scalar(
+                out=bias[:, g, cols.start // SUB : cols.stop // SUB, r, :],
+                in0=root[:, cols].rearrange("p (n w) -> p n w", w=SUB),
+                scalar1=-slope / SCALE, scalar2=0.0, op0=ALU.mult, op1=ALU.add,
+            )
+
+        roots = keep.tile([P, S], BF16, name="roots")
+        column = keep.tile([P, REP, SUB], F32, name="column")
+        slopes = {g: keep.tile([P, REP, SUB], BF16, name="slopes%d" % g) for g in range(STEEP, GROUPS)}
+        nc.gpsimd.iota(
+            column[:], pattern=[[0, REP], [1, SUB]], base=0, channel_multiplier=-1, allow_small_or_imprecise_dtypes=True
+        )
+        def mask_roots():
+            cols = slice(S - SUB, S)
             nc.vector.tensor_scalar(
-                out=dist[:, cols], in0=dist[:, cols], scalar1=0.0, scalar2=MASKED, op0=ALU.min, op1=ALU.mult
+                out=row_dist[:, cols], in0=row_dist[:, cols], scalar1=offset[:], scalar2=0.0, op0=ALU.add, op1=ALU.min
             )
             nc.vector.scalar_tensor_tensor(
-                out=neg_root[:, cols], in0=neg_root[:, cols], scalar=-1.0, in1=dist[:, cols], op0=ALU.mult, op1=ALU.add
-            )
-
-        for e_tile in e_early:
-            nc.vector.memset(e_tile[:].bitcast(F32), 0.0)
-        first = P * (order[0] + 1)
-        mask_root(slice(0, first))
-
-        bias = keep.tile([P, GROUPS, S // SUB, REP, SUB], F32, name="bias")
-
-        def scale_bias(h, cols, engine):
-            slope = 2.0 ** (-(h + 1) / 2.0)
-            engine.tensor_scalar(
-                out=bias[:, h // REP, cols.start // SUB : cols.stop // SUB, h % REP, :],
-                in0=neg_root[:, cols].rearrange("p (n w) -> p n w", w=SUB), scalar1=slope / SCALE, scalar2=0.0,
+                out=row_root[:, cols], in0=row_dist[:, cols], scalar=-MASKED, in1=row_root[:, cols],
                 op0=ALU.mult, op1=ALU.add,
             )
 
-        for h in range(HEADS):
-            if h >= REP:
-                scale_bias(h, slice(0, first), nc.gpsimd)
-        for e_tile in e_late:
-            nc.gpsimd.memset(e_tile[:, 1, :].bitcast(F32), 0.0)
+        def split_roots(engine, cols):
+            engine.tensor_scalar(
+                out=roots[:, cols], in0=row_root[:, cols], scalar1=1.0, scalar2=0.0, op0=ALU.mult, op1=ALU.add
+            )
+            for c in range(2):
+                low = slice((2 * c + 1) * SUB, (2 * c + 2) * SUB)
+                engine.tensor_tensor(
+                    out=roots[low, cols], in0=row_root[low, cols], in1=roots[low, cols], op=ALU.subtract
+                )
+
+        def make_slopes():
+            nc.vector.tensor_scalar(
+                out=column[:], in0=column[:], scalar1=offset[:], scalar2=0.0, op0=ALU.subtract, op1=ALU.is_equal
+            )
+            for g in range(STEEP, GROUPS):
+                for r in range(REP):
+                    nc.gpsimd.tensor_scalar(
+                        out=slopes[g][:, r, :], in0=column[:, r, :], scalar1=power[:, r : r + 1],
+                        scalar2=2.0 ** (-2 * g), op0=ALU.mult, op1=ALU.mult,
+                    )
 
         def transpose_planes(words):
             bank = ps_other.tile([P, 4, P], F32, name="bank", tag="other")
             for a in range(4):
                 nc.tensor.transpose(out=bank[:, a, :], in_=words[:, a * P : (a + 1) * P], identity=ident_f32[:])
             return bank
+
+        def grouped_pair():
+            return grouped_pool.tile([P, 2, 2 * K_PASS], BF16, name="grouped", align_bytes=64)
+
+        def grouped_single():
+            return grouped_pool.tile([P, 1, 2 * K_PASS], BF16, name="grouped_single", align_bytes=64)
 
         def regroup(bank, grouped, copy):
             copy(
@@ -150,18 +200,15 @@ def tile_step1attention_pa_kernel(tc, q, k, x, Wv, out):
                 out=codes.bitcast(FP8X4), scales=scales, in_=grouped[:].rearrange("p n k -> p (n k)")
             )
 
-        def grouped_tile(banks):
-            return grouped_pool.tile([P, 2, 2 * K_PASS], BF16, name="grouped", tag="grouped", align_bytes=64)
-
         row_banks = {}
         row_grouped = {}
 
-        def spread_transposes(n):
-            words = raw[n][:].bitcast(F32)
+        def transpose_rows(n):
+            words = row_raw[n][:].bitcast(F32)
             row_banks[n] = [transpose_planes(words[:, 4 * half * P : 4 * (half + 1) * P]) for half in range(2)]
 
-        def spread_copies(n):
-            row_grouped[n] = grouped_tile(2)
+        def regroup_rows(n):
+            row_grouped[n] = grouped_pair()
             regroup(row_banks[n][0], row_grouped[n][:, 0, :], nc.vector.tensor_copy if n % 2 == 0 else nc.scalar.copy)
             regroup(row_banks[n][1], row_grouped[n][:, 1, :], nc.scalar.copy)
 
@@ -185,113 +232,108 @@ def tile_step1attention_pa_kernel(tc, q, k, x, Wv, out):
                         start=(c == 0),
                         stop=(c == HD // K_PASS - 1),
                     )
-            v_sums[(key_pass, g)] = sums
+            v_sums[key_pass, g] = sums
 
         def group_values(key_pass, g):
-            grouped = grouped_pool.tile([P, P, 4], BF16, name="grouped_v", tag="grouped_v", bufs=3, align_bytes=64)
-            nc.scalar.copy(out=grouped[:], in_=v_sums[(key_pass, g)][:].rearrange("p t n -> p n t"))
-            v_grouped[(key_pass, g)] = grouped
+            grouped = grouped_pool.tile([P, P, 4], BF16, name="v_grouped", bufs=3, align_bytes=64)
+            nc.scalar.copy(out=grouped[:], in_=v_sums[key_pass, g][:].rearrange("p t n -> p n t"))
+            v_grouped[key_pass, g] = grouped
 
         def quantise_values(key_pass, g):
             cols = slice(g * P, (g + 1) * P)
-            nc.vector.quantize_mx(
-                out=v_codes[:, key_pass, cols].bitcast(FP8X4),
-                scales=v_scales[:, key_pass, cols],
-                in_=v_grouped[(key_pass, g)][:].rearrange("p n t -> p (n t)"),
-            )
+            quantise(v_grouped[key_pass, g], v_codes[:, key_pass, cols], v_scales[:, key_pass, cols])
 
         kT = [keep.tile([P, GROUPS, K_PASS], BF16, name="kT%d" % c) for c in range(S // K_PASS)]
         qT = {}
 
-        def transpose_queries(it, part):
+        def transpose_part(it, part):
+            if part == 2:
+                bank = ps_other.tile([P, GROUPS, P], BF16, name="bank_k", tag="other")
+                for g in range(GROUPS):
+                    nc.tensor.transpose(out=bank[:, g, :], in_=k_raw[it][:, g * P : (g + 1) * P], identity=ident_bf[:])
+                return bank
             if part == 0:
-                qT[it] = qT_pool.tile([P, HEADS, P], BF16, name="qT")
-            bank = ps_other.tile([P, 2, REP, REP, SUB], BF16, name="bank_q", tag="other")
-            for j in range(8):
-                h = 8 * part + j
-                nc.tensor.transpose(
-                    out=bank[:, j // REP, :, j % REP, :], in_=q_raw[it][:, h * P : (h + 1) * P], identity=ident_bf[:]
+                qT[it] = qT_pool.tile([P, GROUPS, REP, P], BF16, name="qT")
+            bank = ps_other.tile([P, GROUPS // 2, REP, REP, SUB], BF16, name="bank_q", tag="other")
+            for g in range(GROUPS // 2):
+                for r in range(REP):
+                    h = REP * (GROUPS // 2 * part + g) + r
+                    nc.tensor.transpose(
+                        out=bank[:, g, :, r, :], in_=q_raw[it][:, h * P : (h + 1) * P], identity=ident_bf[:]
+                    )
+            return bank
+
+        def keep_part(it, part, bank, copy):
+            if part == 2:
+                cols = slice(it % ONE_BANK * P, (it % ONE_BANK + 1) * P)
+                copy(out=kT[it // ONE_BANK][:, :, cols], in_=bank[:])
+            else:
+                half = slice(GROUPS // 2 * part, GROUPS // 2 * (part + 1))
+                copy(
+                    out=qT[it][:, half, :, :].rearrange("p g j n -> p (g j n)"),
+                    in_=bank[:].rearrange("p g j r w -> p (g j r w)"),
                 )
-            return bank
-
-        def transpose_keys(t):
-            bank = ps_other.tile([P, GROUPS, P], BF16, name="bank_k", tag="other")
-            for g in range(GROUPS):
-                nc.tensor.transpose(out=bank[:, g, :], in_=k_raw[t][:, g * P : (g + 1) * P], identity=ident_bf[:])
-            return bank
-
-        def keep_queries(it, part, bank, copy):
-            copy(
-                out=qT[it][:, 8 * part : 8 * (part + 1), :].rearrange("p t n -> p (t n)"),
-                in_=bank[:].rearrange("p g j r w -> p (g j r w)"),
-            )
-
-        def keep_keys(t, bank, copy):
-            cols = slice((t % 4) * P, (t % 4 + 1) * P)
-            copy(out=kT[t // 4][:, :, cols], in_=bank[:])
 
         packs = []
-        for place, it in enumerate(order):
-            keys = P * (it + 1)
+        for it in range(Q_TILES):
             for g in range(GROUPS):
-                if keys <= K_PASS:
-                    pairs = [
-                        [(r, 0, keys, keys - P + SUB * (r + 1)) for r in (first_r, first_r + 1)] for first_r in range(0, REP, 2)
-                    ]
+                keys = [P * it + SUB * (j + 1) for j in range(REP)]
+                if it < ONE_BANK:
+                    pairs = [[(j, 0, P * (it + 1), keys[j]) for j in (n, n + 1)] for n in range(0, REP, 2)]
                 else:
                     pairs = [
-                        [(r, 0, K_PASS, K_PASS), (r, K_PASS, keys - K_PASS, keys - K_PASS - P + SUB * (r + 1))]
-                        for r in range(REP)
+                        [(j, 0, K_PASS, K_PASS), (j, K_PASS, P * (it + 1) - K_PASS, keys[j] - K_PASS)] for j in range(REP)
                     ]
-                for slot, bank_list in enumerate(pairs):
+                for slot, banks in enumerate(pairs):
+                    ring = e_early if it < ONE_BANK else e_late
                     packs.append(
-                        {"it": it, "g": g, "banks": bank_list, "slot": slot, "last": slot == len(pairs) - 1,
-                         "place": place, "turn": g * len(pairs) + slot, "e": (e_early if keys <= K_PASS else e_late)[len(packs) % E_RING]}
+                        {"it": it, "g": g, "banks": banks, "slot": slot, "last": slot == len(pairs) - 1,
+                         "turn": g * len(pairs) + slot, "e": ring[len(packs) % E_RING]}
                     )
-        first_late = [pack["it"] >= 4 for pack in packs].index(True)
-
+        count = len(packs)
+        first_late = [pack["it"] for pack in packs].index(ONE_BANK)
         unit = {}
 
-        def open_pack(m):
+        def open_banks(m):
             packs[m]["z"] = [ps_scores.tile([P, K_PASS], F32, name="z") for b in range(2)]
 
         def add_scores(m, first):
             pack = packs[m]
-            for z, (r, k0, width, used) in zip(pack["z"], pack["banks"]):
-                cols = width if first else used
+            for z, (j, k0, whole, used) in zip(pack["z"], pack["banks"]):
                 nc.tensor.matmul(
-                    out=z[:, :cols], lhsT=qT[pack["it"]][:, REP * pack["g"] + r, :],
-                    rhs=kT[k0 // K_PASS][:, pack["g"], :cols], start=first, stop=not first,
+                    out=z[:, :used], lhsT=qT[pack["it"]][:, pack["g"], j, :],
+                    rhs=kT[k0 // K_PASS][:, pack["g"], :used], start=first, stop=not first,
                 )
 
-        def add_bias(m, first):
+        def add_steep_bias(m):
             pack = packs[m]
-            for z, (r, k0, width, used) in zip(pack["z"], pack["banks"]):
-                tiles = width // P
-                for j in range(tiles):
-                    delta = pack["it"] - (k0 // P + j)
+            for z, (j, k0, whole, used) in zip(pack["z"], pack["banks"]):
+                for n in range(whole // P):
+                    delta = pack["it"] - (k0 // P + n)
                     nc.tensor.matmul(
-                        out=z[:, j * P : (j + 1) * P],
-                        lhsT=bias[:, pack["g"], REP * delta + r, :, :].rearrange("p r w -> p (r w)"),
+                        out=z[:, n * P : (n + 1) * P],
+                        lhsT=bias[:, pack["g"], REP * delta + j, :, :].rearrange("p r w -> p (r w)"),
                         rhs=ident_f32[:],
                         is_transpose=True,
-                        start=first and j == 0,
-                        stop=not first and j == tiles - 1,
+                        start=(n == 0),
+                        stop=False,
                     )
 
-        def scale_next(m):
-            it = packs[m]["it"]
-            for r, k0, width, used in packs[m]["banks"]:
-                h = REP * packs[m]["g"] + r
-                if k0 == 0 and it % 2 == 0 and it + 1 < Q_TILES:
-                    scale_bias(h, slice(P * (it + 1), min(P * (it + 3), S)), nc.gpsimd)
+        def add_flat_bias(m):
+            pack = packs[m]
+            for z, (j, k0, whole, used) in zip(pack["z"], pack["banks"]):
+                y = S - SUB - (P * pack["it"] + SUB * j) + k0
+                nc.tensor.matmul(
+                    out=z[:, :used], lhsT=slopes[pack["g"]][:].rearrange("p r w -> p (r w)"),
+                    rhs=roots[:, y : y + used], start=False, stop=True,
+                )
 
         def maximum(m, b):
             pack = packs[m]
-            r, k0, width, used = pack["banks"][b]
+            j, k0, whole, used = pack["banks"][b]
             if b == 0:
                 pack["scaled"] = wide_pool.tile([P, 2, K_PASS], F32, name="scaled", tag="wide")
-                pack["exp_bias"] = [stats.tile([P, 1], F32, name="exp_bias%d" % c, tag="exp_bias%d" % c) for c in range(2)]
+                pack["exp_bias"] = [stats.tile([P, 1], F32, name="exp_bias%d" % c) for c in range(2)]
             nc.vector.tensor_scalar(
                 out=pack["scaled"][:, b, :used], in0=pack["z"][b][:, :used], scalar1=-SCALE,
                 scalar2=pack["exp_bias"][0][:] if k0 > 0 else None,
@@ -302,21 +344,19 @@ def tile_step1attention_pa_kernel(tc, q, k, x, Wv, out):
             pack = packs[m]
             it, g = pack["it"], pack["g"]
             if pack["slot"] == 0:
-                unit[(it, g)] = {"row_sums": stats.tile([P, REP], F32, name="row_sums")}
-            e = pack["e"][:].rearrange("p c k -> p (c k)")
-            scaled = pack["scaled"][:].rearrange("p c k -> p (c k)")
-            if it < 4:
-                pieces = [(r, slice(c * K_PASS, c * K_PASS + used)) for c, (r, k0, width, used) in enumerate(pack["banks"])]
+                unit[it, g] = {"row_sums": stats.tile([P, REP], F32, name="row_sums")}
+            if it < ONE_BANK:
+                pieces = [(j, c, c * K_PASS, used) for c, (j, k0, whole, used) in enumerate(pack["banks"])]
             else:
-                pieces = [(pack["slot"], slice(0, P * it + SUB * (pack["slot"] + 1)))]
-            for r, cols in pieces:
+                pieces = [(pack["slot"], 1, 0, K_PASS + pack["banks"][1][3])]
+            for j, c, begin, used in pieces:
                 nc.scalar.activation(
-                    out=e[:, cols],
-                    in_=scaled[:, cols],
+                    out=pack["e"][:].rearrange("p c k -> p (c k)")[:, begin : begin + used],
+                    in_=pack["scaled"][:].rearrange("p c k -> p (c k)")[:, begin : begin + used],
                     func=ACT.Exp,
-                    bias=pack["exp_bias"][r % 2 if it < 4 else 1][:],
+                    bias=pack["exp_bias"][c][:],
                     scale=-1.0,
-                    accum_out=unit[(it, g)]["row_sums"][:, r : r + 1],
+                    accum_out=unit[it, g]["row_sums"][:, j : j + 1],
                 )
 
         e_banks = []
@@ -330,43 +370,32 @@ def tile_step1attention_pa_kernel(tc, q, k, x, Wv, out):
             if m < first_late + 2:
                 e_banks.append(ps_other.tile([P, 4, P], F32, name="e_bank", tag="other"))
             pack["bank"] = e_banks[m % 2]
-            for plane in range(4 if pack["it"] >= 6 or m < first_late + 2 else 3):
+            whole = pack["banks"][1][2]
+            for plane in range(4 if whole > 2 * P or m < first_late + 2 else 3):
                 nc.tensor.transpose(
                     out=pack["bank"][:, plane, :], in_=words[:, plane * P : (plane + 1) * P], identity=ident_f32[:]
                 )
 
         def regroup_e(m):
             pack = packs[m]
-            n = m % 2
-            pack["grouped"] = grouped_tile(2) if n == 0 else packs[m - 1]["grouped"]
-            regroup(pack["bank"], pack["grouped"][:, n, :], nc.vector.tensor_copy if m in (count - 3, count - 2) else nc.scalar.copy)
+            if m >= first_late:
+                pack["grouped"] = grouped_single()
+            elif m % 2 == 0:
+                pack["grouped"] = grouped_pair()
+            else:
+                pack["grouped"] = packs[m - 1]["grouped"]
+            copy = nc.vector.tensor_copy if m in (count - 3, count - 2) else nc.scalar.copy
+            regroup(pack["bank"], pack["grouped"][:, 0 if m >= first_late else m % 2, :], copy)
 
-        def quantise_e(m):
-            pack = packs[m]
-            tiles = unit[(pack["it"], pack["g"])]
-            if "e_codes" not in tiles:
-                kind = "early" if pack["it"] < 4 else "late"
-                width, bufs = (REP * P, 7) if pack["it"] < 4 else (2 * REP * P, 3)
-                tiles["e_codes"] = e_codes_pool.tile([P, width], U32, name="e_codes", tag="codes_" + kind, bufs=bufs, align_bytes=64)
-                tiles["e_scales"] = e_codes_pool.tile([P, width], U8, name="e_scales", tag="scales_" + kind, bufs=bufs, align_bytes=64)
-            cols = slice(2 * (pack["slot"] + 1 - 2) * P, 2 * (pack["slot"] + 1) * P)
-            quantise(pack["grouped"], tiles["e_codes"][:, cols], tiles["e_scales"][:, cols])
-
-        def invert_sums(it, g, r0, r1):
-            tiles = unit[(it, g)]
-            inv_sum = stats.tile([P, REP], F32, name="inv_sum")
-            nc.vector.reciprocal(out=inv_sum[:, r0:r1], in_=tiles["row_sums"][:, r0:r1])
-            tiles["inv_sum", r0] = inv_sum
-
-        def weighted_values(it, g, r0, r1):
-            tiles = unit[(it, g)]
-            passes = (P * (it + 1) + K_PASS - 1) // K_PASS
+        def weighted_values(it, g, j0, j1):
+            tiles = unit[it, g]
+            passes = 1 if it < ONE_BANK else 2
             sums = ps_other.tile([P, REP, P], F32, name="o_sums", tag="other")
-            for r in range(r0, r1):
+            for j in range(j0, j1):
                 for c in range(passes):
-                    cols = slice((r * passes + c) * P, (r * passes + c + 1) * P)
+                    cols = slice((j * passes + c) * P, (j * passes + c + 1) * P)
                     nc.tensor.matmul_mx(
-                        out=sums[:, r, :],
+                        out=sums[:, j, :],
                         lhsT=tiles["e_codes"][:, cols].bitcast(FP8X4),
                         lhsT_scale=tiles["e_scales"][:, cols],
                         rhs=v_codes[:, c, g * P : (g + 1) * P].bitcast(FP8X4),
@@ -374,183 +403,138 @@ def tile_step1attention_pa_kernel(tc, q, k, x, Wv, out):
                         start=(c == 0),
                         stop=(c == passes - 1),
                     )
-            tiles["sums", r0] = sums
+            tiles["sums", j0] = sums
 
-        def divide_and_store(it, g, r0, r1):
-            tiles = unit[(it, g)]
+        def invert_sums(it, g, j0, j1):
+            tiles = unit[it, g]
+            tiles["inverse", j0] = stats.tile([P, REP], F32, name="inverse")
+            nc.vector.reciprocal(out=tiles["inverse", j0][:, j0:j1], in_=tiles["row_sums"][:, j0:j1])
+
+        def divide_and_store(it, g, j0, j1):
+            sums, inverse = unit[it, g]["sums", j0], unit[it, g]["inverse", j0]
             o = o_pool.tile([P, REP, P], F32, name="o")
-            if g % 2 == 1:
-                for r in range(r0, r1):
-                    nc.scalar.activation(
-                        out=o[:, r, :], in_=tiles["sums", r0][:, r, :], func=ACT.Copy, scale=tiles["inv_sum", r0][:, r : r + 1]
-                    )
+            if g == 3:
+                for j in range(j0, j1):
+                    nc.scalar.activation(out=o[:, j, :], in_=sums[:, j, :], func=ACT.Copy, scale=inverse[:, j : j + 1])
             else:
                 nc.vector.tensor_tensor(
-                    out=o[:, r0:r1, :],
-                    in0=tiles["sums", r0][:, r0:r1, :],
-                    in1=tiles["inv_sum", r0][:, r0:r1].unsqueeze(2).to_broadcast([P, r1 - r0, P]),
-                    op=ALU.mult,
+                    out=o[:, j0:j1, :], in0=sums[:, j0:j1, :],
+                    in1=inverse[:, j0:j1].unsqueeze(2).to_broadcast([P, j1 - j0, P]), op=ALU.mult,
                 )
-            rows = out_rows[it * P + SUB * r0 : it * P + SUB * r1, :]
+            rows = out_rows[it * P + SUB * j0 : it * P + SUB * j1, :]
             for r in range(REP):
-                cols = slice((REP * g + r) * P, (REP * g + r + 1) * P)
+                h = REP * g + r
                 nc.sync.dma_start(
-                    out=rows[:, cols].rearrange("(j w) d -> w j d", w=SUB), in_=o[r * SUB : (r + 1) * SUB, r0:r1, :]
+                    out=rows[:, h * P : (h + 1) * P].rearrange("(j w) d -> w j d", w=SUB),
+                    in_=o[r * SUB : (r + 1) * SUB, j0:j1, :],
                 )
 
-        for t in range(order[0] + 1):
-            keep_keys(t, transpose_keys(t), nc.vector.tensor_copy)
-        for h in range(REP):
-            scale_bias(h, slice(0, first), nc.vector)
-        for part in range(2):
-            keep_queries(order[0], part, transpose_queries(order[0], part), nc.scalar.copy if part == 0 else nc.vector.tensor_copy)
-        count = len(packs)
-        steps = count // 2
-        rows_of_step = {n: [n] for n in range(12)}
-        values_of_step = {6: [(0, 0)], 7: [(0, 1)], 8: [(0, 2)], 9: [(0, 3)], 17: [(1, 0)], 19: [(1, 1)], 21: [(1, 2)], 23: [(1, 3)]}
-        last_values = [max(step for step in values_of_step if any(kp == key_pass for kp, g in values_of_step[step])) for key_pass in range(2)]
         waiting = []
-        dividing = []
-        done = []
 
-        def finish_pack(m, step):
-            done.append(m)
-            quantise_e(m)
+        def quantise_e(m, step):
             pack = packs[m]
-            if m >= count - REP:
-                waiting.append((step + 1, pack["it"], pack["g"], pack["slot"] - 1, pack["slot"] + 1))
-            elif pack["last"]:
-                waiting.append((step + 1, pack["it"], pack["g"], 0, REP))
+            it, g = pack["it"], pack["g"]
+            tiles = unit[it, g]
+            if "e_codes" not in tiles:
+                pool, width = (early_codes, REP * P) if it < ONE_BANK else (late_codes, 2 * REP * P)
+                tiles["e_codes"] = pool.tile([P, width], U32, name="e_codes", align_bytes=64)
+                tiles["e_scales"] = pool.tile([P, width], U8, name="e_scales", align_bytes=64)
+            cols = slice(2 * (pack["slot"] if m >= first_late else pack["slot"] - 1) * P, 2 * (pack["slot"] + 1) * P)
+            quantise(pack["grouped"], tiles["e_codes"][:, cols], tiles["e_scales"][:, cols])
+            if m >= count - REP and m % 2 == 1:
+                waiting.append((step + 1, it, g, pack["slot"] - 1, pack["slot"] + 1))
+            elif pack["last"] and m < count - REP:
+                waiting.append((step + 1, it, g, 0, REP))
 
-        def exp_and_copy(e_pack, copy_pack):
-            if 0 <= e_pack < count:
-                exponentials(e_pack)
-            if 0 <= copy_pack < count:
-                regroup_e(copy_pack)
+        bank_k = transpose_part(0, 2)
+        keep_part(0, 2, bank_k, nc.vector.tensor_copy)
+        for r in range(REP):
+            scale_bias(nc.vector, 0, r, slice(0, P))
+        keep_part(0, 0, transpose_part(0, 0), nc.scalar.copy)
+        keep_part(0, 1, transpose_part(0, 1), nc.vector.tensor_copy)
+        for r in range(REP):
+            scale_bias(nc.gpsimd, 1, r, slice(0, P))
+        for e_tile in e_early[:2]:
+            nc.gpsimd.memset(e_tile[:].bitcast(F32), 0.0)
+        mask_roots()
 
-        first_pair = 96
-        for m in range(-1, first_pair):
-            e_pack = m - 3
-            if 0 <= e_pack < count:
-                transpose_e(e_pack)
-            part = packs[m]["turn"] - 3 if 0 <= m < count and packs[m]["place"] + 1 < len(order) else -1
+        rows_of_step = {n - 1: n for n in range(len(row_tiles))}
+        values_of_step = {5: (0, 0), 6: (0, 1), 7: (0, 2), 8: (0, 3), 17: (1, 0), 19: (1, 1), 21: (1, 2), 23: (1, 3)}
+        ready = {key_pass: max(m for m in values_of_step if values_of_step[m][0] == key_pass) + 2 for key_pass in range(2)}
+
+        to_divide = []
+        m = -1
+        while m < count + 3 or waiting or to_divide:
+            new_e = m - 3
+            if 0 <= new_e < count:
+                transpose_e(new_e)
+            part = packs[m]["turn"] - 3 if 0 <= m < count and packs[m]["it"] + 1 < Q_TILES else -1
             if 0 <= part < 3:
-                after = order[packs[m]["place"] + 1]
-                if part < 2:
-                    part_bank = transpose_queries(after, part)
-                elif after > 0:
-                    part_bank = transpose_keys(after)
-            for n in rows_of_step.get(m, []):
-                spread_transposes(n)
+                part_bank = transpose_part(packs[m]["it"] + 1, part)
+            if m in rows_of_step:
+                transpose_rows(rows_of_step[m])
             if m + 1 < count:
-                open_pack(m + 1)
-            if m + 1 < first_pair:
-                add_bias(m + 1, True)
-                add_scores(m + 1, False)
-            elif m + 1 < count:
-                add_scores(m + 1, True)
-            for key_pass, g in values_of_step.get(m, []):
-                project_values(key_pass, g)
-            finished = dividing
-            dividing = []
-            if waiting and waiting[0][0] <= m and m > last_values[0 if waiting[0][1] < 4 else 1] + 1:
-                dividing.append(waiting[0][1:])
+                open_banks(m + 1)
+                if packs[m + 1]["g"] < STEEP:
+                    add_steep_bias(m + 1)
+                    add_scores(m + 1, False)
+                else:
+                    add_scores(m + 1, True)
+                    add_flat_bias(m + 1)
+            if m in values_of_step:
+                project_values(*values_of_step[m])
+            dividing = to_divide
+            to_divide = []
+            if waiting and waiting[0][0] <= m and m >= ready[0 if waiting[0][1] < ONE_BANK else 1]:
+                to_divide.append(waiting[0][1:])
                 waiting.remove(waiting[0])
-                weighted_values(*dividing[0])
+                weighted_values(*to_divide[0])
             if 0 <= m < count:
                 maximum(m, 0)
-            if m - 5 >= 0 and (m - 5) % 2 == 1:
-                finish_pack(m - 5, m)
+            behind = m - 5
+            if 0 <= behind < count - REP and (behind % 2 == 1 or behind >= first_late):
+                quantise_e(behind, m)
+            else:
+                for work in dividing:
+                    divide_and_store(*work)
+                dividing = []
             if 0 <= m < count:
                 maximum(m, 1)
             if m == 0:
-                mask_root(slice(first, S))
-            if 0 <= m < count:
-                scale_next(m)
+                for e_tile in e_early[2:]:
+                    nc.vector.memset(e_tile[:].bitcast(F32), 0.0)
+                split_roots(nc.vector, slice(S - P, S))
+                make_slopes()
+                split_roots(nc.gpsimd, slice(0, S - P))
+                for e_tile in e_late:
+                    nc.gpsimd.memset(e_tile[:, 1, :].bitcast(F32), 0.0)
+            if 0 <= m < count and packs[m]["g"] < STEEP and packs[m]["it"] % 2 == 0:
+                for j, k0, whole, used in packs[m]["banks"]:
+                    if k0 == 0:
+                        scale_bias(nc.gpsimd, packs[m]["g"], j, slice(P * (packs[m]["it"] + 1), min(P * (packs[m]["it"] + 3), S)))
             if 0 <= m - 1 < count:
                 exponentials(m - 1)
-            if 0 <= e_pack < count:
-                regroup_e(e_pack)
-            if 0 <= part < 2:
-                keep_queries(after, part, part_bank, nc.scalar.copy)
-            if part == 2:
-                if after > 0:
-                    keep_keys(after, part_bank, nc.scalar.copy)
-                if packs[m]["place"] + 2 < len(order):
-                    if order[packs[m]["place"] + 2] > 0:
-                        load_keys(order[packs[m]["place"] + 2])
-                    load_queries(order[packs[m]["place"] + 2])
-            for n in rows_of_step.get(m - 1, []):
-                quantise_rows(n)
-            for n in rows_of_step.get(m, []):
-                spread_copies(n)
-                if n + 4 < len(row_tiles):
-                    load_rows(n + 4)
-            for key_pass, g in values_of_step.get(m - 1, []):
-                quantise_values(key_pass, g)
-            for key_pass, g in values_of_step.get(m, []):
-                group_values(key_pass, g)
-            for part_of_unit in finished:
-                divide_and_store(*part_of_unit)
-            for part_of_unit in dividing:
-                invert_sums(*part_of_unit)
-
-        waiting = [(0,) + entry[1:] for entry in waiting]
-        s = first_pair // 2
-        while s < steps + 3 or waiting or dividing:
-            a, b = 2 * s, 2 * s + 1
-            turned = [m for m in (a - 3, a - 2) if 0 <= m < count]
-            if 0 <= s < steps:
-                add_bias(a, False)
-                open_pack(b)
-                add_bias(b, True)
-            for m in turned:
-                transpose_e(m)
-            new_parts = []
-            if 0 <= s < steps and packs[a]["place"] + 1 < len(order):
-                after = order[packs[a]["place"] + 1]
-                turn = packs[a]["turn"] // 2 - 0
-                new_parts = [[0], [1], [2], []][turn] if 0 <= turn < 4 else []
-            part_banks = [transpose_queries(after, part) if part < 2 else transpose_keys(after) for part in new_parts if part < 2 or after > 0]
-            if 0 <= s < steps:
-                add_scores(b, False)
-            if s + 1 < steps:
-                open_pack(a + 2)
-                add_scores(a + 2, True)
-            finished = dividing
-            dividing = []
-            while waiting and waiting[0][0] <= s and len(dividing) < 1:
-                dividing.append(waiting[0][1:])
-                waiting.remove(waiting[0])
-                weighted_values(*dividing[-1])
-            if 0 <= s < steps:
-                maximum(a, 0)
-                maximum(a, 1)
-            q_pack = a - 5
-            if 0 <= q_pack < count and s < steps:
-                finish_pack(q_pack, s)
-            if 0 <= s < steps:
-                maximum(b, 0)
-                maximum(b, 1)
-            for part_of_unit in finished:
-                divide_and_store(*part_of_unit)
-            for m in (a, b):
-                if 0 <= m < count:
-                    scale_next(m)
-            exp_and_copy(a - 1, a - 3)
-            exp_and_copy(a - 0, a - 2)
-            if s >= steps:
-                for m in range(max(q_pack, 0), min(a - 2, count)):
-                    if m % 2 == 1 and m not in done:
-                        finish_pack(m, s)
-            for part, part_bank in zip(new_parts, part_banks):
-                if part < 2:
-                    keep_queries(after, part, part_bank, nc.scalar.copy)
-                else:
-                    keep_keys(after, part_bank, nc.scalar.copy)
-            if 2 in new_parts and packs[a]["place"] + 2 < len(order):
-                load_keys(order[packs[a]["place"] + 2])
-                load_queries(order[packs[a]["place"] + 2])
-            for part_of_unit in dividing:
-                invert_sums(*part_of_unit)
-            s += 1
+            if 0 <= new_e < count:
+                regroup_e(new_e)
+                if new_e >= count - REP:
+                    quantise_e(new_e, m)
+            if 0 <= part < 3:
+                keep_part(packs[m]["it"] + 1, part, part_bank, nc.scalar.copy)
+                if part == 2 and packs[m]["it"] + 2 < Q_TILES:
+                    load_keys(packs[m]["it"] + 2)
+                    load_queries(packs[m]["it"] + 2, pieces=1)
+            if m - 1 in rows_of_step:
+                quantise_rows(rows_of_step[m - 1])
+            if m in rows_of_step:
+                regroup_rows(rows_of_step[m])
+                if rows_of_step[m] + ROWS_AHEAD < len(row_tiles):
+                    load_rows(rows_of_step[m] + ROWS_AHEAD)
+            if m - 1 in values_of_step:
+                quantise_values(*values_of_step[m - 1])
+            if m in values_of_step:
+                group_values(*values_of_step[m])
+            for work in dividing:
+                divide_and_store(*work)
+            for work in to_divide:
+                invert_sums(*work)
+            m += 1

import math
from contextlib import ExitStack

import concourse.mybir as mybir
from concourse.masks import make_identity

F32 = mybir.dt.float32
BF16 = mybir.dt.bfloat16
U32 = mybir.dt.uint32
U8 = mybir.dt.uint8
FP8X4 = mybir.dt.float8_e4m3fn_x4
ALU = mybir.AluOpType
ACT = mybir.ActivationFunctionType

P = 128
S = 1024
HD = 2048
HEADS = 16
GROUPS = 4
REP = HEADS // GROUPS
SUB = P // REP
GD = GROUPS * P
Q_TILES = S // P
K_PASS = 512
ONE_BANK = K_PASS // P
SCALE = 1.0 / math.sqrt(P)
MASKED = 1.0e30
TINY = 1.0e-30
E_RING = REP
STEEP = 2
ROWS_AHEAD = 4

FLOPS = 2 * S * HD * GD + 2 * 2 * HEADS * P * (K_PASS * K_PASS + K_PASS * S)


def tile_step1attention_pa_kernel(tc, q, k, x, Wv, out):
    nc = tc.nc
    q_rows = q.flatten_outer_dims()
    k_rows = k.flatten_outer_dims()
    x_rows = x.flatten_outer_dims()
    out_rows = out.flatten_outer_dims()

    with ExitStack() as ctx:
        ctx.enter_context(tc.manual_schedule())
        keep = ctx.enter_context(tc.tile_pool(name="keep", bufs=1))
        wide_pool = ctx.enter_context(tc.tile_pool(name="wide_pool", bufs=8))
        q_pool = ctx.enter_context(tc.tile_pool(name="q_pool", bufs=2))
        qT_pool = ctx.enter_context(tc.tile_pool(name="qT_pool", bufs=2))
        grouped_pool = ctx.enter_context(tc.tile_pool(name="grouped_pool", bufs=5))
        stats = ctx.enter_context(tc.tile_pool(name="stats", bufs=6))
        early_codes = ctx.enter_context(tc.tile_pool(name="early_codes", bufs=8))
        late_codes = ctx.enter_context(tc.tile_pool(name="late_codes", bufs=3))
        o_pool = ctx.enter_context(tc.tile_pool(name="o_pool", bufs=3))
        ps_scores = ctx.enter_context(tc.psum_pool(name="ps_scores", bufs=4))
        ps_other = ctx.enter_context(tc.psum_pool(name="ps_other", bufs=4))

        k_raw = [keep.tile([P, GD], BF16, name="k_raw%d" % t) for t in range(Q_TILES)]
        q_raw = {}
        row_raw = {}

        def load_keys(t):
            nc.sync.dma_start(out=k_raw[t][:], in_=k_rows[t * P : (t + 1) * P, :])

        def load_queries(it, pieces):
            q_raw[it] = q_pool.tile([P, HD], BF16, name="q_raw")
            for n in range(pieces):
                cols = slice(n * HD // pieces, (n + 1) * HD // pieces)
                nc.sync.dma_start(out=q_raw[it][:, cols], in_=q_rows[it * P : (it + 1) * P, cols])

        w_codes = keep.tile([P, GROUPS, 4 * P], U32, name="w_codes", align_bytes=64)
        w_scales = keep.tile([P, GROUPS, 4 * P], U8, name="w_scales", align_bytes=64)
        x_codes = keep.tile([P, Q_TILES, 4 * P], U32, name="x_codes", align_bytes=64)
        x_scales = keep.tile([P, Q_TILES, 4 * P], U8, name="x_scales", align_bytes=64)
        v_codes = keep.tile([P, S // K_PASS, GD], U32, name="v_codes", align_bytes=64)
        v_scales = keep.tile([P, S // K_PASS, GD], U8, name="v_scales", align_bytes=64)

        x_tiles = x_rows.rearrange("(a p e) c -> a e p c", p=P, e=2)
        w_rows = [(Wv[g * P : (g + 1) * P, :], w_codes[:, g, :], w_scales[:, g, :]) for g in range(GROUPS)]
        x_parts = [(x_tiles[n // 2, n % 2], x_codes[:, n, :], x_scales[:, n, :]) for n in range(Q_TILES)]
        row_tiles = w_rows[:1] + x_parts[:4] + w_rows[1:] + x_parts[4:]

        def load_rows(n):
            row_raw[n] = wide_pool.tile([P, HD], BF16, name="row_raw", tag="wide")
            nc.sync.dma_start(out=row_raw[n][:], in_=row_tiles[n][0])

        load_keys(0)
        load_queries(0, pieces=2)
        for n in range(ROWS_AHEAD):
            load_rows(n)
        load_keys(1)
        load_queries(1, pieces=1)

        offset = keep.tile([P, 1], F32, name="offset")
        factor = keep.tile([P, 1], F32, name="factor")
        power = keep.tile([P, REP], F32, name="power")
        for n in range(REP):
            nc.vector.memset(offset[n * SUB : (n + 1) * SUB, :], -float(n * SUB))
        for c in range(2):
            nc.vector.memset(factor[c * P // 2 : (c + 1) * P // 2, :], float(c + 1))
        nc.vector.memset(power[:], 0.0)
        for r in range(REP):
            c = r % 2
            nc.vector.memset(power[c * P // 2 : (c + 1) * P // 2, r : r + 1], -(2.0 ** (3 - (r + c) // 2)))

        ident_bf = keep.tile([P, P], BF16, name="ident_bf")
        make_identity(nc, ident_bf[:])
        dist = wide_pool.tile([P, S], F32, name="dist", tag="wide")
        nc.gpsimd.iota(
            dist[:], pattern=[[1, S]], base=0, channel_multiplier=-1, allow_small_or_imprecise_dtypes=True
        )
        row_dist = wide_pool.tile([P, S], F32, name="row_dist", tag="wide")
        nc.gpsimd.iota(
            row_dist[:], pattern=[[-1, S]], base=S - SUB, channel_multiplier=1, allow_small_or_imprecise_dtypes=True
        )
        ident_f32 = keep.tile([P, P], F32, name="ident_f32")
        make_identity(nc, ident_f32[:])
        root = keep.tile([P, S], F32, name="root")
        nc.vector.tensor_scalar(out=root[:], in0=dist[:], scalar1=0.0, scalar2=TINY, op0=ALU.add, op1=ALU.max)
        nc.scalar.activation(out=root[:], in_=root[:], func=ACT.Sqrt)

        e_early = [keep.tile([P, 2, K_PASS], BF16, name="e_early%d" % n) for n in range(E_RING)]
        e_late = [keep.tile([P, 2, K_PASS], BF16, name="e_late%d" % n) for n in range(E_RING)]
        row_root = wide_pool.tile([P, S], F32, name="row_root", tag="wide")
        nc.vector.tensor_scalar(
            out=row_root[:], in0=row_dist[:], scalar1=offset[:], scalar2=TINY, op0=ALU.add, op1=ALU.max
        )
        nc.scalar.activation(out=row_root[:], in_=row_root[:], func=ACT.Sqrt, scale=factor[:])
        nc.vector.tensor_scalar(
            out=dist[:, :P], in0=dist[:, :P], scalar1=0.0, scalar2=-MASKED, op0=ALU.min, op1=ALU.mult
        )
        nc.vector.tensor_tensor(out=root[:, :P], in0=root[:, :P], in1=dist[:, :P], op=ALU.add)

        bias = keep.tile([P, STEEP, S // SUB, REP, SUB], F32, name="bias")

        def scale_bias(engine, g, r, cols):
            slope = 2.0 ** (-(REP * g + r + 1) / 2.0)
            engine.tensor_scalar(
                out=bias[:, g, cols.start // SUB : cols.stop // SUB, r, :],
                in0=root[:, cols].rearrange("p (n w) -> p n w", w=SUB),
                scalar1=-slope / SCALE, scalar2=0.0, op0=ALU.mult, op1=ALU.add,
            )

        roots = keep.tile([P, S], BF16, name="roots")
        column = keep.tile([P, REP, SUB], F32, name="column")
        slopes = {g: keep.tile([P, REP, SUB], BF16, name="slopes%d" % g) for g in range(STEEP, GROUPS)}
        nc.gpsimd.iota(
            column[:], pattern=[[0, REP], [1, SUB]], base=0, channel_multiplier=-1, allow_small_or_imprecise_dtypes=True
        )
        def mask_roots():
            cols = slice(S - SUB, S)
            nc.vector.tensor_scalar(
                out=row_dist[:, cols], in0=row_dist[:, cols], scalar1=offset[:], scalar2=0.0, op0=ALU.add, op1=ALU.min
            )
            nc.vector.scalar_tensor_tensor(
                out=row_root[:, cols], in0=row_dist[:, cols], scalar=-MASKED, in1=row_root[:, cols],
                op0=ALU.mult, op1=ALU.add,
            )

        def split_roots(engine, cols):
            engine.tensor_scalar(
                out=roots[:, cols], in0=row_root[:, cols], scalar1=1.0, scalar2=0.0, op0=ALU.mult, op1=ALU.add
            )
            for c in range(2):
                low = slice((2 * c + 1) * SUB, (2 * c + 2) * SUB)
                engine.tensor_tensor(
                    out=roots[low, cols], in0=row_root[low, cols], in1=roots[low, cols], op=ALU.subtract
                )

        def make_slopes():
            nc.vector.tensor_scalar(
                out=column[:], in0=column[:], scalar1=offset[:], scalar2=0.0, op0=ALU.subtract, op1=ALU.is_equal
            )
            for g in range(STEEP, GROUPS):
                for r in range(REP):
                    nc.gpsimd.tensor_scalar(
                        out=slopes[g][:, r, :], in0=column[:, r, :], scalar1=power[:, r : r + 1],
                        scalar2=2.0 ** (-2 * g), op0=ALU.mult, op1=ALU.mult,
                    )

        def transpose_planes(words):
            bank = ps_other.tile([P, 4, P], F32, name="bank", tag="other")
            for a in range(4):
                nc.tensor.transpose(out=bank[:, a, :], in_=words[:, a * P : (a + 1) * P], identity=ident_f32[:])
            return bank

        def grouped_pair():
            return grouped_pool.tile([P, 2, 2 * K_PASS], BF16, name="grouped", align_bytes=64)

        def grouped_single():
            return grouped_pool.tile([P, 1, 2 * K_PASS], BF16, name="grouped_single", align_bytes=64)

        def regroup(bank, grouped, copy):
            copy(
                out=grouped.bitcast(F32).rearrange("p (c w u) -> p c w u", c=2, u=2),
                in_=bank[:].rearrange("p (c u) w -> p c w u", u=2),
            )

        def quantise(grouped, codes, scales):
            nc.vector.quantize_mx(
                out=codes.bitcast(FP8X4), scales=scales, in_=grouped[:].rearrange("p n k -> p (n k)")
            )

        row_banks = {}
        row_grouped = {}

        def transpose_rows(n):
            words = row_raw[n][:].bitcast(F32)
            row_banks[n] = [transpose_planes(words[:, 4 * half * P : 4 * (half + 1) * P]) for half in range(2)]

        def regroup_rows(n):
            row_grouped[n] = grouped_pair()
            regroup(row_banks[n][0], row_grouped[n][:, 0, :], nc.vector.tensor_copy if n % 2 == 0 else nc.scalar.copy)
            regroup(row_banks[n][1], row_grouped[n][:, 1, :], nc.scalar.copy)

        def quantise_rows(n):
            quantise(row_grouped[n], row_tiles[n][1], row_tiles[n][2])

        v_sums = {}
        v_grouped = {}

        def project_values(key_pass, g):
            sums = ps_other.tile([P, 4, P], F32, name="v_sums", tag="other")
            for t in range(4):
                for c in range(HD // K_PASS):
                    cols = slice(c * P, (c + 1) * P)
                    nc.tensor.matmul_mx(
                        out=sums[:, t, :],
                        lhsT=x_codes[:, 4 * key_pass + t, cols].bitcast(FP8X4),
                        lhsT_scale=x_scales[:, 4 * key_pass + t, cols],
                        rhs=w_codes[:, g, cols].bitcast(FP8X4),
                        rhs_scale=w_scales[:, g, cols],
                        start=(c == 0),
                        stop=(c == HD // K_PASS - 1),
                    )
            v_sums[key_pass, g] = sums

        def group_values(key_pass, g):
            grouped = grouped_pool.tile([P, P, 4], BF16, name="v_grouped", bufs=3, align_bytes=64)
            nc.scalar.copy(out=grouped[:], in_=v_sums[key_pass, g][:].rearrange("p t n -> p n t"))
            v_grouped[key_pass, g] = grouped

        def quantise_values(key_pass, g):
            cols = slice(g * P, (g + 1) * P)
            quantise(v_grouped[key_pass, g], v_codes[:, key_pass, cols], v_scales[:, key_pass, cols])

        kT = [keep.tile([P, GROUPS, K_PASS], BF16, name="kT%d" % c) for c in range(S // K_PASS)]
        qT = {}

        def transpose_part(it, part):
            if part == 2:
                bank = ps_other.tile([P, GROUPS, P], BF16, name="bank_k", tag="other")
                for g in range(GROUPS):
                    nc.tensor.transpose(out=bank[:, g, :], in_=k_raw[it][:, g * P : (g + 1) * P], identity=ident_bf[:])
                return bank
            if part == 0:
                qT[it] = qT_pool.tile([P, GROUPS, REP, P], BF16, name="qT")
            bank = ps_other.tile([P, GROUPS // 2, REP, REP, SUB], BF16, name="bank_q", tag="other")
            for g in range(GROUPS // 2):
                for r in range(REP):
                    h = REP * (GROUPS // 2 * part + g) + r
                    nc.tensor.transpose(
                        out=bank[:, g, :, r, :], in_=q_raw[it][:, h * P : (h + 1) * P], identity=ident_bf[:]
                    )
            return bank

        def keep_part(it, part, bank, copy):
            if part == 2:
                cols = slice(it % ONE_BANK * P, (it % ONE_BANK + 1) * P)
                copy(out=kT[it // ONE_BANK][:, :, cols], in_=bank[:])
            else:
                half = slice(GROUPS // 2 * part, GROUPS // 2 * (part + 1))
                copy(
                    out=qT[it][:, half, :, :].rearrange("p g j n -> p (g j n)"),
                    in_=bank[:].rearrange("p g j r w -> p (g j r w)"),
                )

        packs = []
        for it in range(Q_TILES):
            for g in range(GROUPS):
                keys = [P * it + SUB * (j + 1) for j in range(REP)]
                if it < ONE_BANK:
                    pairs = [[(j, 0, P * (it + 1), keys[j]) for j in (n, n + 1)] for n in range(0, REP, 2)]
                else:
                    pairs = [
                        [(j, 0, K_PASS, K_PASS), (j, K_PASS, P * (it + 1) - K_PASS, keys[j] - K_PASS)] for j in range(REP)
                    ]
                for slot, banks in enumerate(pairs):
                    ring = e_early if it < ONE_BANK else e_late
                    packs.append(
                        {"it": it, "g": g, "banks": banks, "slot": slot, "last": slot == len(pairs) - 1,
                         "turn": g * len(pairs) + slot, "e": ring[len(packs) % E_RING]}
                    )
        count = len(packs)
        first_late = [pack["it"] for pack in packs].index(ONE_BANK)
        unit = {}

        def open_banks(m):
            packs[m]["z"] = [ps_scores.tile([P, K_PASS], F32, name="z") for b in range(2)]

        def add_scores(m, first):
            pack = packs[m]
            for z, (j, k0, whole, used) in zip(pack["z"], pack["banks"]):
                nc.tensor.matmul(
                    out=z[:, :used], lhsT=qT[pack["it"]][:, pack["g"], j, :],
                    rhs=kT[k0 // K_PASS][:, pack["g"], :used], start=first, stop=not first,
                )

        def add_steep_bias(m):
            pack = packs[m]
            for z, (j, k0, whole, used) in zip(pack["z"], pack["banks"]):
                for n in range(whole // P):
                    delta = pack["it"] - (k0 // P + n)
                    nc.tensor.matmul(
                        out=z[:, n * P : (n + 1) * P],
                        lhsT=bias[:, pack["g"], REP * delta + j, :, :].rearrange("p r w -> p (r w)"),
                        rhs=ident_f32[:],
                        is_transpose=True,
                        start=(n == 0),
                        stop=False,
                    )

        def add_flat_bias(m):
            pack = packs[m]
            for z, (j, k0, whole, used) in zip(pack["z"], pack["banks"]):
                y = S - SUB - (P * pack["it"] + SUB * j) + k0
                nc.tensor.matmul(
                    out=z[:, :used], lhsT=slopes[pack["g"]][:].rearrange("p r w -> p (r w)"),
                    rhs=roots[:, y : y + used], start=False, stop=True,
                )

        def maximum(m, b):
            pack = packs[m]
            j, k0, whole, used = pack["banks"][b]
            if b == 0:
                pack["scaled"] = wide_pool.tile([P, 2, K_PASS], F32, name="scaled", tag="wide")
                pack["exp_bias"] = [stats.tile([P, 1], F32, name="exp_bias%d" % c) for c in range(2)]
            nc.vector.tensor_scalar(
                out=pack["scaled"][:, b, :used], in0=pack["z"][b][:, :used], scalar1=-SCALE,
                scalar2=pack["exp_bias"][0][:] if k0 > 0 else None,
                op0=ALU.mult, op1=ALU.min, accum_out=pack["exp_bias"][b][:],
            )

        def exponentials(m):
            pack = packs[m]
            it, g = pack["it"], pack["g"]
            if pack["slot"] == 0:
                unit[it, g] = {"row_sums": stats.tile([P, REP], F32, name="row_sums")}
            if it < ONE_BANK:
                pieces = [(j, c, c * K_PASS, used) for c, (j, k0, whole, used) in enumerate(pack["banks"])]
            else:
                pieces = [(pack["slot"], 1, 0, K_PASS + pack["banks"][1][3])]
            for j, c, begin, used in pieces:
                nc.scalar.activation(
                    out=pack["e"][:].rearrange("p c k -> p (c k)")[:, begin : begin + used],
                    in_=pack["scaled"][:].rearrange("p c k -> p (c k)")[:, begin : begin + used],
                    func=ACT.Exp,
                    bias=pack["exp_bias"][c][:],
                    scale=-1.0,
                    accum_out=unit[it, g]["row_sums"][:, j : j + 1],
                )

        e_banks = []

        def transpose_e(m):
            pack = packs[m]
            words = pack["e"][:].rearrange("p c k -> p (c k)").bitcast(F32)
            if m < first_late:
                pack["bank"] = transpose_planes(words)
                return
            if m < first_late + 2:
                e_banks.append(ps_other.tile([P, 4, P], F32, name="e_bank", tag="other"))
            pack["bank"] = e_banks[m % 2]
            whole = pack["banks"][1][2]
            for plane in range(4 if whole > 2 * P or m < first_late + 2 else 3):
                nc.tensor.transpose(
                    out=pack["bank"][:, plane, :], in_=words[:, plane * P : (plane + 1) * P], identity=ident_f32[:]
                )

        def regroup_e(m):
            pack = packs[m]
            if m >= first_late:
                pack["grouped"] = grouped_single()
            elif m % 2 == 0:
                pack["grouped"] = grouped_pair()
            else:
                pack["grouped"] = packs[m - 1]["grouped"]
            copy = nc.vector.tensor_copy if m in (count - 3, count - 2) else nc.scalar.copy
            regroup(pack["bank"], pack["grouped"][:, 0 if m >= first_late else m % 2, :], copy)

        def weighted_values(it, g, j0, j1):
            tiles = unit[it, g]
            passes = 1 if it < ONE_BANK else 2
            sums = ps_other.tile([P, REP, P], F32, name="o_sums", tag="other")
            for j in range(j0, j1):
                for c in range(passes):
                    cols = slice((j * passes + c) * P, (j * passes + c + 1) * P)
                    nc.tensor.matmul_mx(
                        out=sums[:, j, :],
                        lhsT=tiles["e_codes"][:, cols].bitcast(FP8X4),
                        lhsT_scale=tiles["e_scales"][:, cols],
                        rhs=v_codes[:, c, g * P : (g + 1) * P].bitcast(FP8X4),
                        rhs_scale=v_scales[:, c, g * P : (g + 1) * P],
                        start=(c == 0),
                        stop=(c == passes - 1),
                    )
            tiles["sums", j0] = sums

        def invert_sums(it, g, j0, j1):
            tiles = unit[it, g]
            tiles["inverse", j0] = stats.tile([P, REP], F32, name="inverse")
            nc.vector.reciprocal(out=tiles["inverse", j0][:, j0:j1], in_=tiles["row_sums"][:, j0:j1])

        def divide_and_store(it, g, j0, j1):
            sums, inverse = unit[it, g]["sums", j0], unit[it, g]["inverse", j0]
            o = o_pool.tile([P, REP, P], F32, name="o")
            if g == 3:
                for j in range(j0, j1):
                    nc.scalar.activation(out=o[:, j, :], in_=sums[:, j, :], func=ACT.Copy, scale=inverse[:, j : j + 1])
            else:
                nc.vector.tensor_tensor(
                    out=o[:, j0:j1, :], in0=sums[:, j0:j1, :],
                    in1=inverse[:, j0:j1].unsqueeze(2).to_broadcast([P, j1 - j0, P]), op=ALU.mult,
                )
            rows = out_rows[it * P + SUB * j0 : it * P + SUB * j1, :]
            for r in range(REP):
                h = REP * g + r
                nc.sync.dma_start(
                    out=rows[:, h * P : (h + 1) * P].rearrange("(j w) d -> w j d", w=SUB),
                    in_=o[r * SUB : (r + 1) * SUB, j0:j1, :],
                )

        waiting = []

        def quantise_e(m, step):
            pack = packs[m]
            it, g = pack["it"], pack["g"]
            tiles = unit[it, g]
            if "e_codes" not in tiles:
                pool, width = (early_codes, REP * P) if it < ONE_BANK else (late_codes, 2 * REP * P)
                tiles["e_codes"] = pool.tile([P, width], U32, name="e_codes", align_bytes=64)
                tiles["e_scales"] = pool.tile([P, width], U8, name="e_scales", align_bytes=64)
            cols = slice(2 * (pack["slot"] if m >= first_late else pack["slot"] - 1) * P, 2 * (pack["slot"] + 1) * P)
            quantise(pack["grouped"], tiles["e_codes"][:, cols], tiles["e_scales"][:, cols])
            if m >= count - REP and m % 2 == 1:
                waiting.append((step + 1, it, g, pack["slot"] - 1, pack["slot"] + 1))
            elif pack["last"] and m < count - REP:
                waiting.append((step + 1, it, g, 0, REP))

        bank_k = transpose_part(0, 2)
        keep_part(0, 2, bank_k, nc.vector.tensor_copy)
        for r in range(REP):
            scale_bias(nc.vector, 0, r, slice(0, P))
        keep_part(0, 0, transpose_part(0, 0), nc.scalar.copy)
        keep_part(0, 1, transpose_part(0, 1), nc.vector.tensor_copy)
        for r in range(REP):
            scale_bias(nc.gpsimd, 1, r, slice(0, P))
        for e_tile in e_early[:2]:
            nc.gpsimd.memset(e_tile[:].bitcast(F32), 0.0)
        mask_roots()

        rows_of_step = {n - 1: n for n in range(len(row_tiles))}
        values_of_step = {5: (0, 0), 6: (0, 1), 7: (0, 2), 8: (0, 3), 17: (1, 0), 19: (1, 1), 21: (1, 2), 23: (1, 3)}
        ready = {key_pass: max(m for m in values_of_step if values_of_step[m][0] == key_pass) + 2 for key_pass in range(2)}

        to_divide = []
        m = -1
        while m < count + 3 or waiting or to_divide:
            new_e = m - 3
            if 0 <= new_e < count:
                transpose_e(new_e)
            part = packs[m]["turn"] - 3 if 0 <= m < count and packs[m]["it"] + 1 < Q_TILES else -1
            if 0 <= part < 3:
                part_bank = transpose_part(packs[m]["it"] + 1, part)
            if m in rows_of_step:
                transpose_rows(rows_of_step[m])
            if m + 1 < count:
                open_banks(m + 1)
                if packs[m + 1]["g"] < STEEP:
                    add_steep_bias(m + 1)
                    add_scores(m + 1, False)
                else:
                    add_scores(m + 1, True)
                    add_flat_bias(m + 1)
            if m in values_of_step:
                project_values(*values_of_step[m])
            dividing = to_divide
            to_divide = []
            if waiting and waiting[0][0] <= m and m >= ready[0 if waiting[0][1] < ONE_BANK else 1]:
                to_divide.append(waiting[0][1:])
                waiting.remove(waiting[0])
                weighted_values(*to_divide[0])
            if 0 <= m < count:
                maximum(m, 0)
            behind = m - 5
            if 0 <= behind < count - REP and (behind % 2 == 1 or behind >= first_late):
                quantise_e(behind, m)
            else:
                for work in dividing:
                    divide_and_store(*work)
                dividing = []
            if 0 <= m < count:
                maximum(m, 1)
            if m == 0:
                for e_tile in e_early[2:]:
                    nc.vector.memset(e_tile[:].bitcast(F32), 0.0)
                split_roots(nc.vector, slice(S - P, S))
                make_slopes()
                split_roots(nc.gpsimd, slice(0, S - P))
                for e_tile in e_late:
                    nc.gpsimd.memset(e_tile[:, 1, :].bitcast(F32), 0.0)
            if 0 <= m < count and packs[m]["g"] < STEEP and packs[m]["it"] % 2 == 0:
                for j, k0, whole, used in packs[m]["banks"]:
                    if k0 == 0:
                        scale_bias(nc.gpsimd, packs[m]["g"], j, slice(P * (packs[m]["it"] + 1), min(P * (packs[m]["it"] + 3), S)))
            if 0 <= m - 1 < count:
                exponentials(m - 1)
            if 0 <= new_e < count:
                regroup_e(new_e)
                if new_e >= count - REP:
                    quantise_e(new_e, m)
            if 0 <= part < 3:
                keep_part(packs[m]["it"] + 1, part, part_bank, nc.scalar.copy)
                if part == 2 and packs[m]["it"] + 2 < Q_TILES:
                    load_keys(packs[m]["it"] + 2)
                    load_queries(packs[m]["it"] + 2, pieces=1)
            if m - 1 in rows_of_step:
                quantise_rows(rows_of_step[m - 1])
            if m in rows_of_step:
                regroup_rows(rows_of_step[m])
                if rows_of_step[m] + ROWS_AHEAD < len(row_tiles):
                    load_rows(rows_of_step[m] + ROWS_AHEAD)
            if m - 1 in values_of_step:
                quantise_values(*values_of_step[m - 1])
            if m in values_of_step:
                group_values(*values_of_step[m])
            for work in dividing:
                divide_and_store(*work)
            for work in to_divide:
                invert_sums(*work)
            m += 1
